import numpy as np
import ml_dtypes


def mxq(x, axis, fmt="e4m3"):
    dtype, down = {"e4m3": (ml_dtypes.float8_e4m3fn, 7), "e5m2": (ml_dtypes.float8_e5m2, 14)}[fmt]
    v = np.moveaxis(np.asarray(x, np.float32).astype(ml_dtypes.bfloat16).astype(np.float64), axis, -1)
    blocks = v.reshape(v.shape[:-1] + (-1, 32))
    amax = np.abs(blocks).max(-1, keepdims=True)
    byte = np.maximum(np.where(amax > 0, np.frexp(amax)[1] - 1 + 127, 0) - down, 1)
    scale = np.exp2(byte - 127.0)
    codes = (blocks / scale).astype(np.float32).astype(dtype).astype(np.float64)
    return np.moveaxis((codes * scale).reshape(v.shape), -1, axis)


WIDE = False


def mx_kscale(k, group=512):
    if not WIDE:
        return np.ones(k)
    levels = np.array([20, -20, 10, -10, 0])
    if group != 512:
        return np.exp2(np.random.permutation(np.resize(levels, k // group))).repeat(group)
    a = np.random.permutation(np.resize(levels, k // 512 * 4)).reshape(k // 512, 4)
    idx = np.arange(k)
    return np.exp2(a[idx // 512, idx % 128 // 32])


BF16 = ml_dtypes.bfloat16


def bf(x):
    return np.asarray(x, np.float32).astype(BF16)


def f64(x):
    return np.asarray(x).astype(np.float64)


B, N, C, F = 2, 32, 1024, 1024
T = B * N * N
EPS_STD = 1e-5


def messages(x, e_enc, W_pre, b_pre):
    w = f64(W_pre)
    xf = f64(x)
    tgt = xf @ w[:C]
    src = xf @ w[C:2 * C]
    edg = f64(e_enc) @ w[2 * C:]
    return tgt[:, :, None, :] + src[:, None, :, :] + edg + f64(b_pre)


def row_stats(m):
    mean = m.mean(axis=2)
    var = (m * m).mean(axis=2) - mean * mean
    rstd = 1.0 / np.sqrt(np.maximum(var, 0.0) + EPS_STD)
    stat = np.concatenate([mean, rstd], axis=-1)
    arg = np.concatenate([f64(m.argmin(axis=2)), f64(m.argmax(axis=2))], axis=-1)
    return stat, arg


def setup_inputs():
    sb = mx_kscale(T, group=N * N)[::N * N]
    x0 = bf(np.random.standard_normal((B, N, C)))
    e0 = bf(np.random.standard_normal((B, N, N, C)))
    W_pre = bf(np.random.standard_normal((3 * C, F)) / np.sqrt(3 * C))
    b_pre = bf(np.random.standard_normal(F) * 0.3)
    g = bf(np.random.standard_normal((B, N, 4 * F)) * np.exp2(np.random.randint(-12, 1, (B, N, 1))) / sb[:, None, None])
    m = messages(x0, e0, W_pre, b_pre)
    stat, arg = row_stats(m)
    return {"x": bf(f64(x0) * sb[:, None, None]),
            "e_enc": bf(f64(e0) * sb[:, None, None, None]),
            "W_pre": W_pre,
            "b_pre": b_pre,
            "m": np.asarray(m, np.float32),
            "stat": np.asarray(stat, np.float32),
            "arg": np.asarray(arg, np.float32),
            "grad_out": g}


def reference(x, e_enc, W_pre, b_pre, m, stat, arg, grad_out):
    g = f64(grad_out)
    g_mean, g_min, g_max, g_std = g[..., :F], g[..., F:2 * F], g[..., 2 * F:3 * F], g[..., 3 * F:]
    st, ar = f64(stat), f64(arg)
    mean, rstd = st[..., :F], st[..., F:]
    jmin, jmax = ar[..., :F], ar[..., F:]
    j = np.arange(N, dtype=np.float64)[None, None, :, None]
    dm = (g_mean[:, :, None, :] / N
          + g_min[:, :, None, :] * (j == jmin[:, :, None, :])
          + g_max[:, :, None, :] * (j == jmax[:, :, None, :])
          + (g_std * rstd)[:, :, None, :] * (f64(m) - mean[:, :, None, :]) / N)
    xf = f64(x).reshape(B * N, C)
    d_tgt = xf.T @ dm.sum(axis=2).reshape(B * N, F)
    d_src = xf.T @ dm.sum(axis=1).reshape(B * N, F)
    d_edg = mxq(f64(e_enc).reshape(T, C), 0, "e4m3").T @ mxq(dm.reshape(T, F), 0, "e5m2")
    return np.concatenate([d_tgt, d_src, d_edg], axis=0)

@@ -1,0 +1,291 @@
+from contextlib import ExitStack
+
+import concourse.mybir as mybir
+from concourse.masks import make_identity
+
+F32 = mybir.dt.float32
+BF16 = mybir.dt.bfloat16
+I32 = mybir.dt.int32
+U32 = mybir.dt.uint32
+U8 = mybir.dt.uint8
+E4M3X4 = mybir.dt.float8_e4m3fn_x4
+E5M2X4 = mybir.dt.float8_e5m2_x4
+ALU = mybir.AluOpType
+
+P = 128
+PACK = 4
+K_PASS = P * PACK
+GRAPHS, NODES, C, F = 2, 32, 1024, 1024
+ALL_NODES = GRAPHS * NODES
+EDGES = ALL_NODES * NODES
+PASSES = EDGES // K_PASS
+TARGETS = K_PASS // NODES
+SPREAD = P // TARGETS
+HALF = 512
+HALVES = F // HALF
+BLK = 128
+BLKS = HALF // BLK
+C_BLKS = C // BLK
+SUMS = TARGETS + NODES
+
+FLOPS = 2 * EDGES * C * F + 2 * 2 * ALL_NODES * C * F
+BYTES = 2 * (ALL_NODES * C + EDGES * C + ALL_NODES * 4 * F) + 4 * (EDGES * F + 2 * ALL_NODES * 2 * F + 3 * C * F)
+
+
+def tile_gnnlayer_pa_v_kernel(tc, x, e_enc, W_pre, b_pre, m, stat, arg, grad_out, out):
+    nc = tc.nc
+    x_rows = x.rearrange("b n c -> (b n) c")
+    e_rows = e_enc.rearrange("b i j c -> (b i j) c")
+    m_rows = m.rearrange("b i j f -> (b i j) f")
+    stat_rows = stat.rearrange("b n s -> (b n) s")
+    arg_rows = arg.rearrange("b n s -> (b n) s")
+    g_rows = grad_out.rearrange("b n g -> (b n) g")
+    lo = slice(0, ALL_NODES)
+    hi = slice(ALL_NODES, P)
+
+    with ExitStack() as ctx:
+        const = ctx.enter_context(tc.tile_pool(name="const", bufs=1))
+        keep = ctx.enter_context(tc.tile_pool(name="keep", bufs=1))
+        setup = ctx.enter_context(tc.tile_pool(name="setup", bufs=1))
+        e_pool = ctx.enter_context(tc.tile_pool(name="e_pool", bufs=2))
+        rep_pool = ctx.enter_context(tc.tile_pool(name="rep_pool", bufs=2))
+        m_pool = ctx.enter_context(tc.tile_pool(name="m_pool", bufs=3))
+        work = ctx.enter_context(tc.tile_pool(name="work", bufs=2))
+        per_half = ctx.enter_context(tc.tile_pool(name="per_half", bufs=2))
+        o_pool = ctx.enter_context(tc.tile_pool(name="o_pool", bufs=4))
+        psum = ctx.enter_context(tc.psum_pool(name="psum", bufs=1))
+
+        ident_f = const.tile([P, P], F32)
+        make_identity(nc, ident_f[:])
+        ident_b = const.tile([P, P], BF16)
+        make_identity(nc, ident_b[:])
+
+        edge_i = const.tile([P, PACK], I32)
+        nc.gpsimd.iota(edge_i[:], pattern=[[1, PACK]], base=0, channel_multiplier=PACK)
+        src_i = const.tile([P, PACK], I32)
+        nc.vector.tensor_single_scalar(out=src_i[:], in_=edge_i[:], scalar=NODES - 1, op=ALU.bitwise_and)
+        src_f = const.tile([P, PACK], F32)
+        nc.vector.tensor_copy(out=src_f[:], in_=src_i[:])
+        tgt_i = const.tile([P, 1], I32)
+        nc.vector.tensor_single_scalar(out=tgt_i[:], in_=edge_i[:, 0:1], scalar=5, op=ALU.logical_shift_right)
+        tgt_f = const.tile([P, 1], F32)
+        nc.vector.tensor_copy(out=tgt_f[:], in_=tgt_i[:])
+        col_i = const.tile([P, NODES], I32)
+        nc.gpsimd.iota(col_i[:], pattern=[[1, NODES]], base=0, channel_multiplier=0)
+        col_f = const.tile([P, NODES], F32)
+        nc.vector.tensor_copy(out=col_f[:], in_=col_i[:])
+        pick = const.tile([P, PACK, SUMS], F32)
+        for t in range(PACK):
+            nc.vector.tensor_scalar(
+                out=pick[:, t, 0:TARGETS], in0=col_f[:, 0:TARGETS], scalar1=tgt_f[:, 0:1], scalar2=None, op0=ALU.is_equal
+            )
+            nc.vector.tensor_scalar(
+                out=pick[:, t, TARGETS:SUMS], in0=col_f[:], scalar1=src_f[:, t : t + 1], scalar2=None, op0=ALU.is_equal
+            )
+
+        g_std2 = setup.tile([P, F], BF16)
+        rstd2 = setup.tile([P, F], F32)
+        mean_hi = setup.tile([P, F], F32)
+        g_mean_hi = setup.tile([P, F], BF16)
+        for rows in (lo, hi):
+            nc.scalar.dma_start(out=g_std2[rows, :], in_=g_rows[:, 3 * F : 4 * F])
+            nc.scalar.dma_start(out=rstd2[rows, :], in_=stat_rows[:, F : 2 * F])
+        nc.scalar.dma_start(out=mean_hi[hi, :], in_=stat_rows[:, 0:F])
+        nc.scalar.dma_start(out=g_mean_hi[hi, :], in_=g_rows[:, 0:F])
+        ca = setup.tile([P, F], F32)
+        nc.vector.scalar_tensor_tensor(
+            out=ca[:], in0=g_std2[:], scalar=1.0 / NODES, in1=rstd2[:], op0=ALU.mult, op1=ALU.mult
+        )
+        nc.vector.tensor_tensor(out=mean_hi[hi, :], in0=ca[hi, :], in1=mean_hi[hi, :], op=ALU.mult)
+        nc.vector.scalar_tensor_tensor(
+            out=ca[hi, :], in0=g_mean_hi[hi, :], scalar=1.0 / NODES, in1=mean_hi[hi, :], op0=ALU.mult, op1=ALU.subtract
+        )
+        gg = setup.tile([P, F], BF16)
+        nc.scalar.dma_start(out=gg[lo, :], in_=g_rows[:, F : 2 * F])
+        nc.scalar.dma_start(out=gg[hi, :], in_=g_rows[:, 2 * F : 3 * F])
+        jj_f = setup.tile([P, F], F32)
+        nc.scalar.dma_start(out=jj_f[lo, :], in_=arg_rows[:, 0:F])
+        nc.scalar.dma_start(out=jj_f[hi, :], in_=arg_rows[:, F : 2 * F])
+        jj = setup.tile([P, F], BF16)
+        nc.scalar.copy(out=jj[:], in_=jj_f[:])
+
+        ca_t = keep.tile([P, HALVES * BLKS, P], F32)
+        for h in range(HALVES):
+            turned = psum.tile([P, BLKS, P], F32, tag="acc", bufs=2)
+            for fb in range(BLKS):
+                col0 = (h * BLKS + fb) * BLK
+                nc.tensor.transpose(out=turned[:, fb, :], in_=ca[:, col0 : col0 + BLK], identity=ident_f[:])
+            nc.scalar.copy(out=ca_t[:, h * BLKS : (h + 1) * BLKS, :], in_=turned[:])
+        gg_t = keep.tile([P, HALVES * BLKS, P], BF16)
+        jj_t = keep.tile([P, HALVES * BLKS, P], BF16)
+        for table, table_t in ((jj, jj_t), (gg, gg_t)):
+            turned = psum.tile([P, HALVES * BLKS, P], BF16, tag="acc", bufs=2)
+            for fb in range(HALVES * BLKS):
+                nc.tensor.transpose(out=turned[:, fb, :], in_=table[:, fb * BLK : (fb + 1) * BLK], identity=ident_b[:])
+            nc.scalar.copy(out=table_t[:], in_=turned[:])
+
+        x_b = setup.tile([P, 2, C], BF16)
+        nc.scalar.dma_start(out=x_b[lo, 0, :], in_=x_rows)
+        for s in range(PASSES):
+            graph = s // (PASSES // GRAPHS)
+            nc.scalar.dma_start(
+                out=x_b[s * NODES : (s + 1) * NODES, 1, :], in_=x_rows[graph * NODES : (graph + 1) * NODES, :]
+            )
+        x_tgt = keep.tile([P, C], F32)
+        nc.vector.memset(x_tgt[hi, :], 0.0)
+        nc.scalar.copy(out=x_tgt[lo, :], in_=x_b[lo, 0, :])
+        x_src = keep.tile([P, C], F32)
+        nc.scalar.copy(out=x_src[:], in_=x_b[:, 1, :])
+
+        e_codes = keep.tile([P, PASSES, C], U32, align_bytes=64)
+        e_scales = keep.tile([P, PASSES, C], U8, align_bytes=64)
+        for s in range(PASSES):
+            e_raw = e_pool.tile([P, PACK, C], BF16)
+            nc.sync.dma_start(
+                out=e_raw[:], in_=e_rows[s * K_PASS : (s + 1) * K_PASS, :].rearrange("(p t) c -> p t c", t=PACK)
+            )
+            e_grp = e_pool.tile([P, C, PACK], BF16, align_bytes=64)
+            nc.vector.tensor_copy(
+                out=e_grp[:].rearrange("p (c i) t -> p c t i", i=4), in_=e_raw[:].rearrange("p t (c i) -> p c t i", i=4)
+            )
+            nc.vector.quantize_mx(
+                out=e_codes[:, s, :].bitcast(E4M3X4), scales=e_scales[:, s, :], in_=e_grp[:].rearrange("p c t -> p (c t)")
+            )
+
+        def spread_tables(h, s):
+            spread = {}
+            for name, table_t, dtype, ident in (
+                ("ca", ca_t, F32, ident_f),
+                ("jj", jj_t, BF16, ident_b),
+                ("gg", gg_t, BF16, ident_b),
+            ):
+                repeated = rep_pool.tile([P, BLKS, 2, TARGETS, SPREAD], dtype, name="rep_" + name)
+                rows = table_t[:, h * BLKS : (h + 1) * BLKS, :].rearrange("p f (a n) -> p f a n", a=2)
+                rows = rows[:, :, :, s * TARGETS : (s + 1) * TARGETS]
+                nc.scalar.copy(out=repeated[:], in_=rows.unsqueeze(4).to_broadcast([P, BLKS, 2, TARGETS, SPREAD]))
+                for a in range(2):
+                    if dtype == F32:
+                        bank = psum.tile([P, HALF], F32, name="ps_" + name + str(a))
+                        spread[name + str(a)] = bank
+                    elif a == 0:
+                        pair = psum.tile([P, 2, HALF], BF16, name="ps_" + name)
+                        spread[name] = pair
+                        bank = pair[:, 0, :]
+                    else:
+                        bank = spread[name][:, 1, :]
+                    for fb in range(BLKS):
+                        nc.tensor.transpose(
+                            out=bank[:, fb * BLK : (fb + 1) * BLK],
+                            in_=repeated[:, fb, a].rearrange("p q r -> p (q r)"),
+                            identity=ident[:],
+                        )
+            jj_sb = work.tile([P, 2, HALF], BF16)
+            nc.scalar.copy(out=jj_sb[:], in_=spread["jj"][:])
+            spread["jj"] = jj_sb
+            return spread
+
+        def message_gradient(h, s, spread):
+            dm = m_pool.tile([P, PACK, HALF], F32)
+            nc.sync.dma_start(
+                out=dm[:],
+                in_=m_rows[s * K_PASS : (s + 1) * K_PASS, h * HALF : (h + 1) * HALF].rearrange("(p t) f -> p t f", t=PACK),
+            )
+            over_slots = [P, PACK, HALF]
+            nc.vector.tensor_tensor(out=dm[:], in0=dm[:], in1=spread["ca0"][:].unsqueeze(1).to_broadcast(over_slots), op=ALU.mult)
+            nc.vector.tensor_tensor(out=dm[:], in0=dm[:], in1=spread["ca1"][:].unsqueeze(1).to_broadcast(over_slots), op=ALU.add)
+            hit = work.tile([P, 2, PACK, HALF], BF16)
+            for t in range(PACK):
+                nc.vector.tensor_scalar(
+                    out=hit[:, :, t, :], in0=spread["jj"][:], scalar1=src_f[:, t : t + 1], scalar2=None, op0=ALU.is_equal
+                )
+            nc.vector.tensor_tensor(
+                out=hit[:], in0=hit[:], in1=spread["gg"][:].unsqueeze(2).to_broadcast([P, 2, PACK, HALF]), op=ALU.mult
+            )
+            nc.vector.tensor_tensor(out=dm[:], in0=dm[:], in1=hit[:, 0], op=ALU.add)
+            nc.vector.tensor_tensor(out=dm[:], in0=dm[:], in1=hit[:, 1], op=ALU.add)
+            return dm
+
+        def partial_sums(dm, s, sums_tgt_t, sums_src_t):
+            sums_ps = psum.tile([P, BLKS, SUMS], F32)
+            for fb in range(BLKS):
+                for t in range(PACK):
+                    nc.tensor.matmul(
+                        out=sums_ps[:, fb, :],
+                        lhsT=dm[:, t, fb * BLK : (fb + 1) * BLK],
+                        rhs=pick[:, t, :],
+                        start=(t == 0),
+                        stop=(t == PACK - 1),
+                    )
+            nc.scalar.copy(out=sums_tgt_t[:, :, s * TARGETS : (s + 1) * TARGETS], in_=sums_ps[:, :, 0:TARGETS])
+            nc.scalar.copy(out=sums_src_t[:, :, s * NODES : (s + 1) * NODES], in_=sums_ps[:, :, TARGETS:SUMS])
+
+        def quantise_gradient(dm, s, d_codes, d_scales):
+            d_grp = work.tile([P, HALF, PACK], BF16, align_bytes=64)
+            nc.scalar.copy(
+                out=d_grp[:].rearrange("p (c i) t -> p c t i", i=4), in_=dm[:].rearrange("p t (c i) -> p c t i", i=4)
+            )
+            nc.vector.quantize_mx(
+                out=d_codes[:, s, :].bitcast(E5M2X4), scales=d_scales[:, s, :], in_=d_grp[:].rearrange("p c t -> p (c t)")
+            )
+
+        def turn_sums(sums_t, label):
+            turned = psum.tile([P, HALF], F32, name="ps_turn")
+            for fb in range(BLKS):
+                nc.tensor.transpose(out=turned[:, fb * BLK : (fb + 1) * BLK], in_=sums_t[:, fb, :], identity=ident_f[:])
+            sums = per_half.tile([P, HALF], F32, name="sums_" + label)
+            nc.scalar.copy(out=sums[:], in_=turned[:])
+            return sums
+
+        def store(acc, row0, h, on_vector):
+            result = o_pool.tile([P, HALF], F32)
+            if on_vector:
+                nc.vector.tensor_copy(out=result[:], in_=acc[:])
+            else:
+                nc.scalar.copy(out=result[:], in_=acc[:])
+            nc.sync.dma_start(out=out[row0 : row0 + BLK, h * HALF : (h + 1) * HALF], in_=result[:])
+
+        def outputs(h, cb, done, vector_helps):
+            cols = slice(cb * BLK, (cb + 1) * BLK)
+            for third, (x_rows_t, sums) in enumerate(((x_tgt, done["tgt"]), (x_src, done["src"]))):
+                acc = psum.tile([P, HALF], F32, tag="acc", bufs=2)
+                nc.tensor.matmul(out=acc[:], lhsT=x_rows_t[:, cols], rhs=sums[:], start=True, stop=True)
+                store(acc, third * C + cb * BLK, h, vector_helps and third == 1)
+            acc = psum.tile([P, HALF], F32, tag="acc", bufs=2)
+            for s in range(PASSES):
+                nc.tensor.matmul_mx(
+                    out=acc[:],
+                    lhsT=e_codes[:, s, cols].bitcast(E4M3X4),
+                    lhsT_scale=e_scales[:, s, cols],
+                    rhs=done["codes"][:, s, :].bitcast(E5M2X4),
+                    rhs_scale=done["scales"][:, s, :],
+                    start=(s == 0),
+                    stop=(s == PASSES - 1),
+                )
+            store(acc, 2 * C + cb * BLK, h, vector_helps and cb % 2 == 1)
+
+        steps = [(h, s) for h in range(HALVES) for s in range(PASSES)]
+        done = {}
+        spread = spread_tables(0, 0)
+        for k, (h, s) in enumerate(steps):
+            if s == 0:
+                cur = {
+                    "codes": per_half.tile([P, PASSES, HALF], U32, align_bytes=64, name="d_codes"),
+                    "scales": per_half.tile([P, PASSES, HALF], U8, align_bytes=64, name="d_scales"),
+                }
+                sums_tgt_t = per_half.tile([P, BLKS, P], F32, name="tgt_t")
+                nc.vector.memset(sums_tgt_t[:, :, ALL_NODES:P], 0.0)
+                sums_src_t = per_half.tile([P, BLKS, P], F32, name="src_t")
+            dm = message_gradient(h, s, spread)
+            if k + 1 < len(steps):
+                spread = spread_tables(*steps[k + 1])
+            partial_sums(dm, s, sums_tgt_t, sums_src_t)
+            quantise_gradient(dm, s, cur["codes"], cur["scales"])
+            if h > 0:
+                for cb in range(s * C_BLKS // PASSES, (s + 1) * C_BLKS // PASSES):
+                    outputs(h - 1, cb, done, False)
+            if s == PASSES - 1:
+                cur["tgt"] = turn_sums(sums_tgt_t, "tgt")
+                cur["src"] = turn_sums(sums_src_t, "src")
+                done = cur
+        for cb in range(C_BLKS):
+            outputs(HALVES - 1, cb, done, True)

@@ -19,12 +19,16 @@ GRAPHS, NODES, C, F = 2, 32, 1024, 1024
 ALL_NODES = GRAPHS * NODES
 EDGES = ALL_NODES * NODES
 PASSES = EDGES // K_PASS
+PAIR = PASSES // GRAPHS
 TARGETS = K_PASS // NODES
 SPREAD = P // TARGETS
 HALF = 512
 HALVES = F // HALF
+QUARTER = 256
+QUARTERS = F // QUARTER
 BLK = 128
 BLKS = HALF // BLK
+Q_BLKS = QUARTER // BLK
 C_BLKS = C // BLK
 SUMS = TARGETS + NODES
 
@@ -40,8 +44,7 @@ def tile_gnnlayer_pa_v_kernel(tc, x, e_enc, W_pre, b_pre, m, stat, arg, grad_out
     stat_rows = stat.rearrange("b n s -> (b n) s")
     arg_rows = arg.rearrange("b n s -> (b n) s")
     g_rows = grad_out.rearrange("b n g -> (b n) g")
-    lo = slice(0, ALL_NODES)
-    hi = slice(ALL_NODES, P)
+    steps = [(g, b) for g in range(QUARTERS) for b in range(GRAPHS)]
 
     with ExitStack() as ctx:
         const = ctx.enter_context(tc.tile_pool(name="const", bufs=1))
@@ -49,19 +52,62 @@ def tile_gnnlayer_pa_v_kernel(tc, x, e_enc, W_pre, b_pre, m, stat, arg, grad_out
         setup = ctx.enter_context(tc.tile_pool(name="setup", bufs=1))
         e_pool = ctx.enter_context(tc.tile_pool(name="e_pool", bufs=2))
         rep_pool = ctx.enter_context(tc.tile_pool(name="rep_pool", bufs=2))
-        m_pool = ctx.enter_context(tc.tile_pool(name="m_pool", bufs=3))
+        m_pool = ctx.enter_context(tc.tile_pool(name="m_pool", bufs=4))
         work = ctx.enter_context(tc.tile_pool(name="work", bufs=2))
-        per_half = ctx.enter_context(tc.tile_pool(name="per_half", bufs=2))
         o_pool = ctx.enter_context(tc.tile_pool(name="o_pool", bufs=4))
         psum = ctx.enter_context(tc.psum_pool(name="psum", bufs=1))
+
+        def load_table(rows, col0, dtype, name):
+            table = setup.tile([P, HALF], dtype, name=name)
+            for h in range(HALVES):
+                nc.sync.dma_start(out=table[h:P:HALVES, :], in_=rows[:, col0 + h * HALF : col0 + (h + 1) * HALF])
+            return table
+
+        def load_edges(s):
+            e_raw = e_pool.tile([P, PACK, C], BF16, name="e_raw")
+            nc.sync.dma_start(
+                out=e_raw[:], in_=e_rows[s * K_PASS : (s + 1) * K_PASS, :].rearrange("(p t) c -> p t c", t=PACK)
+            )
+            return e_raw
+
+        def load_messages(g, b):
+            dm = m_pool.tile([P, PAIR, PACK, QUARTER], F32, name="dm")
+            for sp in range(PAIR):
+                row0 = (b * PAIR + sp) * K_PASS
+                nc.sync.dma_start(
+                    out=dm[:, sp],
+                    in_=m_rows[row0 : row0 + K_PASS, g * QUARTER : (g + 1) * QUARTER].rearrange("(p t) f -> p t f", t=PACK),
+                )
+            return dm
+
+        g_std = load_table(g_rows, 3 * F, BF16, "g_std")
+        rstd = load_table(stat_rows, F, F32, "rstd")
+        mean = load_table(stat_rows, 0, F32, "mean")
+        g_mean = load_table(g_rows, 0, BF16, "g_mean")
+        e_raw = {0: load_edges(0)}
+        dm_of = {0: load_messages(*steps[0])}
+        jmin = load_table(arg_rows, 0, F32, "jmin")
+        jmax = load_table(arg_rows, F, F32, "jmax")
+        g_min = load_table(g_rows, F, BF16, "g_min")
+        g_max = load_table(g_rows, 2 * F, BF16, "g_max")
+        dm_of[1] = load_messages(*steps[1])
+        e_raw[1] = load_edges(1)
+        x_b = setup.tile([P, 2, C], BF16)
+        nc.sync.dma_start(out=x_b[0:ALL_NODES, 0, :], in_=x_rows)
+        for s in range(PASSES):
+            graph = s // PAIR
+            nc.sync.dma_start(
+                out=x_b[s * NODES : (s + 1) * NODES, 1, :], in_=x_rows[graph * NODES : (graph + 1) * NODES, :]
+            )
 
         ident_f = const.tile([P, P], F32)
         make_identity(nc, ident_f[:])
         ident_b = const.tile([P, P], BF16)
         make_identity(nc, ident_b[:])
-
         edge_i = const.tile([P, PACK], I32)
         nc.gpsimd.iota(edge_i[:], pattern=[[1, PACK]], base=0, channel_multiplier=PACK)
+        col_i = const.tile([P, NODES], I32)
+        nc.gpsimd.iota(col_i[:], pattern=[[1, NODES]], base=0, channel_multiplier=0)
         src_i = const.tile([P, PACK], I32)
         nc.vector.tensor_single_scalar(out=src_i[:], in_=edge_i[:], scalar=NODES - 1, op=ALU.bitwise_and)
         src_f = const.tile([P, PACK], F32)
@@ -70,8 +116,6 @@ def tile_gnnlayer_pa_v_kernel(tc, x, e_enc, W_pre, b_pre, m, stat, arg, grad_out
         nc.vector.tensor_single_scalar(out=tgt_i[:], in_=edge_i[:, 0:1], scalar=5, op=ALU.logical_shift_right)
         tgt_f = const.tile([P, 1], F32)
         nc.vector.tensor_copy(out=tgt_f[:], in_=tgt_i[:])
-        col_i = const.tile([P, NODES], I32)
-        nc.gpsimd.iota(col_i[:], pattern=[[1, NODES]], base=0, channel_multiplier=0)
         col_f = const.tile([P, NODES], F32)
         nc.vector.tensor_copy(out=col_f[:], in_=col_i[:])
         pick = const.tile([P, PACK, SUMS], F32)
@@ -82,210 +126,216 @@ def tile_gnnlayer_pa_v_kernel(tc, x, e_enc, W_pre, b_pre, m, stat, arg, grad_out
             nc.vector.tensor_scalar(
                 out=pick[:, t, TARGETS:SUMS], in0=col_f[:], scalar1=src_f[:, t : t + 1], scalar2=None, op0=ALU.is_equal
             )
+        x_f = keep.tile([P, 2, C], F32)
+        nc.gpsimd.memset(x_f[ALL_NODES:P, 0, :], 0.0)
+        nc.gpsimd.tensor_copy(out=x_f[0:ALL_NODES, 0, :], in_=x_b[0:ALL_NODES, 0, :])
+        nc.gpsimd.tensor_copy(out=x_f[:, 1, :], in_=x_b[:, 1, :])
 
-        g_std2 = setup.tile([P, F], BF16)
-        rstd2 = setup.tile([P, F], F32)
-        mean_hi = setup.tile([P, F], F32)
-        g_mean_hi = setup.tile([P, F], BF16)
-        for rows in (lo, hi):
-            nc.scalar.dma_start(out=g_std2[rows, :], in_=g_rows[:, 3 * F : 4 * F])
-            nc.scalar.dma_start(out=rstd2[rows, :], in_=stat_rows[:, F : 2 * F])
-        nc.scalar.dma_start(out=mean_hi[hi, :], in_=stat_rows[:, 0:F])
-        nc.scalar.dma_start(out=g_mean_hi[hi, :], in_=g_rows[:, 0:F])
-        ca = setup.tile([P, F], F32)
+        c_tab = setup.tile([P, HALF], F32)
         nc.vector.scalar_tensor_tensor(
-            out=ca[:], in0=g_std2[:], scalar=1.0 / NODES, in1=rstd2[:], op0=ALU.mult, op1=ALU.mult
+            out=c_tab[:], in0=g_std[:], scalar=1.0 / NODES, in1=rstd[:], op0=ALU.mult, op1=ALU.mult
         )
-        nc.vector.tensor_tensor(out=mean_hi[hi, :], in0=ca[hi, :], in1=mean_hi[hi, :], op=ALU.mult)
+        nc.vector.tensor_tensor(out=mean[:], in0=c_tab[:], in1=mean[:], op=ALU.mult)
+        a_tab = setup.tile([P, HALF], F32)
         nc.vector.scalar_tensor_tensor(
-            out=ca[hi, :], in0=g_mean_hi[hi, :], scalar=1.0 / NODES, in1=mean_hi[hi, :], op0=ALU.mult, op1=ALU.subtract
+            out=a_tab[:], in0=g_mean[:], scalar=1.0 / NODES, in1=mean[:], op0=ALU.mult, op1=ALU.subtract
         )
-        gg = setup.tile([P, F], BF16)
-        nc.scalar.dma_start(out=gg[lo, :], in_=g_rows[:, F : 2 * F])
-        nc.scalar.dma_start(out=gg[hi, :], in_=g_rows[:, 2 * F : 3 * F])
-        jj_f = setup.tile([P, F], F32)
-        nc.scalar.dma_start(out=jj_f[lo, :], in_=arg_rows[:, 0:F])
-        nc.scalar.dma_start(out=jj_f[hi, :], in_=arg_rows[:, F : 2 * F])
-        jj = setup.tile([P, F], BF16)
-        nc.scalar.copy(out=jj[:], in_=jj_f[:])
 
-        ca_t = keep.tile([P, HALVES * BLKS, P], F32)
-        for h in range(HALVES):
-            turned = psum.tile([P, BLKS, P], F32, tag="acc", bufs=2)
-            for fb in range(BLKS):
-                col0 = (h * BLKS + fb) * BLK
-                nc.tensor.transpose(out=turned[:, fb, :], in_=ca[:, col0 : col0 + BLK], identity=ident_f[:])
-            nc.scalar.copy(out=ca_t[:, h * BLKS : (h + 1) * BLKS, :], in_=turned[:])
-        gg_t = keep.tile([P, HALVES * BLKS, P], BF16)
-        jj_t = keep.tile([P, HALVES * BLKS, P], BF16)
-        for table, table_t in ((jj, jj_t), (gg, gg_t)):
-            turned = psum.tile([P, HALVES * BLKS, P], BF16, tag="acc", bufs=2)
-            for fb in range(HALVES * BLKS):
-                nc.tensor.transpose(out=turned[:, fb, :], in_=table[:, fb * BLK : (fb + 1) * BLK], identity=ident_b[:])
-            nc.scalar.copy(out=table_t[:], in_=turned[:])
+        def turn_tables(pair, ident, out_dtype, name):
+            turned_sb = keep.tile([P, BLKS, 2, P], out_dtype, name=name)
+            for a, table in enumerate(pair):
+                turned = psum.tile([P, BLKS, P], table.dtype, tag="acc", bufs=2, name="turned")
+                for fb in range(BLKS):
+                    nc.tensor.transpose(out=turned[:, fb, :], in_=table[:, fb * BLK : (fb + 1) * BLK], identity=ident[:])
+                nc.scalar.copy(out=turned_sb[:, :, a, :], in_=turned[:])
+            return turned_sb
 
-        x_b = setup.tile([P, 2, C], BF16)
-        nc.scalar.dma_start(out=x_b[lo, 0, :], in_=x_rows)
-        for s in range(PASSES):
-            graph = s // (PASSES // GRAPHS)
-            nc.scalar.dma_start(
-                out=x_b[s * NODES : (s + 1) * NODES, 1, :], in_=x_rows[graph * NODES : (graph + 1) * NODES, :]
-            )
-        x_tgt = keep.tile([P, C], F32)
-        nc.vector.memset(x_tgt[hi, :], 0.0)
-        nc.scalar.copy(out=x_tgt[lo, :], in_=x_b[lo, 0, :])
-        x_src = keep.tile([P, C], F32)
-        nc.scalar.copy(out=x_src[:], in_=x_b[:, 1, :])
+        def repeat_rows(turned_sb, g, b, name):
+            repeated = rep_pool.tile([P, Q_BLKS, 2, NODES, SPREAD], turned_sb.dtype, name=name)
+            h, fb0 = g // HALVES, (g % HALVES) * Q_BLKS
+            rows = turned_sb[:].rearrange("p f a (n h) -> p f a n h", h=HALVES)
+            rows = rows[:, fb0 : fb0 + Q_BLKS, :, b * NODES : (b + 1) * NODES, h]
+            nc.scalar.copy(out=repeated[:], in_=rows.unsqueeze(4).to_broadcast([P, Q_BLKS, 2, NODES, SPREAD]))
+            return repeated
 
-        e_codes = keep.tile([P, PASSES, C], U32, align_bytes=64)
-        e_scales = keep.tile([P, PASSES, C], U8, align_bytes=64)
-        for s in range(PASSES):
-            e_raw = e_pool.tile([P, PACK, C], BF16)
-            nc.sync.dma_start(
-                out=e_raw[:], in_=e_rows[s * K_PASS : (s + 1) * K_PASS, :].rearrange("(p t) c -> p t c", t=PACK)
-            )
-            e_grp = e_pool.tile([P, C, PACK], BF16, align_bytes=64)
-            nc.vector.tensor_copy(
-                out=e_grp[:].rearrange("p (c i) t -> p c t i", i=4), in_=e_raw[:].rearrange("p t (c i) -> p c t i", i=4)
-            )
-            nc.vector.quantize_mx(
-                out=e_codes[:, s, :].bitcast(E4M3X4), scales=e_scales[:, s, :], in_=e_grp[:].rearrange("p c t -> p (c t)")
-            )
-
-        def spread_tables(h, s):
-            spread = {}
-            for name, table_t, dtype, ident in (
-                ("ca", ca_t, F32, ident_f),
-                ("jj", jj_t, BF16, ident_b),
-                ("gg", gg_t, BF16, ident_b),
-            ):
-                repeated = rep_pool.tile([P, BLKS, 2, TARGETS, SPREAD], dtype, name="rep_" + name)
-                rows = table_t[:, h * BLKS : (h + 1) * BLKS, :].rearrange("p f (a n) -> p f a n", a=2)
-                rows = rows[:, :, :, s * TARGETS : (s + 1) * TARGETS]
-                nc.scalar.copy(out=repeated[:], in_=rows.unsqueeze(4).to_broadcast([P, BLKS, 2, TARGETS, SPREAD]))
-                for a in range(2):
-                    if dtype == F32:
-                        bank = psum.tile([P, HALF], F32, name="ps_" + name + str(a))
-                        spread[name + str(a)] = bank
-                    elif a == 0:
-                        pair = psum.tile([P, 2, HALF], BF16, name="ps_" + name)
-                        spread[name] = pair
-                        bank = pair[:, 0, :]
-                    else:
-                        bank = spread[name][:, 1, :]
-                    for fb in range(BLKS):
+        def turn_back(repeated, ident, name):
+            spread = psum.tile([P, 2, PAIR, QUARTER], repeated.dtype, name=name)
+            for a in range(2):
+                for sp in range(PAIR):
+                    for fb in range(Q_BLKS):
                         nc.tensor.transpose(
-                            out=bank[:, fb * BLK : (fb + 1) * BLK],
-                            in_=repeated[:, fb, a].rearrange("p q r -> p (q r)"),
+                            out=spread[:, a, sp, fb * BLK : (fb + 1) * BLK],
+                            in_=repeated[:, fb, a, sp * TARGETS : (sp + 1) * TARGETS, :].rearrange("p q r -> p (q r)"),
                             identity=ident[:],
                         )
-            jj_sb = work.tile([P, 2, HALF], BF16)
-            nc.scalar.copy(out=jj_sb[:], in_=spread["jj"][:])
-            spread["jj"] = jj_sb
             return spread
 
-        def message_gradient(h, s, spread):
-            dm = m_pool.tile([P, PACK, HALF], F32)
-            nc.sync.dma_start(
-                out=dm[:],
-                in_=m_rows[s * K_PASS : (s + 1) * K_PASS, h * HALF : (h + 1) * HALF].rearrange("(p t) f -> p t f", t=PACK),
-            )
-            over_slots = [P, PACK, HALF]
-            nc.vector.tensor_tensor(out=dm[:], in0=dm[:], in1=spread["ca0"][:].unsqueeze(1).to_broadcast(over_slots), op=ALU.mult)
-            nc.vector.tensor_tensor(out=dm[:], in0=dm[:], in1=spread["ca1"][:].unsqueeze(1).to_broadcast(over_slots), op=ALU.add)
-            hit = work.tile([P, 2, PACK, HALF], BF16)
-            for t in range(PACK):
-                nc.vector.tensor_scalar(
-                    out=hit[:, :, t, :], in0=spread["jj"][:], scalar1=src_f[:, t : t + 1], scalar2=None, op0=ALU.is_equal
-                )
-            nc.vector.tensor_tensor(
-                out=hit[:], in0=hit[:], in1=spread["gg"][:].unsqueeze(2).to_broadcast([P, 2, PACK, HALF]), op=ALU.mult
-            )
-            nc.vector.tensor_tensor(out=dm[:], in0=dm[:], in1=hit[:, 0], op=ALU.add)
-            nc.vector.tensor_tensor(out=dm[:], in0=dm[:], in1=hit[:, 1], op=ALU.add)
-            return dm
+        def to_sbuf(spread):
+            jj_sb = work.tile([P, 2, PAIR, QUARTER], BF16, name="jj_sb")
+            nc.scalar.copy(out=jj_sb[:], in_=spread[:])
+            return jj_sb
 
-        def partial_sums(dm, s, sums_tgt_t, sums_src_t):
-            sums_ps = psum.tile([P, BLKS, SUMS], F32)
-            for fb in range(BLKS):
-                for t in range(PACK):
-                    nc.tensor.matmul(
-                        out=sums_ps[:, fb, :],
-                        lhsT=dm[:, t, fb * BLK : (fb + 1) * BLK],
-                        rhs=pick[:, t, :],
-                        start=(t == 0),
-                        stop=(t == PACK - 1),
-                    )
-            nc.scalar.copy(out=sums_tgt_t[:, :, s * TARGETS : (s + 1) * TARGETS], in_=sums_ps[:, :, 0:TARGETS])
-            nc.scalar.copy(out=sums_src_t[:, :, s * NODES : (s + 1) * NODES], in_=sums_ps[:, :, TARGETS:SUMS])
+        def regroup(engine_copy, grouped, raw):
+            engine_copy(out=grouped.rearrange("p (c i) t -> p c t i", i=4), in_=raw.rearrange("p t (c i) -> p c t i", i=4))
 
-        def quantise_gradient(dm, s, d_codes, d_scales):
-            d_grp = work.tile([P, HALF, PACK], BF16, align_bytes=64)
+        def quantise(grouped, codes, scales, fmt):
+            nc.vector.quantize_mx(out=codes.bitcast(fmt), scales=scales, in_=grouped.rearrange("p c t -> p (c t)"))
+
+        def regroup_edges(s):
+            e_grp = work.tile([P, C, PACK], BF16, align_bytes=64, name="e_grp")
+            regroup(nc.vector.tensor_copy, e_grp[:], e_raw[s][:])
+            return e_grp
+
+        def regroup_gradient(dm):
+            d_grp = work.tile([P, PAIR, QUARTER, PACK], BF16, align_bytes=64, name="d_grp")
+            for sp in range(PAIR):
+                regroup(nc.scalar.copy, d_grp[:, sp], dm[:, sp])
+            return d_grp
+
+        def quantise_gradient(d_grp, g, b, d_mx):
+            cols = slice((g % HALVES) * QUARTER, (g % HALVES + 1) * QUARTER)
+            for sp in range(PAIR):
+                s = b * PAIR + sp
+                quantise(d_grp[:, sp], d_mx["codes"][:, s, cols], d_mx["scales"][:, s, cols], E5M2X4)
+
+        def partial_sums(dm, b, sums_ps):
+            for sp in range(PAIR):
+                for fb in range(Q_BLKS):
+                    for t in range(PACK):
+                        nc.tensor.matmul(
+                            out=sums_ps[:, b * PAIR + sp, fb, :],
+                            lhsT=dm[:, sp, t, fb * BLK : (fb + 1) * BLK],
+                            rhs=pick[:, t, :],
+                            start=(t == 0),
+                            stop=(t == PACK - 1),
+                        )
+
+        def turn_sums(sums_ps):
+            sums_t = work.tile([P, 2, Q_BLKS, P], F32, name="sums_t")
+            nc.gpsimd.memset(sums_t[:, 0, :, ALL_NODES:P], 0.0)
             nc.scalar.copy(
-                out=d_grp[:].rearrange("p (c i) t -> p c t i", i=4), in_=dm[:].rearrange("p t (c i) -> p c t i", i=4)
+                out=sums_t[:, 0, :, 0:ALL_NODES].rearrange("p f (s q) -> p s f q", q=TARGETS), in_=sums_ps[:, :, :, 0:TARGETS]
             )
-            nc.vector.quantize_mx(
-                out=d_codes[:, s, :].bitcast(E5M2X4), scales=d_scales[:, s, :], in_=d_grp[:].rearrange("p c t -> p (c t)")
-            )
-
-        def turn_sums(sums_t, label):
-            turned = psum.tile([P, HALF], F32, name="ps_turn")
-            for fb in range(BLKS):
-                nc.tensor.transpose(out=turned[:, fb * BLK : (fb + 1) * BLK], in_=sums_t[:, fb, :], identity=ident_f[:])
-            sums = per_half.tile([P, HALF], F32, name="sums_" + label)
+            nc.scalar.copy(out=sums_t[:, 1].rearrange("p f (s j) -> p s f j", j=NODES), in_=sums_ps[:, :, :, TARGETS:SUMS])
+            turned = psum.tile([P, 2, QUARTER], F32, name="ps_turn")
+            for plane in range(2):
+                for fb in range(Q_BLKS):
+                    nc.tensor.transpose(
+                        out=turned[:, plane, fb * BLK : (fb + 1) * BLK], in_=sums_t[:, plane, fb, :], identity=ident_f[:]
+                    )
+            sums = work.tile([P, 2, QUARTER], F32, name="sums")
             nc.scalar.copy(out=sums[:], in_=turned[:])
             return sums
 
-        def store(acc, row0, h, on_vector):
-            result = o_pool.tile([P, HALF], F32)
+        def leave_psum(acc, on_vector):
+            result = o_pool.tile([P, HALF], F32, name="result")
             if on_vector:
-                nc.vector.tensor_copy(out=result[:], in_=acc[:])
+                nc.vector.tensor_copy(out=result[:], in_=acc)
             else:
-                nc.scalar.copy(out=result[:], in_=acc[:])
-            nc.sync.dma_start(out=out[row0 : row0 + BLK, h * HALF : (h + 1) * HALF], in_=result[:])
+                nc.scalar.copy(out=result[:], in_=acc)
+            return result
 
-        def outputs(h, cb, done, vector_helps):
+        def node_products(g, cb, sums, on_vector):
+            acc = psum.tile([P, 2, QUARTER], F32, tag="acc", bufs=2, name="acc")
+            for plane in range(2):
+                nc.tensor.matmul(
+                    out=acc[:, plane, :], lhsT=x_f[:, plane, cb * BLK : (cb + 1) * BLK], rhs=sums[:, plane, :], start=True, stop=True
+                )
+            result = leave_psum(acc[:].rearrange("p a f -> p (a f)"), on_vector)
+            both = out[0 : 2 * C, g * QUARTER : (g + 1) * QUARTER].rearrange("(a r) f -> r a f", a=2)
+            nc.sync.dma_start(out=both[cb * BLK : (cb + 1) * BLK], in_=result[:].rearrange("p (a f) -> p a f", a=2))
+
+        def edge_product(h, cb, d_mx, on_vector):
             cols = slice(cb * BLK, (cb + 1) * BLK)
-            for third, (x_rows_t, sums) in enumerate(((x_tgt, done["tgt"]), (x_src, done["src"]))):
-                acc = psum.tile([P, HALF], F32, tag="acc", bufs=2)
-                nc.tensor.matmul(out=acc[:], lhsT=x_rows_t[:, cols], rhs=sums[:], start=True, stop=True)
-                store(acc, third * C + cb * BLK, h, vector_helps and third == 1)
-            acc = psum.tile([P, HALF], F32, tag="acc", bufs=2)
+            acc = psum.tile([P, HALF], F32, tag="acc", bufs=2, name="acc")
             for s in range(PASSES):
                 nc.tensor.matmul_mx(
                     out=acc[:],
                     lhsT=e_codes[:, s, cols].bitcast(E4M3X4),
                     lhsT_scale=e_scales[:, s, cols],
-                    rhs=done["codes"][:, s, :].bitcast(E5M2X4),
-                    rhs_scale=done["scales"][:, s, :],
+                    rhs=d_mx["codes"][:, s, :].bitcast(E5M2X4),
+                    rhs_scale=d_mx["scales"][:, s, :],
                     start=(s == 0),
                     stop=(s == PASSES - 1),
                 )
-            store(acc, 2 * C + cb * BLK, h, vector_helps and cb % 2 == 1)
+            result = leave_psum(acc[:], on_vector)
+            row0 = 2 * C + cb * BLK
+            nc.sync.dma_start(out=out[row0 : row0 + BLK, h * HALF : (h + 1) * HALF], in_=result[:])
 
-        steps = [(h, s) for h in range(HALVES) for s in range(PASSES)]
-        done = {}
-        spread = spread_tables(0, 0)
-        for k, (h, s) in enumerate(steps):
-            if s == 0:
-                cur = {
-                    "codes": per_half.tile([P, PASSES, HALF], U32, align_bytes=64, name="d_codes"),
-                    "scales": per_half.tile([P, PASSES, HALF], U8, align_bytes=64, name="d_scales"),
-                }
-                sums_tgt_t = per_half.tile([P, BLKS, P], F32, name="tgt_t")
-                nc.vector.memset(sums_tgt_t[:, :, ALL_NODES:P], 0.0)
-                sums_src_t = per_half.tile([P, BLKS, P], F32, name="src_t")
-            dm = message_gradient(h, s, spread)
+        e_codes = keep.tile([P, PASSES, C], U32, align_bytes=64)
+        e_scales = keep.tile([P, PASSES, C], U8, align_bytes=64)
+        d_mx_of = {}
+        for h in range(HALVES):
+            d_mx_of[h] = {
+                "codes": keep.tile([P, PASSES, HALF], U32, align_bytes=64, name="d_codes" + str(h)),
+                "scales": keep.tile([P, PASSES, HALF], U8, align_bytes=64, name="d_scales" + str(h)),
+            }
+        ca_t = turn_tables((c_tab, a_tab), ident_f, F32, "ca_t")
+        ca_rep = repeat_rows(ca_t, 0, 0, "ca_rep")
+        nxt = {"ca": turn_back(ca_rep, ident_f, "ca_ps")}
+        jj_t = turn_tables((jmin, jmax), ident_f, BF16, "jj_t")
+        jj_rep = repeat_rows(jj_t, 0, 0, "jj_rep")
+        nxt["jj"] = to_sbuf(turn_back(jj_rep, ident_b, "jj_ps"))
+        gg_t = turn_tables((g_min, g_max), ident_b, BF16, "gg_t")
+        gg_rep = repeat_rows(gg_t, 0, 0, "gg_rep")
+        nxt["gg"] = turn_back(gg_rep, ident_b, "gg_ps")
+        e_grp = {0: regroup_edges(0)}
+
+        over_slots = [P, PAIR, PACK, QUARTER]
+        d_grp = {}
+        sums_of = {}
+        for k, (g, b) in enumerate(steps):
+            now = nxt
+            if k + 2 < len(steps):
+                dm_of[k + 2] = load_messages(*steps[k + 2])
+            if k + 2 < PASSES:
+                e_raw[k + 2] = load_edges(k + 2)
+            dm = dm_of[k]
+            if b == 0:
+                sums_ps = psum.tile([P, PASSES, Q_BLKS, SUMS], F32, name="sums_ps")
+
+            hit = work.tile([P, 2, PAIR, PACK, QUARTER], BF16, name="hit")
+            nc.vector.tensor_tensor(out=dm[:], in0=dm[:], in1=now["ca"][:, 0].unsqueeze(2).to_broadcast(over_slots), op=ALU.mult)
+            for t in range(PACK):
+                nc.vector.tensor_scalar(
+                    out=hit[:, :, :, t, :], in0=now["jj"][:], scalar1=src_f[:, t : t + 1], scalar2=None, op0=ALU.is_equal
+                )
+            nc.vector.tensor_tensor(out=dm[:], in0=dm[:], in1=now["ca"][:, 1].unsqueeze(2).to_broadcast(over_slots), op=ALU.add)
+            nc.vector.tensor_tensor(
+                out=hit[:], in0=hit[:], in1=now["gg"][:].unsqueeze(3).to_broadcast([P, 2] + over_slots[1:]), op=ALU.mult
+            )
+            if k > 0:
+                was_g, was_b = steps[k - 1]
+                quantise_gradient(d_grp[k - 1], was_g, was_b, d_mx_of[was_g // HALVES])
+            if k < PASSES:
+                quantise(e_grp[k][:], e_codes[:, k, :], e_scales[:, k, :], E4M3X4)
+            nc.vector.tensor_tensor(out=dm[:], in0=dm[:], in1=hit[:, 0], op=ALU.add)
+            nc.gpsimd.tensor_tensor(out=dm[:], in0=dm[:], in1=hit[:, 1], op=ALU.add)
+            if k + 1 < PASSES:
+                e_grp[k + 1] = regroup_edges(k + 1)
+
             if k + 1 < len(steps):
-                spread = spread_tables(*steps[k + 1])
-            partial_sums(dm, s, sums_tgt_t, sums_src_t)
-            quantise_gradient(dm, s, cur["codes"], cur["scales"])
-            if h > 0:
-                for cb in range(s * C_BLKS // PASSES, (s + 1) * C_BLKS // PASSES):
-                    outputs(h - 1, cb, done, False)
-            if s == PASSES - 1:
-                cur["tgt"] = turn_sums(sums_tgt_t, "tgt")
-                cur["src"] = turn_sums(sums_src_t, "src")
-                done = cur
+                ca_rep = repeat_rows(ca_t, *steps[k + 1], "ca_rep")
+                jj_rep = repeat_rows(jj_t, *steps[k + 1], "jj_rep")
+                gg_rep = repeat_rows(gg_t, *steps[k + 1], "gg_rep")
+                nxt = {"ca": turn_back(ca_rep, ident_f, "ca_ps")}
+                nxt["jj"] = to_sbuf(turn_back(jj_rep, ident_b, "jj_ps"))
+            if g > 0:
+                for cb in range(b * C_BLKS // GRAPHS, (b + 1) * C_BLKS // GRAPHS):
+                    node_products(g - 1, cb, sums_of[g - 1], False)
+            if g >= HALVES:
+                first = (k - len(steps) // HALVES) * HALVES
+                for cb in range(first, first + HALVES):
+                    edge_product(0, cb, d_mx_of[0], True)
+            if k + 1 < len(steps):
+                nxt["gg"] = turn_back(gg_rep, ident_b, "gg_ps")
+
+            d_grp[k] = regroup_gradient(dm)
+            partial_sums(dm, b, sums_ps)
+            if b == GRAPHS - 1:
+                sums_of[g] = turn_sums(sums_ps)
+
+        quantise_gradient(d_grp[len(steps) - 1], *steps[-1], d_mx_of[HALVES - 1])
         for cb in range(C_BLKS):
-            outputs(HALVES - 1, cb, done, True)
+            edge_product(HALVES - 1, cb, d_mx_of[HALVES - 1], True)
+            node_products(QUARTERS - 1, cb, sums_of[QUARTERS - 1], False)

@@ -54,7 +54,7 @@ def tile_gnnlayer_pa_v_kernel(tc, x, e_enc, W_pre, b_pre, m, stat, arg, grad_out
         rep_pool = ctx.enter_context(tc.tile_pool(name="rep_pool", bufs=2))
         m_pool = ctx.enter_context(tc.tile_pool(name="m_pool", bufs=4))
         work = ctx.enter_context(tc.tile_pool(name="work", bufs=2))
-        o_pool = ctx.enter_context(tc.tile_pool(name="o_pool", bufs=4))
+        o_pool = ctx.enter_context(tc.tile_pool(name="o_pool", bufs=6))
         psum = ctx.enter_context(tc.psum_pool(name="psum", bufs=1))
 
         def load_table(rows, col0, dtype, name):
@@ -85,13 +85,13 @@ def tile_gnnlayer_pa_v_kernel(tc, x, e_enc, W_pre, b_pre, m, stat, arg, grad_out
         mean = load_table(stat_rows, 0, F32, "mean")
         g_mean = load_table(g_rows, 0, BF16, "g_mean")
         e_raw = {0: load_edges(0)}
-        dm_of = {0: load_messages(*steps[0])}
         jmin = load_table(arg_rows, 0, F32, "jmin")
         jmax = load_table(arg_rows, F, F32, "jmax")
         g_min = load_table(g_rows, F, BF16, "g_min")
         g_max = load_table(g_rows, 2 * F, BF16, "g_max")
-        dm_of[1] = load_messages(*steps[1])
         e_raw[1] = load_edges(1)
+        dm_of = {0: load_messages(*steps[0])}
+        dm_of[1] = load_messages(*steps[1])
         x_b = setup.tile([P, 2, C], BF16)
         nc.sync.dma_start(out=x_b[0:ALL_NODES, 0, :], in_=x_rows)
         for s in range(PASSES):
@@ -144,7 +144,7 @@ def tile_gnnlayer_pa_v_kernel(tc, x, e_enc, W_pre, b_pre, m, stat, arg, grad_out
         def turn_tables(pair, ident, out_dtype, name):
             turned_sb = keep.tile([P, BLKS, 2, P], out_dtype, name=name)
             for a, table in enumerate(pair):
-                turned = psum.tile([P, BLKS, P], table.dtype, tag="acc", bufs=2, name="turned")
+                turned = psum.tile([P, BLKS, P], table.dtype, tag="acc", bufs=4, name="turned")
                 for fb in range(BLKS):
                     nc.tensor.transpose(out=turned[:, fb, :], in_=table[:, fb * BLK : (fb + 1) * BLK], identity=ident[:])
                 nc.scalar.copy(out=turned_sb[:, :, a, :], in_=turned[:])
@@ -158,8 +158,8 @@ def tile_gnnlayer_pa_v_kernel(tc, x, e_enc, W_pre, b_pre, m, stat, arg, grad_out
             nc.scalar.copy(out=repeated[:], in_=rows.unsqueeze(4).to_broadcast([P, Q_BLKS, 2, NODES, SPREAD]))
             return repeated
 
-        def turn_back(repeated, ident, name):
-            spread = psum.tile([P, 2, PAIR, QUARTER], repeated.dtype, name=name)
+        def turn_back(repeated, ident, name, tag, bufs):
+            spread = psum.tile([P, 2, PAIR, QUARTER], repeated.dtype, name=name, tag=tag, bufs=bufs)
             for a in range(2):
                 for sp in range(PAIR):
                     for fb in range(Q_BLKS):
@@ -183,7 +183,7 @@ def tile_gnnlayer_pa_v_kernel(tc, x, e_enc, W_pre, b_pre, m, stat, arg, grad_out
 
         def regroup_edges(s):
             e_grp = work.tile([P, C, PACK], BF16, align_bytes=64, name="e_grp")
-            regroup(nc.vector.tensor_copy, e_grp[:], e_raw[s][:])
+            regroup(nc.vector.tensor_copy if s < PAIR else nc.scalar.copy, e_grp[:], e_raw[s][:])
             return e_grp
 
         def regroup_gradient(dm):
@@ -217,7 +217,7 @@ def tile_gnnlayer_pa_v_kernel(tc, x, e_enc, W_pre, b_pre, m, stat, arg, grad_out
                 out=sums_t[:, 0, :, 0:ALL_NODES].rearrange("p f (s q) -> p s f q", q=TARGETS), in_=sums_ps[:, :, :, 0:TARGETS]
             )
             nc.scalar.copy(out=sums_t[:, 1].rearrange("p f (s j) -> p s f j", j=NODES), in_=sums_ps[:, :, :, TARGETS:SUMS])
-            turned = psum.tile([P, 2, QUARTER], F32, name="ps_turn")
+            turned = psum.tile([P, 2, QUARTER], F32, tag="acc", bufs=4, name="ps_turn")
             for plane in range(2):
                 for fb in range(Q_BLKS):
                     nc.tensor.transpose(
@@ -236,7 +236,7 @@ def tile_gnnlayer_pa_v_kernel(tc, x, e_enc, W_pre, b_pre, m, stat, arg, grad_out
             return result
 
         def node_products(g, cb, sums, on_vector):
-            acc = psum.tile([P, 2, QUARTER], F32, tag="acc", bufs=2, name="acc")
+            acc = psum.tile([P, 2, QUARTER], F32, tag="acc", bufs=4, name="acc")
             for plane in range(2):
                 nc.tensor.matmul(
                     out=acc[:, plane, :], lhsT=x_f[:, plane, cb * BLK : (cb + 1) * BLK], rhs=sums[:, plane, :], start=True, stop=True
@@ -247,7 +247,7 @@ def tile_gnnlayer_pa_v_kernel(tc, x, e_enc, W_pre, b_pre, m, stat, arg, grad_out
 
         def edge_product(h, cb, d_mx, on_vector):
             cols = slice(cb * BLK, (cb + 1) * BLK)
-            acc = psum.tile([P, HALF], F32, tag="acc", bufs=2, name="acc")
+            acc = psum.tile([P, HALF], F32, tag="acc", bufs=4, name="acc")
             for s in range(PASSES):
                 nc.tensor.matmul_mx(
                     out=acc[:],
@@ -272,13 +272,13 @@ def tile_gnnlayer_pa_v_kernel(tc, x, e_enc, W_pre, b_pre, m, stat, arg, grad_out
             }
         ca_t = turn_tables((c_tab, a_tab), ident_f, F32, "ca_t")
         ca_rep = repeat_rows(ca_t, 0, 0, "ca_rep")
-        nxt = {"ca": turn_back(ca_rep, ident_f, "ca_ps")}
+        nxt = {"ca": turn_back(ca_rep, ident_f, "ca_ps", "ca_ps", 1)}
         jj_t = turn_tables((jmin, jmax), ident_f, BF16, "jj_t")
         jj_rep = repeat_rows(jj_t, 0, 0, "jj_rep")
-        nxt["jj"] = to_sbuf(turn_back(jj_rep, ident_b, "jj_ps"))
+        nxt["jj"] = to_sbuf(turn_back(jj_rep, ident_b, "jj_ps", "acc", 4))
         gg_t = turn_tables((g_min, g_max), ident_b, BF16, "gg_t")
         gg_rep = repeat_rows(gg_t, 0, 0, "gg_rep")
-        nxt["gg"] = turn_back(gg_rep, ident_b, "gg_ps")
+        nxt["gg"] = turn_back(gg_rep, ident_b, "gg_ps", "gg_ps", 1)
         e_grp = {0: regroup_edges(0)}
 
         over_slots = [P, PAIR, PACK, QUARTER]
@@ -310,7 +310,8 @@ def tile_gnnlayer_pa_v_kernel(tc, x, e_enc, W_pre, b_pre, m, stat, arg, grad_out
             if k < PASSES:
                 quantise(e_grp[k][:], e_codes[:, k, :], e_scales[:, k, :], E4M3X4)
             nc.vector.tensor_tensor(out=dm[:], in0=dm[:], in1=hit[:, 0], op=ALU.add)
-            nc.gpsimd.tensor_tensor(out=dm[:], in0=dm[:], in1=hit[:, 1], op=ALU.add)
+            second_adder = nc.gpsimd if k + 1 < len(steps) else nc.vector
+            second_adder.tensor_tensor(out=dm[:], in0=dm[:], in1=hit[:, 1], op=ALU.add)
             if k + 1 < PASSES:
                 e_grp[k + 1] = regroup_edges(k + 1)
 
@@ -318,8 +319,8 @@ def tile_gnnlayer_pa_v_kernel(tc, x, e_enc, W_pre, b_pre, m, stat, arg, grad_out
                 ca_rep = repeat_rows(ca_t, *steps[k + 1], "ca_rep")
                 jj_rep = repeat_rows(jj_t, *steps[k + 1], "jj_rep")
                 gg_rep = repeat_rows(gg_t, *steps[k + 1], "gg_rep")
-                nxt = {"ca": turn_back(ca_rep, ident_f, "ca_ps")}
-                nxt["jj"] = to_sbuf(turn_back(jj_rep, ident_b, "jj_ps"))
+                nxt = {"ca": turn_back(ca_rep, ident_f, "ca_ps", "ca_ps", 1)}
+                nxt["jj"] = to_sbuf(turn_back(jj_rep, ident_b, "jj_ps", "acc", 4))
             if g > 0:
                 for cb in range(b * C_BLKS // GRAPHS, (b + 1) * C_BLKS // GRAPHS):
                     node_products(g - 1, cb, sums_of[g - 1], False)
@@ -328,7 +329,7 @@ def tile_gnnlayer_pa_v_kernel(tc, x, e_enc, W_pre, b_pre, m, stat, arg, grad_out
                 for cb in range(first, first + HALVES):
                     edge_product(0, cb, d_mx_of[0], True)
             if k + 1 < len(steps):
-                nxt["gg"] = turn_back(gg_rep, ident_b, "gg_ps")
+                nxt["gg"] = turn_back(gg_rep, ident_b, "gg_ps", "gg_ps", 1)
 
             d_grp[k] = regroup_gradient(dm)
             partial_sums(dm, b, sums_ps)

@@ -26,11 +26,14 @@ HALF = 512
 HALVES = F // HALF
 QUARTER = 256
 QUARTERS = F // QUARTER
+QUARTERS_IN_HALF = HALF // QUARTER
 BLK = 128
 BLKS = HALF // BLK
 Q_BLKS = QUARTER // BLK
 C_BLKS = C // BLK
 SUMS = TARGETS + NODES
+STEPS = QUARTERS * GRAPHS
+SHORT_LIVED_BANKS = 4
 
 FLOPS = 2 * EDGES * C * F + 2 * 2 * ALL_NODES * C * F
 BYTES = 2 * (ALL_NODES * C + EDGES * C + ALL_NODES * 4 * F) + 4 * (EDGES * F + 2 * ALL_NODES * 2 * F + 3 * C * F)
@@ -44,18 +47,22 @@ def tile_gnnlayer_pa_v_kernel(tc, x, e_enc, W_pre, b_pre, m, stat, arg, grad_out
     stat_rows = stat.rearrange("b n s -> (b n) s")
     arg_rows = arg.rearrange("b n s -> (b n) s")
     g_rows = grad_out.rearrange("b n g -> (b n) g")
-    steps = [(g, b) for g in range(QUARTERS) for b in range(GRAPHS)]
+    steps = [(quarter, graph) for quarter in range(QUARTERS) for graph in range(GRAPHS)]
 
     with ExitStack() as ctx:
+        ctx.enter_context(tc.manual_schedule())
         const = ctx.enter_context(tc.tile_pool(name="const", bufs=1))
         keep = ctx.enter_context(tc.tile_pool(name="keep", bufs=1))
         setup = ctx.enter_context(tc.tile_pool(name="setup", bufs=1))
         e_pool = ctx.enter_context(tc.tile_pool(name="e_pool", bufs=2))
-        rep_pool = ctx.enter_context(tc.tile_pool(name="rep_pool", bufs=2))
+        rep_pool = ctx.enter_context(tc.tile_pool(name="rep_pool", bufs=3))
         m_pool = ctx.enter_context(tc.tile_pool(name="m_pool", bufs=4))
         work = ctx.enter_context(tc.tile_pool(name="work", bufs=2))
         o_pool = ctx.enter_context(tc.tile_pool(name="o_pool", bufs=6))
         psum = ctx.enter_context(tc.psum_pool(name="psum", bufs=1))
+
+        def short_lived(shape, dtype, name):
+            return psum.tile(shape, dtype, tag="acc", bufs=SHORT_LIVED_BANKS, name=name)
 
         def load_table(rows, col0, dtype, name):
             table = setup.tile([P, HALF], dtype, name=name)
@@ -70,13 +77,15 @@ def tile_gnnlayer_pa_v_kernel(tc, x, e_enc, W_pre, b_pre, m, stat, arg, grad_out
             )
             return e_raw
 
-        def load_messages(g, b):
+        def load_messages(quarter, graph):
             dm = m_pool.tile([P, PAIR, PACK, QUARTER], F32, name="dm")
             for sp in range(PAIR):
-                row0 = (b * PAIR + sp) * K_PASS
+                row0 = (graph * PAIR + sp) * K_PASS
                 nc.sync.dma_start(
                     out=dm[:, sp],
-                    in_=m_rows[row0 : row0 + K_PASS, g * QUARTER : (g + 1) * QUARTER].rearrange("(p t) f -> p t f", t=PACK),
+                    in_=m_rows[row0 : row0 + K_PASS, quarter * QUARTER : (quarter + 1) * QUARTER].rearrange(
+                        "(p t) f -> p t f", t=PACK
+                    ),
                 )
             return dm
 
@@ -84,13 +93,13 @@ def tile_gnnlayer_pa_v_kernel(tc, x, e_enc, W_pre, b_pre, m, stat, arg, grad_out
         rstd = load_table(stat_rows, F, F32, "rstd")
         mean = load_table(stat_rows, 0, F32, "mean")
         g_mean = load_table(g_rows, 0, BF16, "g_mean")
-        e_raw = {0: load_edges(0)}
         jmin = load_table(arg_rows, 0, F32, "jmin")
         jmax = load_table(arg_rows, F, F32, "jmax")
         g_min = load_table(g_rows, F, BF16, "g_min")
         g_max = load_table(g_rows, 2 * F, BF16, "g_max")
-        e_raw[1] = load_edges(1)
+        e_raw = {0: load_edges(0)}
         dm_of = {0: load_messages(*steps[0])}
+        e_raw[1] = load_edges(1)
         dm_of[1] = load_messages(*steps[1])
         x_b = setup.tile([P, 2, C], BF16)
         nc.sync.dma_start(out=x_b[0:ALL_NODES, 0, :], in_=x_rows)
@@ -128,8 +137,10 @@ def tile_gnnlayer_pa_v_kernel(tc, x, e_enc, W_pre, b_pre, m, stat, arg, grad_out
             )
         x_f = keep.tile([P, 2, C], F32)
         nc.gpsimd.memset(x_f[ALL_NODES:P, 0, :], 0.0)
-        nc.gpsimd.tensor_copy(out=x_f[0:ALL_NODES, 0, :], in_=x_b[0:ALL_NODES, 0, :])
-        nc.gpsimd.tensor_copy(out=x_f[:, 1, :], in_=x_b[:, 1, :])
+        nc.gpsimd.tensor_scalar(
+            out=x_f[0:ALL_NODES, 0, :], in0=x_b[0:ALL_NODES, 0, :], scalar1=1.0, scalar2=0.0, op0=ALU.mult, op1=ALU.add
+        )
+        nc.gpsimd.tensor_scalar(out=x_f[:, 1, :], in0=x_b[:, 1, :], scalar1=1.0, scalar2=0.0, op0=ALU.mult, op1=ALU.add)
 
         c_tab = setup.tile([P, HALF], F32)
         nc.vector.scalar_tensor_tensor(
@@ -144,22 +155,21 @@ def tile_gnnlayer_pa_v_kernel(tc, x, e_enc, W_pre, b_pre, m, stat, arg, grad_out
         def turn_tables(pair, ident, out_dtype, name):
             turned_sb = keep.tile([P, BLKS, 2, P], out_dtype, name=name)
             for a, table in enumerate(pair):
-                turned = psum.tile([P, BLKS, P], table.dtype, tag="acc", bufs=4, name="turned")
+                turned = short_lived([P, BLKS, P], table.dtype, "turned")
                 for fb in range(BLKS):
                     nc.tensor.transpose(out=turned[:, fb, :], in_=table[:, fb * BLK : (fb + 1) * BLK], identity=ident[:])
                 nc.scalar.copy(out=turned_sb[:, :, a, :], in_=turned[:])
             return turned_sb
 
-        def repeat_rows(turned_sb, g, b, name):
+        def repeat_rows(turned_sb, quarter, graph, name):
             repeated = rep_pool.tile([P, Q_BLKS, 2, NODES, SPREAD], turned_sb.dtype, name=name)
-            h, fb0 = g // HALVES, (g % HALVES) * Q_BLKS
+            h, fb0 = quarter // QUARTERS_IN_HALF, (quarter % QUARTERS_IN_HALF) * Q_BLKS
             rows = turned_sb[:].rearrange("p f a (n h) -> p f a n h", h=HALVES)
-            rows = rows[:, fb0 : fb0 + Q_BLKS, :, b * NODES : (b + 1) * NODES, h]
+            rows = rows[:, fb0 : fb0 + Q_BLKS, :, graph * NODES : (graph + 1) * NODES, h]
             nc.scalar.copy(out=repeated[:], in_=rows.unsqueeze(4).to_broadcast([P, Q_BLKS, 2, NODES, SPREAD]))
             return repeated
 
-        def turn_back(repeated, ident, name, tag, bufs):
-            spread = psum.tile([P, 2, PAIR, QUARTER], repeated.dtype, name=name, tag=tag, bufs=bufs)
+        def turn_back(repeated, ident, spread):
             for a in range(2):
                 for sp in range(PAIR):
                     for fb in range(Q_BLKS):
@@ -170,10 +180,28 @@ def tile_gnnlayer_pa_v_kernel(tc, x, e_enc, W_pre, b_pre, m, stat, arg, grad_out
                         )
             return spread
 
-        def to_sbuf(spread):
-            jj_sb = work.tile([P, 2, PAIR, QUARTER], BF16, name="jj_sb")
-            nc.scalar.copy(out=jj_sb[:], in_=spread[:])
-            return jj_sb
+        tables = {}
+        rep_of = {}
+        spread_of = {}
+
+        def repeat_all(k):
+            rep_of[k] = {name: repeat_rows(tables[name], *steps[k], name + "_rep") for name in ("ca", "jj", "gg")}
+
+        def spread_all(k):
+            shape = [P, 2, PAIR, QUARTER]
+            ca = turn_back(rep_of[k]["ca"], ident_f, psum.tile(shape, F32, name="ca_ps"))
+            jj_ps = turn_back(rep_of[k]["jj"], ident_b, short_lived(shape, BF16, "jj_ps"))
+            jj = work.tile(shape, BF16, name="jj_sb")
+            nc.scalar.copy(out=jj[:], in_=jj_ps[:])
+            gg = turn_back(rep_of[k]["gg"], ident_b, psum.tile(shape, BF16, name="gg_ps"))
+            spread_of[k] = {"ca": ca, "jj": jj, "gg": gg}
+
+        e_codes = keep.tile([P, PASSES, C], U32, align_bytes=64)
+        e_scales = keep.tile([P, PASSES, C], U8, align_bytes=64)
+        d_codes = [keep.tile([P, PASSES, HALF], U32, align_bytes=64, name="d_codes" + str(h)) for h in range(HALVES)]
+        d_scales = [keep.tile([P, PASSES, HALF], U8, align_bytes=64, name="d_scales" + str(h)) for h in range(HALVES)]
+        e_grp = {}
+        d_grp = {}
 
         def regroup(engine_copy, grouped, raw):
             engine_copy(out=grouped.rearrange("p (c i) t -> p c t i", i=4), in_=raw.rearrange("p t (c i) -> p c t i", i=4))
@@ -181,162 +209,170 @@ def tile_gnnlayer_pa_v_kernel(tc, x, e_enc, W_pre, b_pre, m, stat, arg, grad_out
         def quantise(grouped, codes, scales, fmt):
             nc.vector.quantize_mx(out=codes.bitcast(fmt), scales=scales, in_=grouped.rearrange("p c t -> p (c t)"))
 
-        def regroup_edges(s):
-            e_grp = work.tile([P, C, PACK], BF16, align_bytes=64, name="e_grp")
-            regroup(nc.vector.tensor_copy if s < PAIR else nc.scalar.copy, e_grp[:], e_raw[s][:])
-            return e_grp
+        def regroup_edges(s, engine_copy):
+            e_grp[s] = work.tile([P, C, PACK], BF16, align_bytes=64, name="e_grp")
+            regroup(engine_copy, e_grp[s][:], e_raw[s][:])
 
-        def regroup_gradient(dm):
-            d_grp = work.tile([P, PAIR, QUARTER, PACK], BF16, align_bytes=64, name="d_grp")
+        def regroup_gradient(k):
+            d_grp[k] = work.tile([P, PAIR, QUARTER, PACK], BF16, align_bytes=64, name="d_grp")
             for sp in range(PAIR):
-                regroup(nc.scalar.copy, d_grp[:, sp], dm[:, sp])
-            return d_grp
+                regroup(nc.scalar.copy, d_grp[k][:, sp], dm_of[k][:, sp])
 
-        def quantise_gradient(d_grp, g, b, d_mx):
-            cols = slice((g % HALVES) * QUARTER, (g % HALVES + 1) * QUARTER)
+        def quantise_gradient(k):
+            quarter, graph = steps[k]
+            h = quarter // QUARTERS_IN_HALF
+            col0 = (quarter % QUARTERS_IN_HALF) * QUARTER
             for sp in range(PAIR):
-                s = b * PAIR + sp
-                quantise(d_grp[:, sp], d_mx["codes"][:, s, cols], d_mx["scales"][:, s, cols], E5M2X4)
+                s = graph * PAIR + sp
+                quantise(
+                    d_grp[k][:, sp], d_codes[h][:, s, col0 : col0 + QUARTER], d_scales[h][:, s, col0 : col0 + QUARTER], E5M2X4
+                )
 
-        def partial_sums(dm, b, sums_ps):
+        sums_ps_of = {}
+        sums_of = {}
+        sums_t_of = [keep.tile([P, 2, Q_BLKS, P], F32, name="sums_t" + str(i)) for i in range(2)]
+        for sums_t in sums_t_of:
+            nc.gpsimd.memset(sums_t[:, 0], 0.0)
+
+        def partial_sums(k):
+            quarter, graph = steps[k]
             for sp in range(PAIR):
                 for fb in range(Q_BLKS):
                     for t in range(PACK):
                         nc.tensor.matmul(
-                            out=sums_ps[:, b * PAIR + sp, fb, :],
-                            lhsT=dm[:, sp, t, fb * BLK : (fb + 1) * BLK],
+                            out=sums_ps_of[quarter][:, graph * PAIR + sp, fb, :],
+                            lhsT=dm_of[k][:, sp, t, fb * BLK : (fb + 1) * BLK],
                             rhs=pick[:, t, :],
                             start=(t == 0),
                             stop=(t == PACK - 1),
                         )
 
-        def turn_sums(sums_ps):
-            sums_t = work.tile([P, 2, Q_BLKS, P], F32, name="sums_t")
-            nc.gpsimd.memset(sums_t[:, 0, :, ALL_NODES:P], 0.0)
+        def turn_sums(quarter):
+            sums_ps, sums_t = sums_ps_of[quarter], sums_t_of[quarter % 2]
             nc.scalar.copy(
                 out=sums_t[:, 0, :, 0:ALL_NODES].rearrange("p f (s q) -> p s f q", q=TARGETS), in_=sums_ps[:, :, :, 0:TARGETS]
             )
             nc.scalar.copy(out=sums_t[:, 1].rearrange("p f (s j) -> p s f j", j=NODES), in_=sums_ps[:, :, :, TARGETS:SUMS])
-            turned = psum.tile([P, 2, QUARTER], F32, tag="acc", bufs=4, name="ps_turn")
+            turned = short_lived([P, 2, QUARTER], F32, "ps_turn")
             for plane in range(2):
                 for fb in range(Q_BLKS):
                     nc.tensor.transpose(
                         out=turned[:, plane, fb * BLK : (fb + 1) * BLK], in_=sums_t[:, plane, fb, :], identity=ident_f[:]
                     )
-            sums = work.tile([P, 2, QUARTER], F32, name="sums")
-            nc.scalar.copy(out=sums[:], in_=turned[:])
-            return sums
+            sums_of[quarter] = work.tile([P, 2, QUARTER], F32, name="sums")
+            nc.scalar.copy(out=sums_of[quarter][:], in_=turned[:])
 
-        def leave_psum(acc, on_vector):
-            result = o_pool.tile([P, HALF], F32, name="result")
-            if on_vector:
-                nc.vector.tensor_copy(out=result[:], in_=acc)
-            else:
-                nc.scalar.copy(out=result[:], in_=acc)
-            return result
-
-        def node_products(g, cb, sums, on_vector):
-            acc = psum.tile([P, 2, QUARTER], F32, tag="acc", bufs=4, name="acc")
+        def node_products(quarter, cb):
+            acc = short_lived([P, 2, QUARTER], F32, "acc")
             for plane in range(2):
                 nc.tensor.matmul(
-                    out=acc[:, plane, :], lhsT=x_f[:, plane, cb * BLK : (cb + 1) * BLK], rhs=sums[:, plane, :], start=True, stop=True
+                    out=acc[:, plane, :],
+                    lhsT=x_f[:, plane, cb * BLK : (cb + 1) * BLK],
+                    rhs=sums_of[quarter][:, plane, :],
+                    start=True,
+                    stop=True,
                 )
-            result = leave_psum(acc[:].rearrange("p a f -> p (a f)"), on_vector)
-            both = out[0 : 2 * C, g * QUARTER : (g + 1) * QUARTER].rearrange("(a r) f -> r a f", a=2)
-            nc.sync.dma_start(out=both[cb * BLK : (cb + 1) * BLK], in_=result[:].rearrange("p (a f) -> p a f", a=2))
+            result = o_pool.tile([P, 2, QUARTER], F32, name="result")
+            nc.scalar.copy(out=result[:], in_=acc[:])
+            both = out[0 : 2 * C, quarter * QUARTER : (quarter + 1) * QUARTER].rearrange("(a r) f -> r a f", a=2)
+            nc.sync.dma_start(out=both[cb * BLK : (cb + 1) * BLK], in_=result[:])
 
-        def edge_product(h, cb, d_mx, on_vector):
-            cols = slice(cb * BLK, (cb + 1) * BLK)
-            acc = psum.tile([P, HALF], F32, tag="acc", bufs=4, name="acc")
+        def edge_product(h, cb):
+            acc = short_lived([P, HALF], F32, "acc")
             for s in range(PASSES):
                 nc.tensor.matmul_mx(
                     out=acc[:],
-                    lhsT=e_codes[:, s, cols].bitcast(E4M3X4),
-                    lhsT_scale=e_scales[:, s, cols],
-                    rhs=d_mx["codes"][:, s, :].bitcast(E5M2X4),
-                    rhs_scale=d_mx["scales"][:, s, :],
+                    lhsT=e_codes[:, s, cb * BLK : (cb + 1) * BLK].bitcast(E4M3X4),
+                    lhsT_scale=e_scales[:, s, cb * BLK : (cb + 1) * BLK],
+                    rhs=d_codes[h][:, s, :].bitcast(E5M2X4),
+                    rhs_scale=d_scales[h][:, s, :],
                     start=(s == 0),
                     stop=(s == PASSES - 1),
                 )
-            result = leave_psum(acc[:], on_vector)
+            return acc
+
+        def store_edge_product(acc, h, cb):
+            result = o_pool.tile([P, HALF], F32, name="result")
+            nc.vector.tensor_copy(out=result[:], in_=acc[:])
             row0 = 2 * C + cb * BLK
             nc.sync.dma_start(out=out[row0 : row0 + BLK, h * HALF : (h + 1) * HALF], in_=result[:])
 
-        e_codes = keep.tile([P, PASSES, C], U32, align_bytes=64)
-        e_scales = keep.tile([P, PASSES, C], U8, align_bytes=64)
-        d_mx_of = {}
-        for h in range(HALVES):
-            d_mx_of[h] = {
-                "codes": keep.tile([P, PASSES, HALF], U32, align_bytes=64, name="d_codes" + str(h)),
-                "scales": keep.tile([P, PASSES, HALF], U8, align_bytes=64, name="d_scales" + str(h)),
-            }
-        ca_t = turn_tables((c_tab, a_tab), ident_f, F32, "ca_t")
-        ca_rep = repeat_rows(ca_t, 0, 0, "ca_rep")
-        nxt = {"ca": turn_back(ca_rep, ident_f, "ca_ps", "ca_ps", 1)}
-        jj_t = turn_tables((jmin, jmax), ident_f, BF16, "jj_t")
-        jj_rep = repeat_rows(jj_t, 0, 0, "jj_rep")
-        nxt["jj"] = to_sbuf(turn_back(jj_rep, ident_b, "jj_ps", "acc", 4))
-        gg_t = turn_tables((g_min, g_max), ident_b, BF16, "gg_t")
-        gg_rep = repeat_rows(gg_t, 0, 0, "gg_rep")
-        nxt["gg"] = turn_back(gg_rep, ident_b, "gg_ps", "gg_ps", 1)
-        e_grp = {0: regroup_edges(0)}
+        def outputs_and_last_step(k):
+            if k >= 3:
+                quarter, part = (k - 3) // GRAPHS, (k - 3) % GRAPHS
+                for cb in range(part * C_BLKS // GRAPHS, (part + 1) * C_BLKS // GRAPHS):
+                    node_products(quarter, cb)
+            if k >= 1:
+                regroup_gradient(k - 1)
+            edge_acc = {}
+            if k >= 5:
+                for cb in range((k - 5) * C_BLKS // 4, (k - 4) * C_BLKS // 4):
+                    edge_acc[cb] = edge_product(0, cb)
+            if k >= 1:
+                partial_sums(k - 1)
+            return edge_acc
 
-        over_slots = [P, PAIR, PACK, QUARTER]
-        d_grp = {}
-        sums_of = {}
-        for k, (g, b) in enumerate(steps):
-            now = nxt
-            if k + 2 < len(steps):
+        def step(k, edge_acc):
+            quarter, graph = steps[k]
+            ca, jj, gg = spread_of[k]["ca"], spread_of[k]["jj"], spread_of[k]["gg"]
+            dm = dm_of[k]
+            if k + 2 < STEPS:
                 dm_of[k + 2] = load_messages(*steps[k + 2])
             if k + 2 < PASSES:
                 e_raw[k + 2] = load_edges(k + 2)
-            dm = dm_of[k]
-            if b == 0:
-                sums_ps = psum.tile([P, PASSES, Q_BLKS, SUMS], F32, name="sums_ps")
+            if graph == 0:
+                sums_ps_of[quarter] = psum.tile([P, PASSES, Q_BLKS, SUMS], F32, name="sums_ps")
 
+            over_slots = [P, PAIR, PACK, QUARTER]
+            nc.vector.tensor_tensor(out=dm[:], in0=dm[:], in1=ca[:, 0].unsqueeze(2).to_broadcast(over_slots), op=ALU.mult)
+            nc.vector.tensor_tensor(out=dm[:], in0=dm[:], in1=ca[:, 1].unsqueeze(2).to_broadcast(over_slots), op=ALU.add)
             hit = work.tile([P, 2, PAIR, PACK, QUARTER], BF16, name="hit")
-            nc.vector.tensor_tensor(out=dm[:], in0=dm[:], in1=now["ca"][:, 0].unsqueeze(2).to_broadcast(over_slots), op=ALU.mult)
             for t in range(PACK):
                 nc.vector.tensor_scalar(
-                    out=hit[:, :, :, t, :], in0=now["jj"][:], scalar1=src_f[:, t : t + 1], scalar2=None, op0=ALU.is_equal
+                    out=hit[:, :, :, t, :], in0=jj[:], scalar1=src_f[:, t : t + 1], scalar2=None, op0=ALU.is_equal
                 )
-            nc.vector.tensor_tensor(out=dm[:], in0=dm[:], in1=now["ca"][:, 1].unsqueeze(2).to_broadcast(over_slots), op=ALU.add)
             nc.vector.tensor_tensor(
-                out=hit[:], in0=hit[:], in1=now["gg"][:].unsqueeze(3).to_broadcast([P, 2] + over_slots[1:]), op=ALU.mult
+                out=hit[:], in0=hit[:], in1=gg[:].unsqueeze(3).to_broadcast([P, 2] + over_slots[1:]), op=ALU.mult
             )
-            if k > 0:
-                was_g, was_b = steps[k - 1]
-                quantise_gradient(d_grp[k - 1], was_g, was_b, d_mx_of[was_g // HALVES])
+            for cb in edge_acc:
+                store_edge_product(edge_acc[cb], 0, cb)
+            if k >= 1:
+                quantise_gradient(k - 1)
             if k < PASSES:
                 quantise(e_grp[k][:], e_codes[:, k, :], e_scales[:, k, :], E4M3X4)
             nc.vector.tensor_tensor(out=dm[:], in0=dm[:], in1=hit[:, 0], op=ALU.add)
-            second_adder = nc.gpsimd if k + 1 < len(steps) else nc.vector
+            second_adder = nc.gpsimd if k + 1 < STEPS else nc.vector
             second_adder.tensor_tensor(out=dm[:], in0=dm[:], in1=hit[:, 1], op=ALU.add)
-            if k + 1 < PASSES:
-                e_grp[k + 1] = regroup_edges(k + 1)
 
-            if k + 1 < len(steps):
-                ca_rep = repeat_rows(ca_t, *steps[k + 1], "ca_rep")
-                jj_rep = repeat_rows(jj_t, *steps[k + 1], "jj_rep")
-                gg_rep = repeat_rows(gg_t, *steps[k + 1], "gg_rep")
-                nxt = {"ca": turn_back(ca_rep, ident_f, "ca_ps", "ca_ps", 1)}
-                nxt["jj"] = to_sbuf(turn_back(jj_rep, ident_b, "jj_ps", "acc", 4))
-            if g > 0:
-                for cb in range(b * C_BLKS // GRAPHS, (b + 1) * C_BLKS // GRAPHS):
-                    node_products(g - 1, cb, sums_of[g - 1], False)
-            if g >= HALVES:
-                first = (k - len(steps) // HALVES) * HALVES
-                for cb in range(first, first + HALVES):
-                    edge_product(0, cb, d_mx_of[0], True)
-            if k + 1 < len(steps):
-                nxt["gg"] = turn_back(gg_rep, ident_b, "gg_ps", "gg_ps", 1)
+            if k >= 1 and graph == 0:
+                turn_sums(quarter - 1)
+            if k + 2 < STEPS:
+                repeat_all(k + 2)
+            if k + 1 < STEPS:
+                spread_all(k + 1)
+            if k == 0:
+                regroup_edges(1, nc.vector.tensor_copy)
+            if k + 2 < PASSES:
+                regroup_edges(k + 2, nc.scalar.copy)
 
-            d_grp[k] = regroup_gradient(dm)
-            partial_sums(dm, b, sums_ps)
-            if b == GRAPHS - 1:
-                sums_of[g] = turn_sums(sums_ps)
+        tables["ca"] = turn_tables((c_tab, a_tab), ident_f, F32, "ca_t")
+        rep_of[0] = {"ca": repeat_rows(tables["ca"], *steps[0], "ca_rep")}
+        tables["jj"] = turn_tables((jmin, jmax), ident_f, BF16, "jj_t")
+        rep_of[0]["jj"] = repeat_rows(tables["jj"], *steps[0], "jj_rep")
+        tables["gg"] = turn_tables((g_min, g_max), ident_b, BF16, "gg_t")
+        rep_of[0]["gg"] = repeat_rows(tables["gg"], *steps[0], "gg_rep")
+        spread_all(0)
+        repeat_all(1)
+        regroup_edges(0, nc.vector.tensor_copy)
 
-        quantise_gradient(d_grp[len(steps) - 1], *steps[-1], d_mx_of[HALVES - 1])
+        for k in range(STEPS):
+            step(k, outputs_and_last_step(k))
+
+        edge_acc = outputs_and_last_step(STEPS)
+        for cb in edge_acc:
+            store_edge_product(edge_acc[cb], 0, cb)
+        quantise_gradient(STEPS - 1)
+        turn_sums(QUARTERS - 1)
         for cb in range(C_BLKS):
-            edge_product(HALVES - 1, cb, d_mx_of[HALVES - 1], True)
-            node_products(QUARTERS - 1, cb, sums_of[QUARTERS - 1], False)
+            store_edge_product(edge_product(HALVES - 1, cb), HALVES - 1, cb)
+            node_products(QUARTERS - 1, cb)

@@ -24,16 +24,16 @@ TARGETS = K_PASS // NODES
 SPREAD = P // TARGETS
 HALF = 512
 HALVES = F // HALF
-QUARTER = 256
-QUARTERS = F // QUARTER
-QUARTERS_IN_HALF = HALF // QUARTER
+WIDTHS = (256, 256, 256, 128, 128)
+WIDE = max(WIDTHS)
+GROUPS = [(sum(WIDTHS[:i]), w) for i, w in enumerate(WIDTHS)]
 BLK = 128
 BLKS = HALF // BLK
-Q_BLKS = QUARTER // BLK
 C_BLKS = C // BLK
 SUMS = TARGETS + NODES
-STEPS = QUARTERS * GRAPHS
-SHORT_LIVED_BANKS = 4
+STEPS = len(GROUPS) * GRAPHS
+EUNITS = {-1: (0, 1), 0: (2,), 1: (3,), 2: (4,), 3: (5,), 4: (6,), 5: (7,)}
+SHORT_LIVED_BANKS = 5
 
 FLOPS = 2 * EDGES * C * F + 2 * 2 * ALL_NODES * C * F
 BYTES = 2 * (ALL_NODES * C + EDGES * C + ALL_NODES * 4 * F) + 4 * (EDGES * F + 2 * ALL_NODES * 2 * F + 3 * C * F)
@@ -47,7 +47,7 @@ def tile_gnnlayer_pa_v_kernel(tc, x, e_enc, W_pre, b_pre, m, stat, arg, grad_out
     stat_rows = stat.rearrange("b n s -> (b n) s")
     arg_rows = arg.rearrange("b n s -> (b n) s")
     g_rows = grad_out.rearrange("b n g -> (b n) g")
-    steps = [(quarter, graph) for quarter in range(QUARTERS) for graph in range(GRAPHS)]
+    steps = [(group, graph) for group in range(len(GROUPS)) for graph in range(GRAPHS)]
 
     with ExitStack() as ctx:
         ctx.enter_context(tc.manual_schedule())
@@ -55,10 +55,11 @@ def tile_gnnlayer_pa_v_kernel(tc, x, e_enc, W_pre, b_pre, m, stat, arg, grad_out
         keep = ctx.enter_context(tc.tile_pool(name="keep", bufs=1))
         setup = ctx.enter_context(tc.tile_pool(name="setup", bufs=1))
         e_pool = ctx.enter_context(tc.tile_pool(name="e_pool", bufs=2))
-        rep_pool = ctx.enter_context(tc.tile_pool(name="rep_pool", bufs=3))
+        e_grp_pool = ctx.enter_context(tc.tile_pool(name="e_grp_pool", bufs=3))
+        rep_pool = ctx.enter_context(tc.tile_pool(name="rep_pool", bufs=2))
         m_pool = ctx.enter_context(tc.tile_pool(name="m_pool", bufs=4))
         work = ctx.enter_context(tc.tile_pool(name="work", bufs=2))
-        o_pool = ctx.enter_context(tc.tile_pool(name="o_pool", bufs=6))
+        o_pool = ctx.enter_context(tc.tile_pool(name="o_pool", bufs=5))
         psum = ctx.enter_context(tc.psum_pool(name="psum", bufs=1))
 
         def short_lived(shape, dtype, name):
@@ -77,15 +78,14 @@ def tile_gnnlayer_pa_v_kernel(tc, x, e_enc, W_pre, b_pre, m, stat, arg, grad_out
             )
             return e_raw
 
-        def load_messages(quarter, graph):
-            dm = m_pool.tile([P, PAIR, PACK, QUARTER], F32, name="dm")
+        def load_messages(group, graph):
+            col0, width = GROUPS[group]
+            dm = m_pool.tile([P, PAIR, PACK, width], F32, name="dm")
             for sp in range(PAIR):
                 row0 = (graph * PAIR + sp) * K_PASS
                 nc.sync.dma_start(
                     out=dm[:, sp],
-                    in_=m_rows[row0 : row0 + K_PASS, quarter * QUARTER : (quarter + 1) * QUARTER].rearrange(
-                        "(p t) f -> p t f", t=PACK
-                    ),
+                    in_=m_rows[row0 : row0 + K_PASS, col0 : col0 + width].rearrange("(p t) f -> p t f", t=PACK),
                 )
             return dm
 
@@ -93,12 +93,29 @@ def tile_gnnlayer_pa_v_kernel(tc, x, e_enc, W_pre, b_pre, m, stat, arg, grad_out
         rstd = load_table(stat_rows, F, F32, "rstd")
         mean = load_table(stat_rows, 0, F32, "mean")
         g_mean = load_table(g_rows, 0, BF16, "g_mean")
-        jmin = load_table(arg_rows, 0, F32, "jmin")
-        jmax = load_table(arg_rows, F, F32, "jmax")
-        g_min = load_table(g_rows, F, BF16, "g_min")
-        g_max = load_table(g_rows, 2 * F, BF16, "g_max")
+        g_hits = keep.tile([P, PASSES, 2, F], BF16)
+
+        def load_g_hits():
+            for r in range(SPREAD):
+                nc.sync.dma_start(
+                    out=g_hits[r:P:SPREAD].rearrange("q s a f -> q s (a f)"),
+                    in_=g_rows[:, F : 3 * F].rearrange("(s q) f -> q s f", q=TARGETS),
+                )
+
+        def load_j_rows(h):
+            rows_h = keep.tile([P, 2, PASSES, HALF], F32, name="j_rows" + str(h))
+            for a in range(2):
+                for r in range(SPREAD):
+                    nc.sync.dma_start(
+                        out=rows_h[r:P:SPREAD, a],
+                        in_=arg_rows[:, a * F + h * HALF : a * F + (h + 1) * HALF].rearrange("(s q) f -> q s f", q=TARGETS),
+                    )
+            return rows_h
+
         e_raw = {0: load_edges(0)}
         dm_of = {0: load_messages(*steps[0])}
+        j_rows = {0: load_j_rows(0)}
+        load_g_hits()
         e_raw[1] = load_edges(1)
         dm_of[1] = load_messages(*steps[1])
         x_b = setup.tile([P, 2, C], BF16)
@@ -135,13 +152,6 @@ def tile_gnnlayer_pa_v_kernel(tc, x, e_enc, W_pre, b_pre, m, stat, arg, grad_out
             nc.vector.tensor_scalar(
                 out=pick[:, t, TARGETS:SUMS], in0=col_f[:], scalar1=src_f[:, t : t + 1], scalar2=None, op0=ALU.is_equal
             )
-        x_f = keep.tile([P, 2, C], F32)
-        nc.gpsimd.memset(x_f[ALL_NODES:P, 0, :], 0.0)
-        nc.gpsimd.tensor_scalar(
-            out=x_f[0:ALL_NODES, 0, :], in0=x_b[0:ALL_NODES, 0, :], scalar1=1.0, scalar2=0.0, op0=ALU.mult, op1=ALU.add
-        )
-        nc.gpsimd.tensor_scalar(out=x_f[:, 1, :], in0=x_b[:, 1, :], scalar1=1.0, scalar2=0.0, op0=ALU.mult, op1=ALU.add)
-
         c_tab = setup.tile([P, HALF], F32)
         nc.vector.scalar_tensor_tensor(
             out=c_tab[:], in0=g_std[:], scalar=1.0 / NODES, in1=rstd[:], op0=ALU.mult, op1=ALU.mult
@@ -161,40 +171,49 @@ def tile_gnnlayer_pa_v_kernel(tc, x, e_enc, W_pre, b_pre, m, stat, arg, grad_out
                 nc.scalar.copy(out=turned_sb[:, :, a, :], in_=turned[:])
             return turned_sb
 
-        def repeat_rows(turned_sb, quarter, graph, name):
-            repeated = rep_pool.tile([P, Q_BLKS, 2, NODES, SPREAD], turned_sb.dtype, name=name)
-            h, fb0 = quarter // QUARTERS_IN_HALF, (quarter % QUARTERS_IN_HALF) * Q_BLKS
-            rows = turned_sb[:].rearrange("p f a (n h) -> p f a n h", h=HALVES)
-            rows = rows[:, fb0 : fb0 + Q_BLKS, :, graph * NODES : (graph + 1) * NODES, h]
-            nc.scalar.copy(out=repeated[:], in_=rows.unsqueeze(4).to_broadcast([P, Q_BLKS, 2, NODES, SPREAD]))
-            return repeated
-
-        def turn_back(repeated, ident, spread):
-            for a in range(2):
-                for sp in range(PAIR):
-                    for fb in range(Q_BLKS):
-                        nc.tensor.transpose(
-                            out=spread[:, a, sp, fb * BLK : (fb + 1) * BLK],
-                            in_=repeated[:, fb, a, sp * TARGETS : (sp + 1) * TARGETS, :].rearrange("p q r -> p (q r)"),
-                            identity=ident[:],
-                        )
-            return spread
-
         tables = {}
         rep_of = {}
         spread_of = {}
+        jj_of = {}
 
-        def repeat_all(k):
-            rep_of[k] = {name: repeat_rows(tables[name], *steps[k], name + "_rep") for name in ("ca", "jj", "gg")}
+        def repeat_rows(k):
+            group, graph = steps[k]
+            fb0, blks = GROUPS[group][0] // BLK, GROUPS[group][1] // BLK
+            h = fb0 // BLKS
+            rep_of[k] = rep_pool.tile([P, blks, 2, NODES, SPREAD], F32, name="ca_rep")
+            rows = tables["ca"][:].rearrange("p f a (n h) -> p f a n h", h=HALVES)
+            rows = rows[:, fb0 % BLKS : fb0 % BLKS + blks, :, graph * NODES : (graph + 1) * NODES, h]
+            nc.scalar.copy(out=rep_of[k][:], in_=rows.unsqueeze(4).to_broadcast([P, blks, 2, NODES, SPREAD]))
 
-        def spread_all(k):
-            shape = [P, 2, PAIR, QUARTER]
-            ca = turn_back(rep_of[k]["ca"], ident_f, psum.tile(shape, F32, name="ca_ps"))
-            jj_ps = turn_back(rep_of[k]["jj"], ident_b, short_lived(shape, BF16, "jj_ps"))
-            jj = work.tile(shape, BF16, name="jj_sb")
-            nc.scalar.copy(out=jj[:], in_=jj_ps[:])
-            gg = turn_back(rep_of[k]["gg"], ident_b, psum.tile(shape, BF16, name="gg_ps"))
-            spread_of[k] = {"ca": ca, "jj": jj, "gg": gg}
+        def spread_rows(k):
+            width = GROUPS[steps[k][0]][1]
+            spread_of[k] = []
+            for a in range(2):
+                spread = psum.tile([P, PAIR, width], F32, tag="ca"[a] + "_ps", bufs=1, name="ca"[a] + "_ps")
+                for sp in range(PAIR):
+                    for fb in range(width // BLK):
+                        nc.tensor.transpose(
+                            out=spread[:, sp, fb * BLK : (fb + 1) * BLK],
+                            in_=rep_of[k][:, fb, a, sp * TARGETS : (sp + 1) * TARGETS, :].rearrange("p q r -> p (q r)"),
+                            identity=ident_f[:],
+                        )
+                spread_of[k].append(spread)
+
+        def round_j(k):
+            group, graph = steps[k]
+            col0, width = GROUPS[group]
+            h, col = col0 // HALF, col0 % HALF
+            jj_of[k] = work.tile([P, 2, PAIR, width], BF16, name="jj")
+            nc.scalar.copy(out=jj_of[k][:], in_=j_rows[h][:, :, graph * PAIR : (graph + 1) * PAIR, col : col + width])
+
+        x_f = keep.tile([P, 2, C], F32)
+
+        def cast_x():
+            nc.gpsimd.memset(x_f[ALL_NODES:P, 0, :], 0.0)
+            nc.gpsimd.tensor_scalar(
+                out=x_f[0:ALL_NODES, 0, :], in0=x_b[0:ALL_NODES, 0, :], scalar1=1.0, scalar2=0.0, op0=ALU.mult, op1=ALU.add
+            )
+            nc.gpsimd.tensor_scalar(out=x_f[:, 1, :], in0=x_b[:, 1, :], scalar1=1.0, scalar2=0.0, op0=ALU.mult, op1=ALU.add)
 
         e_codes = keep.tile([P, PASSES, C], U32, align_bytes=64)
         e_scales = keep.tile([P, PASSES, C], U8, align_bytes=64)
@@ -209,79 +228,92 @@ def tile_gnnlayer_pa_v_kernel(tc, x, e_enc, W_pre, b_pre, m, stat, arg, grad_out
         def quantise(grouped, codes, scales, fmt):
             nc.vector.quantize_mx(out=codes.bitcast(fmt), scales=scales, in_=grouped.rearrange("p c t -> p (c t)"))
 
-        def regroup_edges(s, engine_copy):
-            e_grp[s] = work.tile([P, C, PACK], BF16, align_bytes=64, name="e_grp")
-            regroup(engine_copy, e_grp[s][:], e_raw[s][:])
+        def regroup_edges(unit, engine_copy):
+            s, c0 = unit // 2, unit % 2 * (C // 2)
+            e_grp[unit] = e_grp_pool.tile([P, C // 2, PACK], BF16, align_bytes=64, name="e_grp")
+            regroup(engine_copy, e_grp[unit][:], e_raw[s][:, :, c0 : c0 + C // 2])
+
+        def quantise_edges(unit):
+            s, c0 = unit // 2, unit % 2 * (C // 2)
+            quantise(e_grp[unit][:], e_codes[:, s, c0 : c0 + C // 2], e_scales[:, s, c0 : c0 + C // 2], E4M3X4)
 
         def regroup_gradient(k):
-            d_grp[k] = work.tile([P, PAIR, QUARTER, PACK], BF16, align_bytes=64, name="d_grp")
+            width = GROUPS[steps[k][0]][1]
+            d_grp[k] = work.tile([P, PAIR, width, PACK], BF16, align_bytes=64, name="d_grp")
             for sp in range(PAIR):
                 regroup(nc.scalar.copy, d_grp[k][:, sp], dm_of[k][:, sp])
 
         def quantise_gradient(k):
-            quarter, graph = steps[k]
-            h = quarter // QUARTERS_IN_HALF
-            col0 = (quarter % QUARTERS_IN_HALF) * QUARTER
+            group, graph = steps[k]
+            col0, width = GROUPS[group]
+            h, col = col0 // HALF, col0 % HALF
             for sp in range(PAIR):
                 s = graph * PAIR + sp
-                quantise(
-                    d_grp[k][:, sp], d_codes[h][:, s, col0 : col0 + QUARTER], d_scales[h][:, s, col0 : col0 + QUARTER], E5M2X4
-                )
+                quantise(d_grp[k][:, sp], d_codes[h][:, s, col : col + width], d_scales[h][:, s, col : col + width], E5M2X4)
 
         sums_ps_of = {}
         sums_of = {}
-        sums_t_of = [keep.tile([P, 2, Q_BLKS, P], F32, name="sums_t" + str(i)) for i in range(2)]
+        sums_t_of = [keep.tile([P, 2, WIDE // BLK, P], F32, name="sums_t" + str(i)) for i in range(2)]
         for sums_t in sums_t_of:
             nc.gpsimd.memset(sums_t[:, 0], 0.0)
 
         def partial_sums(k):
-            quarter, graph = steps[k]
+            group, graph = steps[k]
+            blks = GROUPS[group][1] // BLK
+            if graph == 0:
+                sums_ps_of[group] = psum.tile([P, PASSES, blks, SUMS], F32, name="sums_ps")
             for sp in range(PAIR):
-                for fb in range(Q_BLKS):
+                for fb in range(blks):
                     for t in range(PACK):
                         nc.tensor.matmul(
-                            out=sums_ps_of[quarter][:, graph * PAIR + sp, fb, :],
+                            out=sums_ps_of[group][:, graph * PAIR + sp, fb, :],
                             lhsT=dm_of[k][:, sp, t, fb * BLK : (fb + 1) * BLK],
                             rhs=pick[:, t, :],
                             start=(t == 0),
                             stop=(t == PACK - 1),
                         )
 
-        def turn_sums(quarter):
-            sums_ps, sums_t = sums_ps_of[quarter], sums_t_of[quarter % 2]
-            nc.scalar.copy(
+        def take_sums(group, engine_copy):
+            sums_ps, blks = sums_ps_of[group], GROUPS[group][1] // BLK
+            sums_t = sums_t_of[group % 2][:, :, 0:blks, :]
+            engine_copy(
                 out=sums_t[:, 0, :, 0:ALL_NODES].rearrange("p f (s q) -> p s f q", q=TARGETS), in_=sums_ps[:, :, :, 0:TARGETS]
             )
-            nc.scalar.copy(out=sums_t[:, 1].rearrange("p f (s j) -> p s f j", j=NODES), in_=sums_ps[:, :, :, TARGETS:SUMS])
-            turned = short_lived([P, 2, QUARTER], F32, "ps_turn")
-            for plane in range(2):
-                for fb in range(Q_BLKS):
-                    nc.tensor.transpose(
-                        out=turned[:, plane, fb * BLK : (fb + 1) * BLK], in_=sums_t[:, plane, fb, :], identity=ident_f[:]
-                    )
-            sums_of[quarter] = work.tile([P, 2, QUARTER], F32, name="sums")
-            nc.scalar.copy(out=sums_of[quarter][:], in_=turned[:])
+            engine_copy(out=sums_t[:, 1].rearrange("p f (s j) -> p s f j", j=NODES), in_=sums_ps[:, :, :, TARGETS:SUMS])
 
-        def node_products(quarter, cb):
-            acc = short_lived([P, 2, QUARTER], F32, "acc")
+        def turn_sums(group, engine_copy):
+            width = GROUPS[group][1]
+            turned = short_lived([P, 2, width], F32, "ps_turn")
+            for plane in range(2):
+                for fb in range(width // BLK):
+                    nc.tensor.transpose(
+                        out=turned[:, plane, fb * BLK : (fb + 1) * BLK],
+                        in_=sums_t_of[group % 2][:, plane, fb, :],
+                        identity=ident_f[:],
+                    )
+            sums_of[group] = work.tile([P, 2, width], F32, name="sums")
+            engine_copy(out=sums_of[group][:], in_=turned[:])
+
+        def node_products(group, cb, engine_copy):
+            col0, width = GROUPS[group]
+            acc = short_lived([P, 2, width], F32, "acc")
             for plane in range(2):
                 nc.tensor.matmul(
                     out=acc[:, plane, :],
                     lhsT=x_f[:, plane, cb * BLK : (cb + 1) * BLK],
-                    rhs=sums_of[quarter][:, plane, :],
+                    rhs=sums_of[group][:, plane, :],
                     start=True,
                     stop=True,
                 )
-            result = o_pool.tile([P, 2, QUARTER], F32, name="result")
-            nc.scalar.copy(out=result[:], in_=acc[:])
-            both = out[0 : 2 * C, quarter * QUARTER : (quarter + 1) * QUARTER].rearrange("(a r) f -> r a f", a=2)
+            result = o_pool.tile([P, 2, width], F32, name="result")
+            engine_copy(out=result[:], in_=acc[:])
+            both = out[0 : 2 * C, col0 : col0 + width].rearrange("(a r) f -> r a f", a=2)
             nc.sync.dma_start(out=both[cb * BLK : (cb + 1) * BLK], in_=result[:])
 
-        def edge_product(h, cb):
-            acc = short_lived([P, HALF], F32, "acc")
-            for s in range(PASSES):
+        def edge_passes(acc, h, cb, passes):
+            for s in passes:
                 nc.tensor.matmul_mx(
-                    out=acc[:],
+                    out=acc,
                     lhsT=e_codes[:, s, cb * BLK : (cb + 1) * BLK].bitcast(E4M3X4),
                     lhsT_scale=e_scales[:, s, cb * BLK : (cb + 1) * BLK],
                     rhs=d_codes[h][:, s, :].bitcast(E5M2X4),
@@ -289,90 +321,114 @@ def tile_gnnlayer_pa_v_kernel(tc, x, e_enc, W_pre, b_pre, m, stat, arg, grad_out
                     start=(s == 0),
                     stop=(s == PASSES - 1),
                 )
-            return acc
 
-        def store_edge_product(acc, h, cb):
+        def store_edge_product(acc, h, cb, engine_copy):
             result = o_pool.tile([P, HALF], F32, name="result")
-            nc.vector.tensor_copy(out=result[:], in_=acc[:])
+            engine_copy(out=result[:], in_=acc)
             row0 = 2 * C + cb * BLK
             nc.sync.dma_start(out=out[row0 : row0 + BLK, h * HALF : (h + 1) * HALF], in_=result[:])
 
-        def outputs_and_last_step(k):
-            if k >= 3:
-                quarter, part = (k - 3) // GRAPHS, (k - 3) % GRAPHS
-                for cb in range(part * C_BLKS // GRAPHS, (part + 1) * C_BLKS // GRAPHS):
-                    node_products(quarter, cb)
-            if k >= 1:
-                regroup_gradient(k - 1)
-            edge_acc = {}
-            if k >= 5:
-                for cb in range((k - 5) * C_BLKS // 4, (k - 4) * C_BLKS // 4):
-                    edge_acc[cb] = edge_product(0, cb)
-            if k >= 1:
-                partial_sums(k - 1)
-            return edge_acc
+        def first_half_edges(cb):
+            acc = short_lived([P, HALF], F32, "acc")
+            edge_passes(acc[:], 0, cb, range(PASSES))
+            store_edge_product(acc[:], 0, cb, nc.scalar.copy)
 
-        def step(k, edge_acc):
-            quarter, graph = steps[k]
-            ca, jj, gg = spread_of[k]["ca"], spread_of[k]["jj"], spread_of[k]["gg"]
-            dm = dm_of[k]
+        pending = []
+        last_of_half_0 = max(k for k in range(STEPS) if GROUPS[steps[k][0]][0] < HALF)
+
+        def outputs(count):
+            for make in pending[0:count]:
+                make()
+            pending[0:count] = []
+
+        def step(k):
+            group, graph = steps[k]
+            col0, width = GROUPS[group]
             if k + 2 < STEPS:
                 dm_of[k + 2] = load_messages(*steps[k + 2])
-            if k + 2 < PASSES:
-                e_raw[k + 2] = load_edges(k + 2)
-            if graph == 0:
-                sums_ps_of[quarter] = psum.tile([P, PASSES, Q_BLKS, SUMS], F32, name="sums_ps")
+            if 1 <= k < PASSES - 1:
+                e_raw[k + 1] = load_edges(k + 1)
+            if k == 2:
+                j_rows[1] = load_j_rows(1)
+            c_row, a_row = spread_of[k]
+            jj, dm = jj_of[k], dm_of[k]
+            gg = g_hits[:, graph * PAIR : (graph + 1) * PAIR, :, col0 : col0 + width]
+            over_slots = [P, PAIR, PACK, width]
+            nc.vector.tensor_tensor(out=dm[:], in0=dm[:], in1=c_row[:].unsqueeze(2).to_broadcast(over_slots), op=ALU.mult)
+            nc.vector.tensor_tensor(out=dm[:], in0=dm[:], in1=a_row[:].unsqueeze(2).to_broadcast(over_slots), op=ALU.add)
+            complete = k >= 1 and steps[k - 1][1] == GRAPHS - 1
+            if k + 1 < STEPS:
+                round_j(k + 1)
+            outputs(2 * width // BLK)
+            if k >= 1:
+                regroup_gradient(k - 1)
+                partial_sums(k - 1)
+            if complete:
+                take_sums(steps[k - 1][0], nc.scalar.copy)
+            if k + 1 < STEPS:
+                spread_rows(k + 1)
+            if complete:
+                turn_sums(steps[k - 1][0], nc.scalar.copy)
+                pending.extend([lambda cb=cb, g=steps[k - 1][0]: node_products(g, cb, nc.scalar.copy) for cb in range(C_BLKS)])
+            outputs(2 * width // BLK)
+            if k + 2 < STEPS:
+                repeat_rows(k + 2)
+            for unit in EUNITS.get(k, ()):
+                regroup_edges(unit, nc.scalar.copy)
 
-            over_slots = [P, PAIR, PACK, QUARTER]
-            nc.vector.tensor_tensor(out=dm[:], in0=dm[:], in1=ca[:, 0].unsqueeze(2).to_broadcast(over_slots), op=ALU.mult)
-            nc.vector.tensor_tensor(out=dm[:], in0=dm[:], in1=ca[:, 1].unsqueeze(2).to_broadcast(over_slots), op=ALU.add)
-            hit = work.tile([P, 2, PAIR, PACK, QUARTER], BF16, name="hit")
+            hit = work.tile([P, 2, PAIR, PACK, width], BF16, name="hit")
             for t in range(PACK):
                 nc.vector.tensor_scalar(
                     out=hit[:, :, :, t, :], in0=jj[:], scalar1=src_f[:, t : t + 1], scalar2=None, op0=ALU.is_equal
                 )
-            nc.vector.tensor_tensor(
-                out=hit[:], in0=hit[:], in1=gg[:].unsqueeze(3).to_broadcast([P, 2] + over_slots[1:]), op=ALU.mult
-            )
-            for cb in edge_acc:
-                store_edge_product(edge_acc[cb], 0, cb)
-            if k >= 1:
-                quantise_gradient(k - 1)
-            if k < PASSES:
-                quantise(e_grp[k][:], e_codes[:, k, :], e_scales[:, k, :], E4M3X4)
+            for a in range(2):
+                nc.vector.tensor_tensor(
+                    out=hit[:, a], in0=hit[:, a], in1=gg[:, :, a].unsqueeze(2).to_broadcast(over_slots), op=ALU.mult
+                )
+            if k >= 2:
+                quantise_gradient(k - 2)
+                if k - 2 == last_of_half_0:
+                    pending.extend([lambda cb=cb: first_half_edges(cb) for cb in range(C_BLKS)])
+            for unit in EUNITS.get(k - 1, ()):
+                quantise_edges(unit)
             nc.vector.tensor_tensor(out=dm[:], in0=dm[:], in1=hit[:, 0], op=ALU.add)
             second_adder = nc.gpsimd if k + 1 < STEPS else nc.vector
             second_adder.tensor_tensor(out=dm[:], in0=dm[:], in1=hit[:, 1], op=ALU.add)
 
-            if k >= 1 and graph == 0:
-                turn_sums(quarter - 1)
-            if k + 2 < STEPS:
-                repeat_all(k + 2)
-            if k + 1 < STEPS:
-                spread_all(k + 1)
-            if k == 0:
-                regroup_edges(1, nc.vector.tensor_copy)
-            if k + 2 < PASSES:
-                regroup_edges(k + 2, nc.scalar.copy)
-
         tables["ca"] = turn_tables((c_tab, a_tab), ident_f, F32, "ca_t")
-        rep_of[0] = {"ca": repeat_rows(tables["ca"], *steps[0], "ca_rep")}
-        tables["jj"] = turn_tables((jmin, jmax), ident_f, BF16, "jj_t")
-        rep_of[0]["jj"] = repeat_rows(tables["jj"], *steps[0], "jj_rep")
-        tables["gg"] = turn_tables((g_min, g_max), ident_b, BF16, "gg_t")
-        rep_of[0]["gg"] = repeat_rows(tables["gg"], *steps[0], "gg_rep")
-        spread_all(0)
-        repeat_all(1)
+        repeat_rows(0)
+        spread_rows(0)
+        round_j(0)
+        repeat_rows(1)
         regroup_edges(0, nc.vector.tensor_copy)
+        regroup_edges(1, nc.vector.tensor_copy)
 
         for k in range(STEPS):
-            step(k, outputs_and_last_step(k))
+            step(k)
+            if k == 0:
+                cast_x()
 
-        edge_acc = outputs_and_last_step(STEPS)
-        for cb in edge_acc:
-            store_edge_product(edge_acc[cb], 0, cb)
-        quantise_gradient(STEPS - 1)
-        turn_sums(QUARTERS - 1)
+        last = STEPS - 1
+        regroup_gradient(last)
+        partial_sums(last)
+        quantise_gradient(last - 1)
+        take_sums(len(GROUPS) - 1, nc.vector.tensor_copy)
+        for make in pending:
+            make()
+        turn_sums(len(GROUPS) - 1, nc.vector.tensor_copy)
+        accs = []
+        for cb in range(4):
+            acc = psum.tile([P, HALF], F32, tag="ca"[cb % 2] + "_ps", bufs=1, name="edge_acc") if cb < 2 else short_lived([P, HALF], F32, "acc")
+            accs.append(acc[:])
+            edge_passes(acc[:], 1, cb, range(PAIR))
+        quantise_gradient(last)
         for cb in range(C_BLKS):
-            store_edge_product(edge_product(HALVES - 1, cb), HALVES - 1, cb)
-            node_products(QUARTERS - 1, cb)
+            if cb < len(accs):
+                edge_passes(accs[cb], 1, cb, range(PAIR, PASSES))
+            else:
+                acc = short_lived([P, HALF], F32, "acc")
+                accs.append(acc[:])
+                edge_passes(acc[:], 1, cb, range(PASSES))
+            store_edge_product(accs[cb], 1, cb, nc.scalar.copy if cb % 2 else nc.vector.tensor_copy)
+        for cb in range(C_BLKS):
+            node_products(len(GROUPS) - 1, cb, nc.scalar.copy if cb % 2 else nc.vector.tensor_copy)

@@ -24,7 +24,7 @@ TARGETS = K_PASS // NODES
 SPREAD = P // TARGETS
 HALF = 512
 HALVES = F // HALF
-WIDTHS = (256, 256, 256, 128, 128)
+WIDTHS = (256, 256, 256, 256)
 WIDE = max(WIDTHS)
 GROUPS = [(sum(WIDTHS[:i]), w) for i, w in enumerate(WIDTHS)]
 BLK = 128
@@ -32,8 +32,8 @@ BLKS = HALF // BLK
 C_BLKS = C // BLK
 SUMS = TARGETS + NODES
 STEPS = len(GROUPS) * GRAPHS
-EUNITS = {-1: (0, 1), 0: (2,), 1: (3,), 2: (4,), 3: (5,), 4: (6,), 5: (7,)}
-SHORT_LIVED_BANKS = 5
+EUNITS = {-1: (0, 1), 0: (2,), 1: (3,4), 2: (5,), 3: (6,), 4:(7,)}
+SHORT_LIVED_BANKS = 4
 
 FLOPS = 2 * EDGES * C * F + 2 * 2 * ALL_NODES * C * F
 BYTES = 2 * (ALL_NODES * C + EDGES * C + ALL_NODES * 4 * F) + 4 * (EDGES * F + 2 * ALL_NODES * 2 * F + 3 * C * F)
@@ -93,29 +93,12 @@ def tile_gnnlayer_pa_v_kernel(tc, x, e_enc, W_pre, b_pre, m, stat, arg, grad_out
         rstd = load_table(stat_rows, F, F32, "rstd")
         mean = load_table(stat_rows, 0, F32, "mean")
         g_mean = load_table(g_rows, 0, BF16, "g_mean")
-        g_hits = keep.tile([P, PASSES, 2, F], BF16)
-
-        def load_g_hits():
-            for r in range(SPREAD):
-                nc.sync.dma_start(
-                    out=g_hits[r:P:SPREAD].rearrange("q s a f -> q s (a f)"),
-                    in_=g_rows[:, F : 3 * F].rearrange("(s q) f -> q s f", q=TARGETS),
-                )
-
-        def load_j_rows(h):
-            rows_h = keep.tile([P, 2, PASSES, HALF], F32, name="j_rows" + str(h))
-            for a in range(2):
-                for r in range(SPREAD):
-                    nc.sync.dma_start(
-                        out=rows_h[r:P:SPREAD, a],
-                        in_=arg_rows[:, a * F + h * HALF : a * F + (h + 1) * HALF].rearrange("(s q) f -> q s f", q=TARGETS),
-                    )
-            return rows_h
-
+        jmin = load_table(arg_rows, 0, F32, "jmin")
+        jmax = load_table(arg_rows, F, F32, "jmax")
+        g_min = load_table(g_rows, F, BF16, "g_min")
+        g_max = load_table(g_rows, 2 * F, BF16, "g_max")
         e_raw = {0: load_edges(0)}
         dm_of = {0: load_messages(*steps[0])}
-        j_rows = {0: load_j_rows(0)}
-        load_g_hits()
         e_raw[1] = load_edges(1)
         dm_of[1] = load_messages(*steps[1])
         x_b = setup.tile([P, 2, C], BF16)
@@ -175,36 +158,60 @@ def tile_gnnlayer_pa_v_kernel(tc, x, e_enc, W_pre, b_pre, m, stat, arg, grad_out
         rep_of = {}
         spread_of = {}
         jj_of = {}
+        gg_of = {}
 
-        def repeat_rows(k):
+        PAIRS = {"ca": (F32, ident_f), "jj": (BF16, ident_b), "gg": (BF16, ident_b)}
+
+        def repeat_rows(k, names=("ca", "jj", "gg")):
             group, graph = steps[k]
             fb0, blks = GROUPS[group][0] // BLK, GROUPS[group][1] // BLK
             h = fb0 // BLKS
-            rep_of[k] = rep_pool.tile([P, blks, 2, NODES, SPREAD], F32, name="ca_rep")
-            rows = tables["ca"][:].rearrange("p f a (n h) -> p f a n h", h=HALVES)
-            rows = rows[:, fb0 % BLKS : fb0 % BLKS + blks, :, graph * NODES : (graph + 1) * NODES, h]
-            nc.scalar.copy(out=rep_of[k][:], in_=rows.unsqueeze(4).to_broadcast([P, blks, 2, NODES, SPREAD]))
+            for name in names:
+                repeated = rep_pool.tile([P, blks, 2, NODES, SPREAD], PAIRS[name][0], name=name + "_rep")
+                rows = tables[name][:].rearrange("p f a (n h) -> p f a n h", h=HALVES)
+                rows = rows[:, fb0 % BLKS : fb0 % BLKS + blks, :, graph * NODES : (graph + 1) * NODES, h]
+                nc.scalar.copy(out=repeated[:], in_=rows.unsqueeze(4).to_broadcast([P, blks, 2, NODES, SPREAD]))
+                rep_of.setdefault(k, {})[name] = repeated
 
-        def spread_rows(k):
+        def turn_back(k, name, a, spread):
+            width = GROUPS[steps[k][0]][1]
+            for sp in range(PAIR):
+                for fb in range(width // BLK):
+                    nc.tensor.transpose(
+                        out=spread[:, sp, fb * BLK : (fb + 1) * BLK],
+                        in_=rep_of[k][name][:, fb, a, sp * TARGETS : (sp + 1) * TARGETS, :].rearrange("p q r -> p (q r)"),
+                        identity=PAIRS[name][1][:],
+                    )
+
+        def spread_ca(k):
             width = GROUPS[steps[k][0]][1]
             spread_of[k] = []
             for a in range(2):
-                spread = psum.tile([P, PAIR, width], F32, tag="ca"[a] + "_ps", bufs=1, name="ca"[a] + "_ps")
-                for sp in range(PAIR):
-                    for fb in range(width // BLK):
-                        nc.tensor.transpose(
-                            out=spread[:, sp, fb * BLK : (fb + 1) * BLK],
-                            in_=rep_of[k][:, fb, a, sp * TARGETS : (sp + 1) * TARGETS, :].rearrange("p q r -> p (q r)"),
-                            identity=ident_f[:],
-                        )
-                spread_of[k].append(spread)
+                spread_of[k].append(psum.tile([P, PAIR, width], F32, tag="ca"[a] + "_ps", bufs=1, name="ca"[a] + "_ps"))
+                turn_back(k, "ca", a, spread_of[k][a])
 
-        def round_j(k):
-            group, graph = steps[k]
-            col0, width = GROUPS[group]
-            h, col = col0 // HALF, col0 % HALF
+        def spread_gg(k):
+            gg_of[k] = psum.tile([P, 2, PAIR, GROUPS[steps[k][0]][1]], BF16, tag="gg_ps", bufs=1, name="gg_ps")
+            for a in range(2):
+                turn_back(k, "gg", a, gg_of[k][:, a])
+
+        def spread_jj(k):
+            width = GROUPS[steps[k][0]][1]
+            jj_ps = short_lived([P, 2, PAIR, width], BF16, "jj_ps")
+            for a in range(2):
+                turn_back(k, "jj", a, jj_ps[:, a])
             jj_of[k] = work.tile([P, 2, PAIR, width], BF16, name="jj")
-            nc.scalar.copy(out=jj_of[k][:], in_=j_rows[h][:, :, graph * PAIR : (graph + 1) * PAIR, col : col + width])
+            nc.scalar.copy(out=jj_of[k][:], in_=jj_ps[:])
+
+        hit_of = {}
+
+        def masks(k):
+            width = GROUPS[steps[k][0]][1]
+            hit_of[k] = work.tile([P, 2, PAIR, PACK, width], BF16, name="hit")
+            for t in range(PACK):
+                nc.vector.tensor_scalar(
+                    out=hit_of[k][:, :, :, t, :], in0=jj_of[k][:], scalar1=src_f[:, t : t + 1], scalar2=None, op0=ALU.is_equal
+                )
 
         x_f = keep.tile([P, 2, C], F32)
 
@@ -346,19 +353,19 @@ def tile_gnnlayer_pa_v_kernel(tc, x, e_enc, W_pre, b_pre, m, stat, arg, grad_out
             col0, width = GROUPS[group]
             if k + 2 < STEPS:
                 dm_of[k + 2] = load_messages(*steps[k + 2])
-            if 1 <= k < PASSES - 1:
-                e_raw[k + 1] = load_edges(k + 1)
-            if k == 2:
-                j_rows[1] = load_j_rows(1)
+            if k < PASSES - 2:
+                e_raw[k + 2] = load_edges(k + 2)
             c_row, a_row = spread_of[k]
-            jj, dm = jj_of[k], dm_of[k]
-            gg = g_hits[:, graph * PAIR : (graph + 1) * PAIR, :, col0 : col0 + width]
+            dm, hit = dm_of[k], hit_of[k]
             over_slots = [P, PAIR, PACK, width]
             nc.vector.tensor_tensor(out=dm[:], in0=dm[:], in1=c_row[:].unsqueeze(2).to_broadcast(over_slots), op=ALU.mult)
             nc.vector.tensor_tensor(out=dm[:], in0=dm[:], in1=a_row[:].unsqueeze(2).to_broadcast(over_slots), op=ALU.add)
+            nc.vector.tensor_tensor(
+                out=hit[:], in0=hit[:], in1=gg_of[k][:].unsqueeze(3).to_broadcast([P, 2] + over_slots[1:]), op=ALU.mult
+            )
+            for unit in EUNITS.get(k, ()):
+                regroup_edges(unit, nc.scalar.copy)
             complete = k >= 1 and steps[k - 1][1] == GRAPHS - 1
-            if k + 1 < STEPS:
-                round_j(k + 1)
             outputs(2 * width // BLK)
             if k >= 1:
                 regroup_gradient(k - 1)
@@ -366,41 +373,47 @@ def tile_gnnlayer_pa_v_kernel(tc, x, e_enc, W_pre, b_pre, m, stat, arg, grad_out
             if complete:
                 take_sums(steps[k - 1][0], nc.scalar.copy)
             if k + 1 < STEPS:
-                spread_rows(k + 1)
+                spread_ca(k + 1)
+            if k + 2 < STEPS:
+                spread_jj(k + 2)
             if complete:
                 turn_sums(steps[k - 1][0], nc.scalar.copy)
                 pending.extend([lambda cb=cb, g=steps[k - 1][0]: node_products(g, cb, nc.scalar.copy) for cb in range(C_BLKS)])
-            outputs(2 * width // BLK)
+            if k + 1 < STEPS:
+                spread_gg(k + 1)
+            outputs(2 * width // BLK if k + 1 < STEPS else len(pending))
             if k + 2 < STEPS:
-                repeat_rows(k + 2)
-            for unit in EUNITS.get(k, ()):
-                regroup_edges(unit, nc.scalar.copy)
-
-            hit = work.tile([P, 2, PAIR, PACK, width], BF16, name="hit")
-            for t in range(PACK):
-                nc.vector.tensor_scalar(
-                    out=hit[:, :, :, t, :], in0=jj[:], scalar1=src_f[:, t : t + 1], scalar2=None, op0=ALU.is_equal
-                )
-            for a in range(2):
-                nc.vector.tensor_tensor(
-                    out=hit[:, a], in0=hit[:, a], in1=gg[:, :, a].unsqueeze(2).to_broadcast(over_slots), op=ALU.mult
-                )
+                repeat_rows(k + 2, ["ca", "gg"])
+            if k + 3 < STEPS:
+                repeat_rows(k + 3, ["jj"])
             if k >= 2:
                 quantise_gradient(k - 2)
                 if k - 2 == last_of_half_0:
                     pending.extend([lambda cb=cb: first_half_edges(cb) for cb in range(C_BLKS)])
             for unit in EUNITS.get(k - 1, ()):
                 quantise_edges(unit)
+            if k + 1 < STEPS:
+                masks(k + 1)
             nc.vector.tensor_tensor(out=dm[:], in0=dm[:], in1=hit[:, 0], op=ALU.add)
-            second_adder = nc.gpsimd if k + 1 < STEPS else nc.vector
-            second_adder.tensor_tensor(out=dm[:], in0=dm[:], in1=hit[:, 1], op=ALU.add)
+            if k + 1 < STEPS:
+                nc.gpsimd.tensor_tensor(out=dm[:], in0=dm[:], in1=hit[:, 1], op=ALU.add)
+            else:
+                nc.vector.tensor_tensor(out=dm[:], in0=dm[:], in1=hit[:, 1], op=ALU.add)
 
         tables["ca"] = turn_tables((c_tab, a_tab), ident_f, F32, "ca_t")
-        repeat_rows(0)
-        spread_rows(0)
-        round_j(0)
+        repeat_rows(0, ["ca"])
+        tables["jj"] = turn_tables((jmin, jmax), ident_f, BF16, "jj_t")
+        repeat_rows(0, ["jj"])
+        tables["gg"] = turn_tables((g_min, g_max), ident_b, BF16, "gg_t")
+        repeat_rows(0, ["gg"])
+        spread_ca(0)
+        spread_jj(0)
+        spread_gg(0)
         repeat_rows(1)
+        spread_jj(1)
+        repeat_rows(2, ["jj"])
         regroup_edges(0, nc.vector.tensor_copy)
+        masks(0)
         regroup_edges(1, nc.vector.tensor_copy)
 
         for k in range(STEPS):
@@ -410,18 +423,17 @@ def tile_gnnlayer_pa_v_kernel(tc, x, e_enc, W_pre, b_pre, m, stat, arg, grad_out
 
         last = STEPS - 1
         regroup_gradient(last)
-        partial_sums(last)
         quantise_gradient(last - 1)
-        take_sums(len(GROUPS) - 1, nc.vector.tensor_copy)
-        for make in pending:
-            make()
-        turn_sums(len(GROUPS) - 1, nc.vector.tensor_copy)
         accs = []
-        for cb in range(4):
-            acc = psum.tile([P, HALF], F32, tag="ca"[cb % 2] + "_ps", bufs=1, name="edge_acc") if cb < 2 else short_lived([P, HALF], F32, "acc")
+        for cb in range(3):
+            acc = psum.tile([P, HALF], F32, tag="ca"[cb % 2] + "_ps", bufs=1, name="edge_acc") if cb < 2 else psum.tile([P, HALF], F32, tag="gg_ps", bufs=1, name="edge_acc") if cb < 3 else short_lived([P, HALF], F32, "acc")
             accs.append(acc[:])
             edge_passes(acc[:], 1, cb, range(PAIR))
+        partial_sums(last)
+        for make in pending:
+            make()
         quantise_gradient(last)
+        take_sums(len(GROUPS) - 1, nc.vector.tensor_copy)
         for cb in range(C_BLKS):
             if cb < len(accs):
                 edge_passes(accs[cb], 1, cb, range(PAIR, PASSES))
@@ -430,5 +442,7 @@ def tile_gnnlayer_pa_v_kernel(tc, x, e_enc, W_pre, b_pre, m, stat, arg, grad_out
                 accs.append(acc[:])
                 edge_passes(acc[:], 1, cb, range(PASSES))
             store_edge_product(accs[cb], 1, cb, nc.scalar.copy if cb % 2 else nc.vector.tensor_copy)
+            if cb == 1:
+                turn_sums(len(GROUPS) - 1, nc.vector.tensor_copy)
         for cb in range(C_BLKS):
             node_products(len(GROUPS) - 1, cb, nc.scalar.copy if cb % 2 else nc.vector.tensor_copy)

@@ -32,8 +32,11 @@ BLKS = HALF // BLK
 C_BLKS = C // BLK
 SUMS = TARGETS + NODES
 STEPS = len(GROUPS) * GRAPHS
-EUNITS = {-1: (0, 1), 0: (2,), 1: (3,4), 2: (5,), 3: (6,), 4:(7,)}
-SHORT_LIVED_BANKS = 4
+N1 = [3 * GROUPS[k // GRAPHS][1] // BLK for k in range(STEPS)]
+N2 = [1 * GROUPS[k // GRAPHS][1] // BLK for k in range(STEPS)]
+E_PIECES = 4
+E_FREE = {k: 8 for k in range(5)}
+SHORT_LIVED_BANKS = 3
 
 FLOPS = 2 * EDGES * C * F + 2 * 2 * ALL_NODES * C * F
 BYTES = 2 * (ALL_NODES * C + EDGES * C + ALL_NODES * 4 * F) + 4 * (EDGES * F + 2 * ALL_NODES * 2 * F + 3 * C * F)
@@ -55,9 +58,10 @@ def tile_gnnlayer_pa_v_kernel(tc, x, e_enc, W_pre, b_pre, m, stat, arg, grad_out
         keep = ctx.enter_context(tc.tile_pool(name="keep", bufs=1))
         setup = ctx.enter_context(tc.tile_pool(name="setup", bufs=1))
         e_pool = ctx.enter_context(tc.tile_pool(name="e_pool", bufs=2))
-        e_grp_pool = ctx.enter_context(tc.tile_pool(name="e_grp_pool", bufs=3))
+        e_grp_pool = ctx.enter_context(tc.tile_pool(name="e_grp_pool", bufs=4))
         rep_pool = ctx.enter_context(tc.tile_pool(name="rep_pool", bufs=2))
         m_pool = ctx.enter_context(tc.tile_pool(name="m_pool", bufs=4))
+        hit_pool = ctx.enter_context(tc.tile_pool(name="hit_pool", bufs=2))
         work = ctx.enter_context(tc.tile_pool(name="work", bufs=2))
         o_pool = ctx.enter_context(tc.tile_pool(name="o_pool", bufs=5))
         psum = ctx.enter_context(tc.psum_pool(name="psum", bufs=1))
@@ -67,9 +71,26 @@ def tile_gnnlayer_pa_v_kernel(tc, x, e_enc, W_pre, b_pre, m, stat, arg, grad_out
 
         def load_table(rows, col0, dtype, name):
             table = setup.tile([P, HALF], dtype, name=name)
-            for h in range(HALVES):
-                nc.sync.dma_start(out=table[h:P:HALVES, :], in_=rows[:, col0 + h * HALF : col0 + (h + 1) * HALF])
+            nc.sync.dma_start(out=table[:], in_=rows[:, col0 : col0 + F].rearrange("n (h f) -> n h f", h=HALVES))
             return table
+
+        hit_tables = {}
+
+        def load_hit_tables(h, graph):
+            j_rows = hit_pool.tile([P, 2, PAIR, HALF], F32, bufs=2, name="j_rows")
+            g_hits = hit_pool.tile([P, 2, PAIR, HALF], BF16, bufs=3, name="g_hits")
+            for dst, rows, col0 in ((j_rows, arg_rows, 0), (g_hits, g_rows, F)):
+                for a in range(2):
+                    for sp in range(PAIR):
+                        row0 = graph * NODES + sp * TARGETS
+                        col = col0 + a * F + h * HALF
+                        nc.sync.dma_start(
+                            out=dst[:, a, sp, :],
+                            in_=rows[row0 : row0 + TARGETS, col : col + HALF]
+                            .unsqueeze(1)
+                            .to_broadcast([TARGETS, SPREAD, HALF]),
+                        )
+            hit_tables[h, graph] = (j_rows, g_hits)
 
         def load_edges(s):
             e_raw = e_pool.tile([P, PACK, C], BF16, name="e_raw")
@@ -93,14 +114,12 @@ def tile_gnnlayer_pa_v_kernel(tc, x, e_enc, W_pre, b_pre, m, stat, arg, grad_out
         rstd = load_table(stat_rows, F, F32, "rstd")
         mean = load_table(stat_rows, 0, F32, "mean")
         g_mean = load_table(g_rows, 0, BF16, "g_mean")
-        jmin = load_table(arg_rows, 0, F32, "jmin")
-        jmax = load_table(arg_rows, F, F32, "jmax")
-        g_min = load_table(g_rows, F, BF16, "g_min")
-        g_max = load_table(g_rows, 2 * F, BF16, "g_max")
-        e_raw = {0: load_edges(0)}
+        load_hit_tables(0, 0)
         dm_of = {0: load_messages(*steps[0])}
-        e_raw[1] = load_edges(1)
+        e_raw = {0: load_edges(0)}
+        load_hit_tables(0, 1)
         dm_of[1] = load_messages(*steps[1])
+        e_raw[1] = load_edges(1)
         x_b = setup.tile([P, 2, C], BF16)
         nc.sync.dma_start(out=x_b[0:ALL_NODES, 0, :], in_=x_rows)
         for s in range(PASSES):
@@ -111,8 +130,6 @@ def tile_gnnlayer_pa_v_kernel(tc, x, e_enc, W_pre, b_pre, m, stat, arg, grad_out
 
         ident_f = const.tile([P, P], F32)
         make_identity(nc, ident_f[:])
-        ident_b = const.tile([P, P], BF16)
-        make_identity(nc, ident_b[:])
         edge_i = const.tile([P, PACK], I32)
         nc.gpsimd.iota(edge_i[:], pattern=[[1, PACK]], base=0, channel_multiplier=PACK)
         col_i = const.tile([P, NODES], I32)
@@ -145,63 +162,48 @@ def tile_gnnlayer_pa_v_kernel(tc, x, e_enc, W_pre, b_pre, m, stat, arg, grad_out
             out=a_tab[:], in0=g_mean[:], scalar=1.0 / NODES, in1=mean[:], op0=ALU.mult, op1=ALU.subtract
         )
 
-        def turn_tables(pair, ident, out_dtype, name):
-            turned_sb = keep.tile([P, BLKS, 2, P], out_dtype, name=name)
+        def turn_tables(pair, name):
+            turned_sb = keep.tile([P, BLKS, 2, P], F32, name=name)
             for a, table in enumerate(pair):
-                turned = short_lived([P, BLKS, P], table.dtype, "turned")
+                turned = short_lived([P, BLKS, P], F32, "turned")
                 for fb in range(BLKS):
-                    nc.tensor.transpose(out=turned[:, fb, :], in_=table[:, fb * BLK : (fb + 1) * BLK], identity=ident[:])
+                    nc.tensor.transpose(out=turned[:, fb, :], in_=table[:, fb * BLK : (fb + 1) * BLK], identity=ident_f[:])
                 nc.scalar.copy(out=turned_sb[:, :, a, :], in_=turned[:])
             return turned_sb
 
-        tables = {}
         rep_of = {}
         spread_of = {}
         jj_of = {}
-        gg_of = {}
 
-        PAIRS = {"ca": (F32, ident_f), "jj": (BF16, ident_b), "gg": (BF16, ident_b)}
-
-        def repeat_rows(k, names=("ca", "jj", "gg")):
+        def repeat_rows(k):
             group, graph = steps[k]
             fb0, blks = GROUPS[group][0] // BLK, GROUPS[group][1] // BLK
             h = fb0 // BLKS
-            for name in names:
-                repeated = rep_pool.tile([P, blks, 2, NODES, SPREAD], PAIRS[name][0], name=name + "_rep")
-                rows = tables[name][:].rearrange("p f a (n h) -> p f a n h", h=HALVES)
-                rows = rows[:, fb0 % BLKS : fb0 % BLKS + blks, :, graph * NODES : (graph + 1) * NODES, h]
-                nc.scalar.copy(out=repeated[:], in_=rows.unsqueeze(4).to_broadcast([P, blks, 2, NODES, SPREAD]))
-                rep_of.setdefault(k, {})[name] = repeated
+            rep_of[k] = rep_pool.tile([P, blks, 2, NODES, SPREAD], F32, name="ca_rep")
+            rows = ca_t[:].rearrange("p f a (n h) -> p f a n h", h=HALVES)
+            rows = rows[:, fb0 % BLKS : fb0 % BLKS + blks, :, graph * NODES : (graph + 1) * NODES, h]
+            nc.scalar.copy(out=rep_of[k][:], in_=rows.unsqueeze(4).to_broadcast([P, blks, 2, NODES, SPREAD]))
 
-        def turn_back(k, name, a, spread):
-            width = GROUPS[steps[k][0]][1]
-            for sp in range(PAIR):
-                for fb in range(width // BLK):
-                    nc.tensor.transpose(
-                        out=spread[:, sp, fb * BLK : (fb + 1) * BLK],
-                        in_=rep_of[k][name][:, fb, a, sp * TARGETS : (sp + 1) * TARGETS, :].rearrange("p q r -> p (q r)"),
-                        identity=PAIRS[name][1][:],
-                    )
-
-        def spread_ca(k):
+        def spread_rows(k):
             width = GROUPS[steps[k][0]][1]
             spread_of[k] = []
             for a in range(2):
-                spread_of[k].append(psum.tile([P, PAIR, width], F32, tag="ca"[a] + "_ps", bufs=1, name="ca"[a] + "_ps"))
-                turn_back(k, "ca", a, spread_of[k][a])
+                spread = psum.tile([P, PAIR, width], F32, tag="ca"[a] + "_ps", bufs=2, name="ca"[a] + "_ps")
+                for sp in range(PAIR):
+                    for fb in range(width // BLK):
+                        nc.tensor.transpose(
+                            out=spread[:, sp, fb * BLK : (fb + 1) * BLK],
+                            in_=rep_of[k][:, fb, a, sp * TARGETS : (sp + 1) * TARGETS, :].rearrange("p q r -> p (q r)"),
+                            identity=ident_f[:],
+                        )
+                spread_of[k].append(spread)
 
-        def spread_gg(k):
-            gg_of[k] = psum.tile([P, 2, PAIR, GROUPS[steps[k][0]][1]], BF16, tag="gg_ps", bufs=1, name="gg_ps")
-            for a in range(2):
-                turn_back(k, "gg", a, gg_of[k][:, a])
-
-        def spread_jj(k):
-            width = GROUPS[steps[k][0]][1]
-            jj_ps = short_lived([P, 2, PAIR, width], BF16, "jj_ps")
-            for a in range(2):
-                turn_back(k, "jj", a, jj_ps[:, a])
+        def round_j(k):
+            group, graph = steps[k]
+            col0, width = GROUPS[group]
             jj_of[k] = work.tile([P, 2, PAIR, width], BF16, name="jj")
-            nc.scalar.copy(out=jj_of[k][:], in_=jj_ps[:])
+            col = col0 % HALF
+            nc.scalar.copy(out=jj_of[k][:], in_=hit_tables[col0 // HALF, graph][0][:, :, :, col : col + width])
 
         hit_of = {}
 
@@ -211,6 +213,19 @@ def tile_gnnlayer_pa_v_kernel(tc, x, e_enc, W_pre, b_pre, m, stat, arg, grad_out
             for t in range(PACK):
                 nc.vector.tensor_scalar(
                     out=hit_of[k][:, :, :, t, :], in0=jj_of[k][:], scalar1=src_f[:, t : t + 1], scalar2=None, op0=ALU.is_equal
+                )
+
+        def hits(k):
+            group, graph = steps[k]
+            col0, width = GROUPS[group]
+            col = col0 % HALF
+            g_hits = hit_tables[col0 // HALF, graph][1]
+            for a in range(2):
+                nc.vector.tensor_tensor(
+                    out=hit_of[k][:, a],
+                    in0=hit_of[k][:, a],
+                    in1=g_hits[:, a, :, col : col + width].unsqueeze(2).to_broadcast([P, PAIR, PACK, width]),
+                    op=ALU.mult,
                 )
 
         x_f = keep.tile([P, 2, C], F32)
@@ -235,10 +250,12 @@ def tile_gnnlayer_pa_v_kernel(tc, x, e_enc, W_pre, b_pre, m, stat, arg, grad_out
         def quantise(grouped, codes, scales, fmt):
             nc.vector.quantize_mx(out=codes.bitcast(fmt), scales=scales, in_=grouped.rearrange("p c t -> p (c t)"))
 
-        def regroup_edges(unit, engine_copy):
-            s, c0 = unit // 2, unit % 2 * (C // 2)
-            e_grp[unit] = e_grp_pool.tile([P, C // 2, PACK], BF16, align_bytes=64, name="e_grp")
-            regroup(engine_copy, e_grp[unit][:], e_raw[s][:, :, c0 : c0 + C // 2])
+        def regroup_edges(unit, piece, engine_copy):
+            s, c0, cols = unit // 2, unit % 2 * (C // 2), C // 2 // E_PIECES
+            if piece == 0:
+                e_grp[unit] = e_grp_pool.tile([P, C // 2, PACK], BF16, align_bytes=64, name="e_grp")
+            at = piece * cols
+            regroup(engine_copy, e_grp[unit][:, at : at + cols, :], e_raw[s][:, :, c0 + at : c0 + at + cols])
 
         def quantise_edges(unit):
             s, c0 = unit // 2, unit % 2 * (C // 2)
@@ -336,16 +353,34 @@ def tile_gnnlayer_pa_v_kernel(tc, x, e_enc, W_pre, b_pre, m, stat, arg, grad_out
             nc.sync.dma_start(out=out[row0 : row0 + BLK, h * HALF : (h + 1) * HALF], in_=result[:])
 
         def first_half_edges(cb):
+            assert not side and not regrouped
             acc = short_lived([P, HALF], F32, "acc")
             edge_passes(acc[:], 0, cb, range(PASSES))
             store_edge_product(acc[:], 0, cb, nc.scalar.copy)
 
         pending = []
+        first_of_tables = {}
+        for k, (group, graph) in enumerate(steps):
+            key = (GROUPS[group][0] // HALF, graph)
+            if key[0] > 0 and key not in first_of_tables.values():
+                first_of_tables[k] = key
         last_of_half_0 = max(k for k in range(STEPS) if GROUPS[steps[k][0]][0] < HALF)
+
+        side = [(unit, piece) for unit in range(2 * PASSES) for piece in range(E_PIECES)]
+        regrouped = []
+
+        def edge_pieces(count):
+            for unit, piece in side[0:count]:
+                if unit // 2 in e_raw:
+                    regroup_edges(unit, piece, nc.scalar.copy)
+                    side.remove((unit, piece))
+                    if piece + 1 == E_PIECES:
+                        regrouped.append(unit)
 
         def outputs(count):
             for make in pending[0:count]:
                 make()
+                edge_pieces(1)
             pending[0:count] = []
 
         def step(k):
@@ -353,68 +388,57 @@ def tile_gnnlayer_pa_v_kernel(tc, x, e_enc, W_pre, b_pre, m, stat, arg, grad_out
             col0, width = GROUPS[group]
             if k + 2 < STEPS:
                 dm_of[k + 2] = load_messages(*steps[k + 2])
-            if k < PASSES - 2:
-                e_raw[k + 2] = load_edges(k + 2)
+            if 1 <= k < PASSES - 1:
+                e_raw[k + 1] = load_edges(k + 1)
+            if k + 3 in first_of_tables:
+                load_hit_tables(*first_of_tables[k + 3])
             c_row, a_row = spread_of[k]
-            dm, hit = dm_of[k], hit_of[k]
-            over_slots = [P, PAIR, PACK, width]
-            nc.vector.tensor_tensor(out=dm[:], in0=dm[:], in1=c_row[:].unsqueeze(2).to_broadcast(over_slots), op=ALU.mult)
-            nc.vector.tensor_tensor(out=dm[:], in0=dm[:], in1=a_row[:].unsqueeze(2).to_broadcast(over_slots), op=ALU.add)
-            nc.vector.tensor_tensor(
-                out=hit[:], in0=hit[:], in1=gg_of[k][:].unsqueeze(3).to_broadcast([P, 2] + over_slots[1:]), op=ALU.mult
-            )
-            for unit in EUNITS.get(k, ()):
-                regroup_edges(unit, nc.scalar.copy)
+            dm = dm_of[k]
+            over_slots = [P, PACK, width]
+            for row, op in ((c_row, ALU.mult), (a_row, ALU.add)):
+                for sp in range(PAIR):
+                    nc.vector.tensor_tensor(
+                        out=dm[:, sp], in0=dm[:, sp], in1=row[:, sp, :].unsqueeze(1).to_broadcast(over_slots), op=op
+                    )
             complete = k >= 1 and steps[k - 1][1] == GRAPHS - 1
-            outputs(2 * width // BLK)
+            for unit in regrouped:
+                quantise_edges(unit)
+            regrouped.clear()
+            if k + 1 < STEPS:
+                spread_rows(k + 1)
+            outputs(N1[k])
+            edge_pieces(E_FREE.get(k, 0))
+            if k + 2 < STEPS:
+                repeat_rows(k + 2)
+                round_j(k + 2)
             if k >= 1:
                 regroup_gradient(k - 1)
                 partial_sums(k - 1)
             if complete:
                 take_sums(steps[k - 1][0], nc.scalar.copy)
-            if k + 1 < STEPS:
-                spread_ca(k + 1)
-            if k + 2 < STEPS:
-                spread_jj(k + 2)
-            if complete:
                 turn_sums(steps[k - 1][0], nc.scalar.copy)
                 pending.extend([lambda cb=cb, g=steps[k - 1][0]: node_products(g, cb, nc.scalar.copy) for cb in range(C_BLKS)])
-            if k + 1 < STEPS:
-                spread_gg(k + 1)
-            outputs(2 * width // BLK if k + 1 < STEPS else len(pending))
-            if k + 2 < STEPS:
-                repeat_rows(k + 2, ["ca", "gg"])
-            if k + 3 < STEPS:
-                repeat_rows(k + 3, ["jj"])
-            if k >= 2:
-                quantise_gradient(k - 2)
-                if k - 2 == last_of_half_0:
-                    pending.extend([lambda cb=cb: first_half_edges(cb) for cb in range(C_BLKS)])
-            for unit in EUNITS.get(k - 1, ()):
-                quantise_edges(unit)
+            outputs(N2[k] if k + 1 < STEPS else len(pending))
             if k + 1 < STEPS:
                 masks(k + 1)
-            nc.vector.tensor_tensor(out=dm[:], in0=dm[:], in1=hit[:, 0], op=ALU.add)
+            for old in [k - 2] * (k - 2 >= 0 and k - 2 != last_of_half_0) + [k - 1] * (k - 1 == last_of_half_0):
+                quantise_gradient(old)
+                if old == last_of_half_0:
+                    pending.extend([lambda cb=cb: first_half_edges(cb) for cb in range(C_BLKS)])
             if k + 1 < STEPS:
-                nc.gpsimd.tensor_tensor(out=dm[:], in0=dm[:], in1=hit[:, 1], op=ALU.add)
-            else:
-                nc.vector.tensor_tensor(out=dm[:], in0=dm[:], in1=hit[:, 1], op=ALU.add)
+                hits(k + 1)
+            nc.vector.tensor_tensor(out=dm[:], in0=dm[:], in1=hit_of[k][:, 0], op=ALU.add)
+            second_adder = nc.gpsimd if k + 1 < STEPS else nc.vector
+            second_adder.tensor_tensor(out=dm[:], in0=dm[:], in1=hit_of[k][:, 1], op=ALU.add)
 
-        tables["ca"] = turn_tables((c_tab, a_tab), ident_f, F32, "ca_t")
-        repeat_rows(0, ["ca"])
-        tables["jj"] = turn_tables((jmin, jmax), ident_f, BF16, "jj_t")
-        repeat_rows(0, ["jj"])
-        tables["gg"] = turn_tables((g_min, g_max), ident_b, BF16, "gg_t")
-        repeat_rows(0, ["gg"])
-        spread_ca(0)
-        spread_jj(0)
-        spread_gg(0)
-        repeat_rows(1)
-        spread_jj(1)
-        repeat_rows(2, ["jj"])
-        regroup_edges(0, nc.vector.tensor_copy)
+        ca_t = turn_tables((c_tab, a_tab), "ca_t")
+        round_j(0)
+        repeat_rows(0)
+        spread_rows(0)
         masks(0)
-        regroup_edges(1, nc.vector.tensor_copy)
+        hits(0)
+        repeat_rows(1)
+        round_j(1)
 
         for k in range(STEPS):
             step(k)
@@ -425,8 +449,8 @@ def tile_gnnlayer_pa_v_kernel(tc, x, e_enc, W_pre, b_pre, m, stat, arg, grad_out
         regroup_gradient(last)
         quantise_gradient(last - 1)
         accs = []
-        for cb in range(3):
-            acc = psum.tile([P, HALF], F32, tag="ca"[cb % 2] + "_ps", bufs=1, name="edge_acc") if cb < 2 else psum.tile([P, HALF], F32, tag="gg_ps", bufs=1, name="edge_acc") if cb < 3 else short_lived([P, HALF], F32, "acc")
+        for cb in range(4):
+            acc = psum.tile([P, HALF], F32, tag="ca"[cb % 2] + "_ps", bufs=2, name="edge_acc")
             accs.append(acc[:])
             edge_passes(acc[:], 1, cb, range(PAIR))
         partial_sums(last)

@@ -35,6 +35,11 @@ STEPS = len(GROUPS) * GRAPHS
 N1 = [3 * GROUPS[k // GRAPHS][1] // BLK for k in range(STEPS)]
 N2 = [1 * GROUPS[k // GRAPHS][1] // BLK for k in range(STEPS)]
 E_PIECES = 4
+E_QUANT = {3: 1, 4: 4, 5: 3}
+LATE_SPREAD = (2, 4)
+ADDS = (("vector", 1, slice(3, PACK)), ("gpsimd", 0, slice(0, PACK)), ("gpsimd", 1, slice(0, 3)))
+TURNED = (6, 7)
+TA, TB = 4, 8
 E_FREE = {k: 8 for k in range(5)}
 SHORT_LIVED_BANKS = 3
 
@@ -58,7 +63,7 @@ def tile_gnnlayer_pa_v_kernel(tc, x, e_enc, W_pre, b_pre, m, stat, arg, grad_out
         keep = ctx.enter_context(tc.tile_pool(name="keep", bufs=1))
         setup = ctx.enter_context(tc.tile_pool(name="setup", bufs=1))
         e_pool = ctx.enter_context(tc.tile_pool(name="e_pool", bufs=2))
-        e_grp_pool = ctx.enter_context(tc.tile_pool(name="e_grp_pool", bufs=4))
+        e_grp_pool = ctx.enter_context(tc.tile_pool(name="e_grp_pool", bufs=7))
         rep_pool = ctx.enter_context(tc.tile_pool(name="rep_pool", bufs=2))
         m_pool = ctx.enter_context(tc.tile_pool(name="m_pool", bufs=4))
         hit_pool = ctx.enter_context(tc.tile_pool(name="hit_pool", bufs=2))
@@ -76,21 +81,25 @@ def tile_gnnlayer_pa_v_kernel(tc, x, e_enc, W_pre, b_pre, m, stat, arg, grad_out
 
         hit_tables = {}
 
-        def load_hit_tables(h, graph):
-            j_rows = hit_pool.tile([P, 2, PAIR, HALF], F32, bufs=2, name="j_rows")
-            g_hits = hit_pool.tile([P, 2, PAIR, HALF], BF16, bufs=3, name="g_hits")
-            for dst, rows, col0 in ((j_rows, arg_rows, 0), (g_hits, g_rows, F)):
+        def load_hit_tables(graph, col0, width):
+            whole = width == HALF
+            j_rows = hit_pool.tile([P, 2, PAIR, width], F32, bufs=1 + whole, name="j_rows" + str(width))
+            g_hits = hit_pool.tile([P, 2, PAIR, width], BF16, bufs=1 + 2 * whole, name="g_hits" + str(width))
+            for dst, rows, first in ((j_rows, arg_rows, 0), (g_hits, g_rows, F)):
                 for a in range(2):
                     for sp in range(PAIR):
                         row0 = graph * NODES + sp * TARGETS
-                        col = col0 + a * F + h * HALF
+                        col = first + a * F + col0
                         nc.sync.dma_start(
                             out=dst[:, a, sp, :],
-                            in_=rows[row0 : row0 + TARGETS, col : col + HALF]
+                            in_=rows[row0 : row0 + TARGETS, col : col + width]
                             .unsqueeze(1)
-                            .to_broadcast([TARGETS, SPREAD, HALF]),
+                            .to_broadcast([TARGETS, SPREAD, width]),
                         )
-            hit_tables[h, graph] = (j_rows, g_hits)
+            for k, (group, of_graph) in enumerate(steps):
+                at = GROUPS[group][0] - col0
+                if of_graph == graph and 0 <= at < width:
+                    hit_tables[k] = (j_rows[:, :, :, at : at + GROUPS[group][1]], g_hits[:, :, :, at : at + GROUPS[group][1]])
 
         def load_edges(s):
             e_raw = e_pool.tile([P, PACK, C], BF16, name="e_raw")
@@ -114,10 +123,10 @@ def tile_gnnlayer_pa_v_kernel(tc, x, e_enc, W_pre, b_pre, m, stat, arg, grad_out
         rstd = load_table(stat_rows, F, F32, "rstd")
         mean = load_table(stat_rows, 0, F32, "mean")
         g_mean = load_table(g_rows, 0, BF16, "g_mean")
-        load_hit_tables(0, 0)
+        load_hit_tables(0, 0, WIDTHS[0])
         dm_of = {0: load_messages(*steps[0])}
         e_raw = {0: load_edges(0)}
-        load_hit_tables(0, 1)
+        load_hit_tables(1, 0, HALF)
         dm_of[1] = load_messages(*steps[1])
         e_raw[1] = load_edges(1)
         x_b = setup.tile([P, 2, C], BF16)
@@ -162,32 +171,38 @@ def tile_gnnlayer_pa_v_kernel(tc, x, e_enc, W_pre, b_pre, m, stat, arg, grad_out
             out=a_tab[:], in0=g_mean[:], scalar=1.0 / NODES, in1=mean[:], op0=ALU.mult, op1=ALU.subtract
         )
 
-        def turn_tables(pair, name):
-            turned_sb = keep.tile([P, BLKS, 2, P], F32, name=name)
-            for a, table in enumerate(pair):
-                turned = short_lived([P, BLKS, P], F32, "turned")
-                for fb in range(BLKS):
-                    nc.tensor.transpose(out=turned[:, fb, :], in_=table[:, fb * BLK : (fb + 1) * BLK], identity=ident_f[:])
-                nc.scalar.copy(out=turned_sb[:, :, a, :], in_=turned[:])
-            return turned_sb
+        ca_t = keep.tile([P, BLKS, 2, P], F32)
+        turned_ca = []
+
+        def turn_table(table):
+            turned = short_lived([P, BLKS, P], F32, "turned")
+            for fb in range(BLKS):
+                nc.tensor.transpose(out=turned[:, fb, :], in_=table[:, fb * BLK : (fb + 1) * BLK], identity=ident_f[:])
+            turned_ca.append(turned)
+
+        def take_turned(a, blks):
+            nc.scalar.copy(out=ca_t[:, blks, a, :], in_=turned_ca[a][:, blks, :])
 
         rep_of = {}
         spread_of = {}
         jj_of = {}
 
-        def repeat_rows(k):
+        def repeat_rows(k, tables=(0, 1)):
             group, graph = steps[k]
             fb0, blks = GROUPS[group][0] // BLK, GROUPS[group][1] // BLK
             h = fb0 // BLKS
-            rep_of[k] = rep_pool.tile([P, blks, 2, NODES, SPREAD], F32, name="ca_rep")
+            if tables[0] == 0:
+                rep_of[k] = rep_pool.tile([P, blks, 2, NODES, SPREAD], F32, name="ca_rep")
             rows = ca_t[:].rearrange("p f a (n h) -> p f a n h", h=HALVES)
-            rows = rows[:, fb0 % BLKS : fb0 % BLKS + blks, :, graph * NODES : (graph + 1) * NODES, h]
-            nc.scalar.copy(out=rep_of[k][:], in_=rows.unsqueeze(4).to_broadcast([P, blks, 2, NODES, SPREAD]))
+            some = slice(tables[0], tables[-1] + 1)
+            rows = rows[:, fb0 % BLKS : fb0 % BLKS + blks, some, graph * NODES : (graph + 1) * NODES, h]
+            nc.scalar.copy(
+                out=rep_of[k][:, :, some], in_=rows.unsqueeze(4).to_broadcast([P, blks, len(tables), NODES, SPREAD])
+            )
 
-        def spread_rows(k):
+        def spread_rows(k, tables=(0, 1)):
             width = GROUPS[steps[k][0]][1]
-            spread_of[k] = []
-            for a in range(2):
+            for a in tables:
                 spread = psum.tile([P, PAIR, width], F32, tag="ca"[a] + "_ps", bufs=2, name="ca"[a] + "_ps")
                 for sp in range(PAIR):
                     for fb in range(width // BLK):
@@ -196,14 +211,13 @@ def tile_gnnlayer_pa_v_kernel(tc, x, e_enc, W_pre, b_pre, m, stat, arg, grad_out
                             in_=rep_of[k][:, fb, a, sp * TARGETS : (sp + 1) * TARGETS, :].rearrange("p q r -> p (q r)"),
                             identity=ident_f[:],
                         )
-                spread_of[k].append(spread)
+                spread_of.setdefault(k, []).append(spread)
 
-        def round_j(k):
+        def round_j(k, engine_copy):
             group, graph = steps[k]
             col0, width = GROUPS[group]
             jj_of[k] = work.tile([P, 2, PAIR, width], BF16, name="jj")
-            col = col0 % HALF
-            nc.scalar.copy(out=jj_of[k][:], in_=hit_tables[col0 // HALF, graph][0][:, :, :, col : col + width])
+            engine_copy(out=jj_of[k][:], in_=hit_tables[k][0])
 
         hit_of = {}
 
@@ -218,13 +232,12 @@ def tile_gnnlayer_pa_v_kernel(tc, x, e_enc, W_pre, b_pre, m, stat, arg, grad_out
         def hits(k):
             group, graph = steps[k]
             col0, width = GROUPS[group]
-            col = col0 % HALF
-            g_hits = hit_tables[col0 // HALF, graph][1]
+            g_hits = hit_tables[k][1]
             for a in range(2):
                 nc.vector.tensor_tensor(
                     out=hit_of[k][:, a],
                     in0=hit_of[k][:, a],
-                    in1=g_hits[:, a, :, col : col + width].unsqueeze(2).to_broadcast([P, PAIR, PACK, width]),
+                    in1=g_hits[:, a].unsqueeze(2).to_broadcast([P, PAIR, PACK, width]),
                     op=ALU.mult,
                 )
 
@@ -261,11 +274,11 @@ def tile_gnnlayer_pa_v_kernel(tc, x, e_enc, W_pre, b_pre, m, stat, arg, grad_out
             s, c0 = unit // 2, unit % 2 * (C // 2)
             quantise(e_grp[unit][:], e_codes[:, s, c0 : c0 + C // 2], e_scales[:, s, c0 : c0 + C // 2], E4M3X4)
 
-        def regroup_gradient(k):
+        def regroup_gradient(k, engine_copy):
             width = GROUPS[steps[k][0]][1]
             d_grp[k] = work.tile([P, PAIR, width, PACK], BF16, align_bytes=64, name="d_grp")
             for sp in range(PAIR):
-                regroup(nc.scalar.copy, d_grp[k][:, sp], dm_of[k][:, sp])
+                regroup(engine_copy, d_grp[k][:, sp], dm_of[k][:, sp])
 
         def quantise_gradient(k):
             group, graph = steps[k]
@@ -283,6 +296,9 @@ def tile_gnnlayer_pa_v_kernel(tc, x, e_enc, W_pre, b_pre, m, stat, arg, grad_out
 
         def partial_sums(k):
             group, graph = steps[k]
+            if k in TURNED:
+                turned_sums(k)
+                return
             blks = GROUPS[group][1] // BLK
             if graph == 0:
                 sums_ps_of[group] = psum.tile([P, PASSES, blks, SUMS], F32, name="sums_ps")
@@ -297,13 +313,38 @@ def tile_gnnlayer_pa_v_kernel(tc, x, e_enc, W_pre, b_pre, m, stat, arg, grad_out
                             stop=(t == PACK - 1),
                         )
 
+        def turned_sums(k):
+            group, graph = steps[k]
+            for sp in range(PAIR):
+                s = graph * PAIR + sp
+                for fb in range(GROUPS[group][1] // BLK):
+                    turned = psum.tile([P, PACK, BLK], F32, tag="ca"[fb % 2] + "_ps", bufs=2, name="dm_turn")
+                    for t in range(PACK):
+                        nc.tensor.transpose(
+                            out=turned[:, t, :], in_=dm_of[k][:, sp, t, fb * BLK : (fb + 1) * BLK], identity=ident_f[:]
+                        )
+                    sums_t = sums_t_of[group % 2]
+                    nc.vector.tensor_reduce(
+                        out=sums_t[:, 0, fb, s * TARGETS : (s + 1) * TARGETS],
+                        in_=turned[:].rearrange("p t (q r) -> p q t r", r=SPREAD),
+                        axis=mybir.AxisListType.XY,
+                        op=ALU.add,
+                    )
+                    nc.vector.tensor_reduce(
+                        out=sums_t[:, 1, fb, s * NODES : (s + 1) * NODES].rearrange("p (r t) -> p r t", t=PACK),
+                        in_=turned[:].rearrange("p t (q r) -> p r t q", r=SPREAD),
+                        axis=mybir.AxisListType.X,
+                        op=ALU.add,
+                    )
+
         def take_sums(group, engine_copy):
             sums_ps, blks = sums_ps_of[group], GROUPS[group][1] // BLK
             sums_t = sums_t_of[group % 2][:, :, 0:blks, :]
+            done = PAIR * sum(1 for graph in range(GRAPHS) if group * GRAPHS + graph not in TURNED)
             engine_copy(
-                out=sums_t[:, 0, :, 0:ALL_NODES].rearrange("p f (s q) -> p s f q", q=TARGETS), in_=sums_ps[:, :, :, 0:TARGETS]
+                out=sums_t[:, 0, :, 0 : done * TARGETS].rearrange("p f (s q) -> p s f q", q=TARGETS), in_=sums_ps[:, 0:done, :, 0:TARGETS]
             )
-            engine_copy(out=sums_t[:, 1].rearrange("p f (s j) -> p s f j", j=NODES), in_=sums_ps[:, :, :, TARGETS:SUMS])
+            engine_copy(out=sums_t[:, 1, :, 0 : done * NODES].rearrange("p f (s j) -> p s f j", j=NODES), in_=sums_ps[:, 0:done, :, TARGETS:SUMS])
 
         def turn_sums(group, engine_copy):
             width = GROUPS[group][1]
@@ -359,11 +400,6 @@ def tile_gnnlayer_pa_v_kernel(tc, x, e_enc, W_pre, b_pre, m, stat, arg, grad_out
             store_edge_product(acc[:], 0, cb, nc.scalar.copy)
 
         pending = []
-        first_of_tables = {}
-        for k, (group, graph) in enumerate(steps):
-            key = (GROUPS[group][0] // HALF, graph)
-            if key[0] > 0 and key not in first_of_tables.values():
-                first_of_tables[k] = key
         last_of_half_0 = max(k for k in range(STEPS) if GROUPS[steps[k][0]][0] < HALF)
 
         side = [(unit, piece) for unit in range(2 * PASSES) for piece in range(E_PIECES)]
@@ -390,8 +426,8 @@ def tile_gnnlayer_pa_v_kernel(tc, x, e_enc, W_pre, b_pre, m, stat, arg, grad_out
                 dm_of[k + 2] = load_messages(*steps[k + 2])
             if 1 <= k < PASSES - 1:
                 e_raw[k + 1] = load_edges(k + 1)
-            if k + 3 in first_of_tables:
-                load_hit_tables(*first_of_tables[k + 3])
+            if k in (1, 2):
+                load_hit_tables(k - 1, HALF, HALF)
             c_row, a_row = spread_of[k]
             dm = dm_of[k]
             over_slots = [P, PACK, width]
@@ -401,21 +437,29 @@ def tile_gnnlayer_pa_v_kernel(tc, x, e_enc, W_pre, b_pre, m, stat, arg, grad_out
                         out=dm[:, sp], in0=dm[:, sp], in1=row[:, sp, :].unsqueeze(1).to_broadcast(over_slots), op=op
                     )
             complete = k >= 1 and steps[k - 1][1] == GRAPHS - 1
-            for unit in regrouped:
+            for unit in regrouped[0 : E_QUANT.get(k, 0)]:
                 quantise_edges(unit)
-            regrouped.clear()
-            if k + 1 < STEPS:
+                regrouped.remove(unit)
+            spread_late = complete and k in LATE_SPREAD
+            if k + 1 < STEPS and not spread_late:
                 spread_rows(k + 1)
+            if k + 1 == STEPS:
+                regroup_gradient(k - 1, nc.scalar.copy)
             outputs(N1[k])
             edge_pieces(E_FREE.get(k, 0))
             if k + 2 < STEPS:
                 repeat_rows(k + 2)
-                round_j(k + 2)
+                round_j(k + 2, nc.scalar.copy)
             if k >= 1:
-                regroup_gradient(k - 1)
-                partial_sums(k - 1)
-            if complete:
+                if k + 1 < STEPS:
+                    regroup_gradient(k - 1, nc.scalar.copy)
+                if k - 1 not in TURNED:
+                    partial_sums(k - 1)
+            if complete and k - 2 not in TURNED:
                 take_sums(steps[k - 1][0], nc.scalar.copy)
+            if k + 1 < STEPS and spread_late:
+                spread_rows(k + 1)
+            if complete and k - 1 not in TURNED:
                 turn_sums(steps[k - 1][0], nc.scalar.copy)
                 pending.extend([lambda cb=cb, g=steps[k - 1][0]: node_products(g, cb, nc.scalar.copy) for cb in range(C_BLKS)])
             outputs(N2[k] if k + 1 < STEPS else len(pending))
@@ -428,17 +472,34 @@ def tile_gnnlayer_pa_v_kernel(tc, x, e_enc, W_pre, b_pre, m, stat, arg, grad_out
             if k + 1 < STEPS:
                 hits(k + 1)
             nc.vector.tensor_tensor(out=dm[:], in0=dm[:], in1=hit_of[k][:, 0], op=ALU.add)
-            second_adder = nc.gpsimd if k + 1 < STEPS else nc.vector
-            second_adder.tensor_tensor(out=dm[:], in0=dm[:], in1=hit_of[k][:, 1], op=ALU.add)
+            if k + 1 == STEPS:
+                nc.vector.tensor_tensor(out=dm[:], in0=dm[:], in1=hit_of[k][:, 1], op=ALU.add)
+            else:
+                for engine, sp, slots in ADDS:
+                    of_engine = nc.vector if engine == "vector" else nc.gpsimd
+                    of_engine.tensor_tensor(
+                        out=dm[:, sp, slots], in0=dm[:, sp, slots], in1=hit_of[k][:, 1, sp, slots], op=ALU.add
+                    )
+            if k >= 1 and k + 1 < STEPS and k - 1 in TURNED:
+                partial_sums(k - 1)
+                if complete:
+                    turn_sums(steps[k - 1][0], nc.vector.tensor_copy)
+                    pending.extend([lambda cb=cb, g=steps[k - 1][0]: node_products(g, cb, nc.scalar.copy) for cb in range(C_BLKS)])
 
-        ca_t = turn_tables((c_tab, a_tab), "ca_t")
-        round_j(0)
-        repeat_rows(0)
-        spread_rows(0)
+        first_blks = slice(0, WIDTHS[0] // BLK)
+        for a, table in enumerate((c_tab, a_tab)):
+            turn_table(table)
+            take_turned(a, first_blks)
+            repeat_rows(0, (a,))
+            spread_rows(0, (a,))
+        round_j(0, nc.vector.tensor_copy)
         masks(0)
         hits(0)
+        load_hit_tables(0, WIDTHS[0], HALF - WIDTHS[0])
+        for a in range(2):
+            take_turned(a, slice(first_blks.stop, BLKS))
         repeat_rows(1)
-        round_j(1)
+        round_j(1, nc.scalar.copy)
 
         for k in range(STEPS):
             step(k)
@@ -446,27 +507,22 @@ def tile_gnnlayer_pa_v_kernel(tc, x, e_enc, W_pre, b_pre, m, stat, arg, grad_out
                 cast_x()
 
         last = STEPS - 1
-        regroup_gradient(last)
+        copies = (nc.scalar.copy, nc.vector.tensor_copy)
+        regroup_gradient(last, nc.vector.tensor_copy)
         quantise_gradient(last - 1)
-        accs = []
-        for cb in range(4):
-            acc = psum.tile([P, HALF], F32, tag="ca"[cb % 2] + "_ps", bufs=2, name="edge_acc")
-            accs.append(acc[:])
-            edge_passes(acc[:], 1, cb, range(PAIR))
-        partial_sums(last)
-        for make in pending:
-            make()
         quantise_gradient(last)
-        take_sums(len(GROUPS) - 1, nc.vector.tensor_copy)
+        turned_sums(last - 1)
+        def last_edges(cb, engine_copy):
+            acc = short_lived([P, HALF], F32, "acc")
+            edge_passes(acc[:], 1, cb, range(PASSES))
+            store_edge_product(acc[:], 1, cb, engine_copy)
+        for cb in range(TA):
+            last_edges(cb, copies[0])
+        turned_sums(last)
+        for cb in range(TA, TB):
+            last_edges(cb, copies[0])
+        turn_sums(len(GROUPS) - 1, nc.vector.tensor_copy)
+        for cb in range(TB, C_BLKS):
+            last_edges(cb, copies[cb % 2])
         for cb in range(C_BLKS):
-            if cb < len(accs):
-                edge_passes(accs[cb], 1, cb, range(PAIR, PASSES))
-            else:
-                acc = short_lived([P, HALF], F32, "acc")
-                accs.append(acc[:])
-                edge_passes(acc[:], 1, cb, range(PASSES))
-            store_edge_product(accs[cb], 1, cb, nc.scalar.copy if cb % 2 else nc.vector.tensor_copy)
-            if cb == 1:
-                turn_sums(len(GROUPS) - 1, nc.vector.tensor_copy)
-        for cb in range(C_BLKS):
-            node_products(len(GROUPS) - 1, cb, nc.scalar.copy if cb % 2 else nc.vector.tensor_copy)
+            node_products(len(GROUPS) - 1, cb, copies[cb % 2])

@@ -32,15 +32,14 @@ BLKS = HALF // BLK
 C_BLKS = C // BLK
 SUMS = TARGETS + NODES
 STEPS = len(GROUPS) * GRAPHS
-N1 = [3 * GROUPS[k // GRAPHS][1] // BLK for k in range(STEPS)]
-N2 = [1 * GROUPS[k // GRAPHS][1] // BLK for k in range(STEPS)]
+OUTPUTS = {2: (0, 0, 2), 3: (4, 0, 0), 4: (0, 2, 2), 5: (6, 0, 0), 6: (0, 6, 2), 7: (8, 0, 8)}
+XCAST = 1
 E_PIECES = 4
-E_QUANT = {3: 1, 4: 4, 5: 3}
 LATE_SPREAD = (2, 4)
-ADDS = (("vector", 1, slice(3, PACK)), ("gpsimd", 0, slice(0, PACK)), ("gpsimd", 1, slice(0, 3)))
 TURNED = (6, 7)
 TA, TB = 4, 8
-E_FREE = {k: 8 for k in range(5)}
+E1 = {0: 4, 1: 4, 2: 2, 4: 2}
+E2 = {2: 2, 4: 2}
 SHORT_LIVED_BANKS = 3
 
 FLOPS = 2 * EDGES * C * F + 2 * 2 * ALL_NODES * C * F
@@ -63,7 +62,7 @@ def tile_gnnlayer_pa_v_kernel(tc, x, e_enc, W_pre, b_pre, m, stat, arg, grad_out
         keep = ctx.enter_context(tc.tile_pool(name="keep", bufs=1))
         setup = ctx.enter_context(tc.tile_pool(name="setup", bufs=1))
         e_pool = ctx.enter_context(tc.tile_pool(name="e_pool", bufs=2))
-        e_grp_pool = ctx.enter_context(tc.tile_pool(name="e_grp_pool", bufs=7))
+        e_grp_pool = ctx.enter_context(tc.tile_pool(name="e_grp_pool", bufs=6))
         rep_pool = ctx.enter_context(tc.tile_pool(name="rep_pool", bufs=2))
         m_pool = ctx.enter_context(tc.tile_pool(name="m_pool", bufs=4))
         hit_pool = ctx.enter_context(tc.tile_pool(name="hit_pool", bufs=2))
@@ -128,15 +127,6 @@ def tile_gnnlayer_pa_v_kernel(tc, x, e_enc, W_pre, b_pre, m, stat, arg, grad_out
         e_raw = {0: load_edges(0)}
         load_hit_tables(1, 0, HALF)
         dm_of[1] = load_messages(*steps[1])
-        e_raw[1] = load_edges(1)
-        x_b = setup.tile([P, 2, C], BF16)
-        nc.sync.dma_start(out=x_b[0:ALL_NODES, 0, :], in_=x_rows)
-        for s in range(PASSES):
-            graph = s // PAIR
-            nc.sync.dma_start(
-                out=x_b[s * NODES : (s + 1) * NODES, 1, :], in_=x_rows[graph * NODES : (graph + 1) * NODES, :]
-            )
-
         ident_f = const.tile([P, P], F32)
         make_identity(nc, ident_f[:])
         edge_i = const.tile([P, PACK], I32)
@@ -244,11 +234,8 @@ def tile_gnnlayer_pa_v_kernel(tc, x, e_enc, W_pre, b_pre, m, stat, arg, grad_out
         x_f = keep.tile([P, 2, C], F32)
 
         def cast_x():
-            nc.gpsimd.memset(x_f[ALL_NODES:P, 0, :], 0.0)
-            nc.gpsimd.tensor_scalar(
-                out=x_f[0:ALL_NODES, 0, :], in0=x_b[0:ALL_NODES, 0, :], scalar1=1.0, scalar2=0.0, op0=ALU.mult, op1=ALU.add
-            )
-            nc.gpsimd.tensor_scalar(out=x_f[:, 1, :], in0=x_b[:, 1, :], scalar1=1.0, scalar2=0.0, op0=ALU.mult, op1=ALU.add)
+            nc.scalar.copy(out=x_f[0:ALL_NODES, 0, :], in_=x_b[0:ALL_NODES, 0, :])
+            nc.scalar.copy(out=x_f[:, 1, :], in_=x_b[:, 1, :])
 
         e_codes = keep.tile([P, PASSES, C], U32, align_bytes=64)
         e_scales = keep.tile([P, PASSES, C], U8, align_bytes=64)
@@ -293,6 +280,7 @@ def tile_gnnlayer_pa_v_kernel(tc, x, e_enc, W_pre, b_pre, m, stat, arg, grad_out
         sums_t_of = [keep.tile([P, 2, WIDE // BLK, P], F32, name="sums_t" + str(i)) for i in range(2)]
         for sums_t in sums_t_of:
             nc.gpsimd.memset(sums_t[:, 0], 0.0)
+        nc.gpsimd.memset(x_f[ALL_NODES:P, 0, :], 0.0)
 
         def partial_sums(k):
             group, graph = steps[k]
@@ -424,8 +412,9 @@ def tile_gnnlayer_pa_v_kernel(tc, x, e_enc, W_pre, b_pre, m, stat, arg, grad_out
             col0, width = GROUPS[group]
             if k + 2 < STEPS:
                 dm_of[k + 2] = load_messages(*steps[k + 2])
-            if 1 <= k < PASSES - 1:
-                e_raw[k + 1] = load_edges(k + 1)
+            loaded = len(e_raw)
+            if k >= 1 and loaded < PASSES and not any(unit // 2 <= loaded - 2 for unit, piece in side):
+                e_raw[loaded] = load_edges(loaded)
             if k in (1, 2):
                 load_hit_tables(k - 1, HALF, HALF)
             c_row, a_row = spread_of[k]
@@ -437,19 +426,21 @@ def tile_gnnlayer_pa_v_kernel(tc, x, e_enc, W_pre, b_pre, m, stat, arg, grad_out
                         out=dm[:, sp], in0=dm[:, sp], in1=row[:, sp, :].unsqueeze(1).to_broadcast(over_slots), op=op
                     )
             complete = k >= 1 and steps[k - 1][1] == GRAPHS - 1
-            for unit in regrouped[0 : E_QUANT.get(k, 0)]:
-                quantise_edges(unit)
-                regrouped.remove(unit)
+            if k > last_of_half_0:
+                for unit in regrouped:
+                    quantise_edges(unit)
+                regrouped.clear()
             spread_late = complete and k in LATE_SPREAD
             if k + 1 < STEPS and not spread_late:
                 spread_rows(k + 1)
             if k + 1 == STEPS:
                 regroup_gradient(k - 1, nc.scalar.copy)
-            outputs(N1[k])
-            edge_pieces(E_FREE.get(k, 0))
+            at_start, in_gap, at_end = OUTPUTS.get(k, (0, 0, 0))
+            outputs(at_start)
             if k + 2 < STEPS:
                 repeat_rows(k + 2)
                 round_j(k + 2, nc.scalar.copy)
+            edge_pieces(E1.get(k, 0))
             if k >= 1:
                 if k + 1 < STEPS:
                     regroup_gradient(k - 1, nc.scalar.copy)
@@ -459,27 +450,34 @@ def tile_gnnlayer_pa_v_kernel(tc, x, e_enc, W_pre, b_pre, m, stat, arg, grad_out
                 take_sums(steps[k - 1][0], nc.scalar.copy)
             if k + 1 < STEPS and spread_late:
                 spread_rows(k + 1)
+            if k == XCAST:
+                cast_x()
+            outputs(in_gap)
             if complete and k - 1 not in TURNED:
                 turn_sums(steps[k - 1][0], nc.scalar.copy)
                 pending.extend([lambda cb=cb, g=steps[k - 1][0]: node_products(g, cb, nc.scalar.copy) for cb in range(C_BLKS)])
-            outputs(N2[k] if k + 1 < STEPS else len(pending))
+            edge_pieces(E2.get(k, 0))
+            outputs(at_end)
             if k + 1 < STEPS:
                 masks(k + 1)
-            for old in [k - 2] * (k - 2 >= 0 and k - 2 != last_of_half_0) + [k - 1] * (k - 1 == last_of_half_0):
-                quantise_gradient(old)
-                if old == last_of_half_0:
+            if k >= 2:
+                quantise_gradient(k - 2)
+                if k - 2 == last_of_half_0:
                     pending.extend([lambda cb=cb: first_half_edges(cb) for cb in range(C_BLKS)])
+            def add_hits(engine, which, part):
+                engine.tensor_tensor(out=dm[part], in0=dm[part], in1=hit_of[k][:, which][part], op=ALU.add)
+
+            everywhere = slice(0, P)
             if k + 1 < STEPS:
+                add_hits(nc.vector, 1, (everywhere, 1, slice(3, PACK)))
                 hits(k + 1)
-            nc.vector.tensor_tensor(out=dm[:], in0=dm[:], in1=hit_of[k][:, 0], op=ALU.add)
-            if k + 1 == STEPS:
-                nc.vector.tensor_tensor(out=dm[:], in0=dm[:], in1=hit_of[k][:, 1], op=ALU.add)
+                add_hits(nc.vector, 0, (everywhere, slice(0, PAIR)))
+                add_hits(nc.gpsimd, 1, (everywhere, 0))
+                add_hits(nc.gpsimd, 1, (everywhere, 1, slice(0, 3)))
             else:
-                for engine, sp, slots in ADDS:
-                    of_engine = nc.vector if engine == "vector" else nc.gpsimd
-                    of_engine.tensor_tensor(
-                        out=dm[:, sp, slots], in0=dm[:, sp, slots], in1=hit_of[k][:, 1, sp, slots], op=ALU.add
-                    )
+                for which in range(2):
+                    for sp in range(PAIR):
+                        add_hits(nc.vector, which, (everywhere, sp))
             if k >= 1 and k + 1 < STEPS and k - 1 in TURNED:
                 partial_sums(k - 1)
                 if complete:
@@ -496,6 +494,14 @@ def tile_gnnlayer_pa_v_kernel(tc, x, e_enc, W_pre, b_pre, m, stat, arg, grad_out
         masks(0)
         hits(0)
         load_hit_tables(0, WIDTHS[0], HALF - WIDTHS[0])
+        e_raw[1] = load_edges(1)
+        x_b = setup.tile([P, 2, C], BF16)
+        nc.sync.dma_start(out=x_b[0:ALL_NODES, 0, :], in_=x_rows)
+        for s in range(PASSES):
+            graph = s // PAIR
+            nc.sync.dma_start(
+                out=x_b[s * NODES : (s + 1) * NODES, 1, :], in_=x_rows[graph * NODES : (graph + 1) * NODES, :]
+            )
         for a in range(2):
             take_turned(a, slice(first_blks.stop, BLKS))
         repeat_rows(1)
@@ -503,8 +509,6 @@ def tile_gnnlayer_pa_v_kernel(tc, x, e_enc, W_pre, b_pre, m, stat, arg, grad_out
 
         for k in range(STEPS):
             step(k)
-            if k == 0:
-                cast_x()
 
         last = STEPS - 1
         copies = (nc.scalar.copy, nc.vector.tensor_copy)

@@ -32,12 +32,13 @@ BLKS = HALF // BLK
 C_BLKS = C // BLK
 SUMS = TARGETS + NODES
 STEPS = len(GROUPS) * GRAPHS
-OUTPUTS = {2: (0, 0, 2), 3: (4, 0, 0), 4: (0, 2, 2), 5: (6, 0, 0), 6: (0, 6, 2), 7: (8, 0, 8)}
+OUTPUTS = {2: (0, 0, 2), 3: (4, 0, 2), 4: (0, 0, 5), 5: (7, 0, 0), 6: (0, 2, 4), 7: (8, 0, 8)}
 XCAST = 1
+LAG = 1
+CUT = 7
 E_PIECES = 4
-LATE_SPREAD = (2, 4)
 TURNED = (6, 7)
-TA, TB = 4, 8
+TA, TB = 3, 7
 E1 = {0: 4, 1: 4, 2: 2, 4: 2}
 E2 = {2: 2, 4: 2}
 SHORT_LIVED_BANKS = 3
@@ -61,8 +62,8 @@ def tile_gnnlayer_pa_v_kernel(tc, x, e_enc, W_pre, b_pre, m, stat, arg, grad_out
         const = ctx.enter_context(tc.tile_pool(name="const", bufs=1))
         keep = ctx.enter_context(tc.tile_pool(name="keep", bufs=1))
         setup = ctx.enter_context(tc.tile_pool(name="setup", bufs=1))
-        e_pool = ctx.enter_context(tc.tile_pool(name="e_pool", bufs=2))
-        e_grp_pool = ctx.enter_context(tc.tile_pool(name="e_grp_pool", bufs=6))
+        e_pool = ctx.enter_context(tc.tile_pool(name="e_pool", bufs=4))
+        e_grp_pool = ctx.enter_context(tc.tile_pool(name="e_grp_pool", bufs=5))
         rep_pool = ctx.enter_context(tc.tile_pool(name="rep_pool", bufs=2))
         m_pool = ctx.enter_context(tc.tile_pool(name="m_pool", bufs=4))
         hit_pool = ctx.enter_context(tc.tile_pool(name="hit_pool", bufs=2))
@@ -100,11 +101,11 @@ def tile_gnnlayer_pa_v_kernel(tc, x, e_enc, W_pre, b_pre, m, stat, arg, grad_out
                 if of_graph == graph and 0 <= at < width:
                     hit_tables[k] = (j_rows[:, :, :, at : at + GROUPS[group][1]], g_hits[:, :, :, at : at + GROUPS[group][1]])
 
-        def load_edges(s):
-            e_raw = e_pool.tile([P, PACK, C], BF16, name="e_raw")
-            nc.sync.dma_start(
-                out=e_raw[:], in_=e_rows[s * K_PASS : (s + 1) * K_PASS, :].rearrange("(p t) c -> p t c", t=PACK)
-            )
+        def load_edges(unit):
+            h, s = unit // PASSES, unit % PASSES
+            e_raw = e_pool.tile([P, PACK, HALF], BF16, name="e_raw")
+            rows = e_rows[s * K_PASS : (s + 1) * K_PASS, h * HALF : (h + 1) * HALF]
+            nc.sync.dma_start(out=e_raw[:], in_=rows.rearrange("(p t) c -> p t c", t=PACK))
             return e_raw
 
         def load_messages(group, graph):
@@ -124,7 +125,7 @@ def tile_gnnlayer_pa_v_kernel(tc, x, e_enc, W_pre, b_pre, m, stat, arg, grad_out
         g_mean = load_table(g_rows, 0, BF16, "g_mean")
         load_hit_tables(0, 0, WIDTHS[0])
         dm_of = {0: load_messages(*steps[0])}
-        e_raw = {0: load_edges(0)}
+        e_raw = {unit: load_edges(unit) for unit in range(2)}
         load_hit_tables(1, 0, HALF)
         dm_of[1] = load_messages(*steps[1])
         ident_f = const.tile([P, P], F32)
@@ -231,6 +232,18 @@ def tile_gnnlayer_pa_v_kernel(tc, x, e_enc, W_pre, b_pre, m, stat, arg, grad_out
                     op=ALU.mult,
                 )
 
+        both_hits_of = {}
+
+        def add_hits(k, engine):
+            width = GROUPS[steps[k][0]][1]
+            slots = slice(0, CUT) if engine is nc.gpsimd else slice(CUT, PAIR * PACK)
+            both = work.tile(
+                [P, slots.stop - slots.start, width], F32, bufs=1 if engine is nc.gpsimd else 2, name="both" + str(slots.start)
+            )
+            hit = [hit_of[k][:, a].rearrange("p s t f -> p (s t) f")[:, slots] for a in range(2)]
+            engine.tensor_tensor(out=both[:], in0=hit[0], in1=hit[1], op=ALU.add)
+            both_hits_of.setdefault(k, []).append((slots, both))
+
         x_f = keep.tile([P, 2, C], F32)
 
         def cast_x():
@@ -251,15 +264,15 @@ def tile_gnnlayer_pa_v_kernel(tc, x, e_enc, W_pre, b_pre, m, stat, arg, grad_out
             nc.vector.quantize_mx(out=codes.bitcast(fmt), scales=scales, in_=grouped.rearrange("p c t -> p (c t)"))
 
         def regroup_edges(unit, piece, engine_copy):
-            s, c0, cols = unit // 2, unit % 2 * (C // 2), C // 2 // E_PIECES
             if piece == 0:
-                e_grp[unit] = e_grp_pool.tile([P, C // 2, PACK], BF16, align_bytes=64, name="e_grp")
-            at = piece * cols
-            regroup(engine_copy, e_grp[unit][:, at : at + cols, :], e_raw[s][:, :, c0 + at : c0 + at + cols])
+                e_grp[unit] = e_grp_pool.tile([P, HALF, PACK], BF16, align_bytes=64, name="e_grp")
+            cols = slice(piece * HALF // E_PIECES, (piece + 1) * HALF // E_PIECES)
+            regroup(engine_copy, e_grp[unit][:, cols, :], e_raw[unit][:, :, cols])
 
         def quantise_edges(unit):
-            s, c0 = unit // 2, unit % 2 * (C // 2)
-            quantise(e_grp[unit][:], e_codes[:, s, c0 : c0 + C // 2], e_scales[:, s, c0 : c0 + C // 2], E4M3X4)
+            h, s = unit // PASSES, unit % PASSES
+            cols = slice(h * HALF, (h + 1) * HALF)
+            quantise(e_grp[unit][:], e_codes[:, s, cols], e_scales[:, s, cols], E4M3X4)
 
         def regroup_gradient(k, engine_copy):
             width = GROUPS[steps[k][0]][1]
@@ -267,13 +280,12 @@ def tile_gnnlayer_pa_v_kernel(tc, x, e_enc, W_pre, b_pre, m, stat, arg, grad_out
             for sp in range(PAIR):
                 regroup(engine_copy, d_grp[k][:, sp], dm_of[k][:, sp])
 
-        def quantise_gradient(k):
+        def quantise_gradient(k, sp):
             group, graph = steps[k]
             col0, width = GROUPS[group]
             h, col = col0 // HALF, col0 % HALF
-            for sp in range(PAIR):
-                s = graph * PAIR + sp
-                quantise(d_grp[k][:, sp], d_codes[h][:, s, col : col + width], d_scales[h][:, s, col : col + width], E5M2X4)
+            s = graph * PAIR + sp
+            quantise(d_grp[k][:, sp], d_codes[h][:, s, col : col + width], d_scales[h][:, s, col : col + width], E5M2X4)
 
         sums_ps_of = {}
         sums_of = {}
@@ -382,7 +394,6 @@ def tile_gnnlayer_pa_v_kernel(tc, x, e_enc, W_pre, b_pre, m, stat, arg, grad_out
             nc.sync.dma_start(out=out[row0 : row0 + BLK, h * HALF : (h + 1) * HALF], in_=result[:])
 
         def first_half_edges(cb):
-            assert not side and not regrouped
             acc = short_lived([P, HALF], F32, "acc")
             edge_passes(acc[:], 0, cb, range(PASSES))
             store_edge_product(acc[:], 0, cb, nc.scalar.copy)
@@ -392,10 +403,12 @@ def tile_gnnlayer_pa_v_kernel(tc, x, e_enc, W_pre, b_pre, m, stat, arg, grad_out
 
         side = [(unit, piece) for unit in range(2 * PASSES) for piece in range(E_PIECES)]
         regrouped = []
+        quantised = {"edges": 0, "gradients": 0}
+        half_0 = list(range(C_BLKS))
 
         def edge_pieces(count):
             for unit, piece in side[0:count]:
-                if unit // 2 in e_raw:
+                if unit in e_raw:
                     regroup_edges(unit, piece, nc.scalar.copy)
                     side.remove((unit, piece))
                     if piece + 1 == E_PIECES:
@@ -407,14 +420,18 @@ def tile_gnnlayer_pa_v_kernel(tc, x, e_enc, W_pre, b_pre, m, stat, arg, grad_out
                 edge_pieces(1)
             pending[0:count] = []
 
+        def more_half_0():
+            while half_0 and quantised["gradients"] > last_of_half_0 and quantised["edges"] >= PASSES * (half_0[0] * BLK // HALF + 1):
+                pending.append(lambda cb=half_0.pop(0): first_half_edges(cb))
+
         def step(k):
             group, graph = steps[k]
             col0, width = GROUPS[group]
             if k + 2 < STEPS:
                 dm_of[k + 2] = load_messages(*steps[k + 2])
-            loaded = len(e_raw)
-            if k >= 1 and loaded < PASSES and not any(unit // 2 <= loaded - 2 for unit, piece in side):
-                e_raw[loaded] = load_edges(loaded)
+            for unit in range(len(e_raw), 2 * PASSES):
+                if not any(earlier == unit - 4 for earlier, piece in side):
+                    e_raw[unit] = load_edges(unit)
             if k in (1, 2):
                 load_hit_tables(k - 1, HALF, HALF)
             c_row, a_row = spread_of[k]
@@ -429,55 +446,51 @@ def tile_gnnlayer_pa_v_kernel(tc, x, e_enc, W_pre, b_pre, m, stat, arg, grad_out
             if k > last_of_half_0:
                 for unit in regrouped:
                     quantise_edges(unit)
+                quantised["edges"] += len(regrouped)
                 regrouped.clear()
-            spread_late = complete and k in LATE_SPREAD
-            if k + 1 < STEPS and not spread_late:
-                spread_rows(k + 1)
-            if k + 1 == STEPS:
-                regroup_gradient(k - 1, nc.scalar.copy)
+                more_half_0()
             at_start, in_gap, at_end = OUTPUTS.get(k, (0, 0, 0))
-            outputs(at_start)
-            if k + 2 < STEPS:
-                repeat_rows(k + 2)
-                round_j(k + 2, nc.scalar.copy)
-            edge_pieces(E1.get(k, 0))
             if k >= 1:
-                if k + 1 < STEPS:
-                    regroup_gradient(k - 1, nc.scalar.copy)
+                regroup_gradient(k - 1, nc.scalar.copy)
                 if k - 1 not in TURNED:
                     partial_sums(k - 1)
+            if k + 2 < STEPS and not complete:
+                repeat_rows(k + 2)
+                round_j(k + 2, nc.scalar.copy)
             if complete and k - 2 not in TURNED:
                 take_sums(steps[k - 1][0], nc.scalar.copy)
-            if k + 1 < STEPS and spread_late:
+            if k + 1 < STEPS:
                 spread_rows(k + 1)
+            edge_pieces(E1.get(k, 0))
+            outputs(at_start)
             if k == XCAST:
                 cast_x()
             outputs(in_gap)
             if complete and k - 1 not in TURNED:
                 turn_sums(steps[k - 1][0], nc.scalar.copy)
                 pending.extend([lambda cb=cb, g=steps[k - 1][0]: node_products(g, cb, nc.scalar.copy) for cb in range(C_BLKS)])
+            if k + 2 < STEPS and complete:
+                repeat_rows(k + 2)
+                round_j(k + 2, nc.scalar.copy)
             edge_pieces(E2.get(k, 0))
             outputs(at_end)
             if k + 1 < STEPS:
                 masks(k + 1)
-            if k >= 2:
-                quantise_gradient(k - 2)
-                if k - 2 == last_of_half_0:
-                    pending.extend([lambda cb=cb: first_half_edges(cb) for cb in range(C_BLKS)])
-            def add_hits(engine, which, part):
-                engine.tensor_tensor(out=dm[part], in0=dm[part], in1=hit_of[k][:, which][part], op=ALU.add)
-
-            everywhere = slice(0, P)
+            if k >= LAG:
+                quantise_gradient(k - LAG, 0)
             if k + 1 < STEPS:
-                add_hits(nc.vector, 1, (everywhere, 1, slice(3, PACK)))
                 hits(k + 1)
-                add_hits(nc.vector, 0, (everywhere, slice(0, PAIR)))
-                add_hits(nc.gpsimd, 1, (everywhere, 0))
-                add_hits(nc.gpsimd, 1, (everywhere, 1, slice(0, 3)))
-            else:
-                for which in range(2):
-                    for sp in range(PAIR):
-                        add_hits(nc.vector, which, (everywhere, sp))
+            if k >= LAG:
+                quantise_gradient(k - LAG, 1)
+                quantised["gradients"] += 1
+                more_half_0()
+            if k + 1 < STEPS:
+                add_hits(k + 1, nc.vector)
+            flat = dm[:].rearrange("p s t f -> p (s t) f")
+            for slots, both in both_hits_of[k]:
+                nc.vector.tensor_tensor(out=flat[:, slots], in0=flat[:, slots], in1=both[:], op=ALU.add)
+            if k + 1 < STEPS:
+                add_hits(k + 1, nc.gpsimd)
             if k >= 1 and k + 1 < STEPS and k - 1 in TURNED:
                 partial_sums(k - 1)
                 if complete:
@@ -493,8 +506,11 @@ def tile_gnnlayer_pa_v_kernel(tc, x, e_enc, W_pre, b_pre, m, stat, arg, grad_out
         round_j(0, nc.vector.tensor_copy)
         masks(0)
         hits(0)
+        add_hits(0, nc.gpsimd)
+        add_hits(0, nc.vector)
         load_hit_tables(0, WIDTHS[0], HALF - WIDTHS[0])
-        e_raw[1] = load_edges(1)
+        e_raw[2] = load_edges(2)
+        e_raw[3] = load_edges(3)
         x_b = setup.tile([P, 2, C], BF16)
         nc.sync.dma_start(out=x_b[0:ALL_NODES, 0, :], in_=x_rows)
         for s in range(PASSES):
@@ -513,8 +529,9 @@ def tile_gnnlayer_pa_v_kernel(tc, x, e_enc, W_pre, b_pre, m, stat, arg, grad_out
         last = STEPS - 1
         copies = (nc.scalar.copy, nc.vector.tensor_copy)
         regroup_gradient(last, nc.vector.tensor_copy)
-        quantise_gradient(last - 1)
-        quantise_gradient(last)
+        for old in range(last - LAG + 1, last + 1):
+            for sp in range(PAIR):
+                quantise_gradient(old, sp)
         turned_sums(last - 1)
         def last_edges(cb, engine_copy):
             acc = short_lived([P, HALF], F32, "acc")

from contextlib import ExitStack

import concourse.mybir as mybir
from concourse.masks import make_identity

F32 = mybir.dt.float32
BF16 = mybir.dt.bfloat16
I32 = mybir.dt.int32
U32 = mybir.dt.uint32
U8 = mybir.dt.uint8
E4M3X4 = mybir.dt.float8_e4m3fn_x4
E5M2X4 = mybir.dt.float8_e5m2_x4
ALU = mybir.AluOpType

P = 128
PACK = 4
K_PASS = P * PACK
GRAPHS, NODES, C, F = 2, 32, 1024, 1024
ALL_NODES = GRAPHS * NODES
EDGES = ALL_NODES * NODES
PASSES = EDGES // K_PASS
PAIR = PASSES // GRAPHS
TARGETS = K_PASS // NODES
SPREAD = P // TARGETS
HALF = 512
HALVES = F // HALF
WIDTHS = (256, 256, 256, 256)
WIDE = max(WIDTHS)
GROUPS = [(sum(WIDTHS[:i]), w) for i, w in enumerate(WIDTHS)]
BLK = 128
BLKS = HALF // BLK
C_BLKS = C // BLK
SUMS = TARGETS + NODES
STEPS = len(GROUPS) * GRAPHS
OUTPUTS = {2: (0, 0, 2), 3: (4, 0, 2), 4: (0, 0, 5), 5: (7, 0, 0), 6: (0, 2, 4), 7: (8, 0, 8)}
XCAST = 1
LAG = 1
CUT = 7
E_PIECES = 4
TURNED = (6, 7)
TA, TB = 3, 7
E1 = {0: 4, 1: 4, 2: 2, 4: 2}
E2 = {2: 2, 4: 2}
SHORT_LIVED_BANKS = 3

FLOPS = 2 * EDGES * C * F + 2 * 2 * ALL_NODES * C * F
BYTES = 2 * (ALL_NODES * C + EDGES * C + ALL_NODES * 4 * F) + 4 * (EDGES * F + 2 * ALL_NODES * 2 * F + 3 * C * F)


def tile_gnnlayer_pa_v_kernel(tc, x, e_enc, W_pre, b_pre, m, stat, arg, grad_out, out):
    nc = tc.nc
    x_rows = x.rearrange("b n c -> (b n) c")
    e_rows = e_enc.rearrange("b i j c -> (b i j) c")
    m_rows = m.rearrange("b i j f -> (b i j) f")
    stat_rows = stat.rearrange("b n s -> (b n) s")
    arg_rows = arg.rearrange("b n s -> (b n) s")
    g_rows = grad_out.rearrange("b n g -> (b n) g")
    steps = [(group, graph) for group in range(len(GROUPS)) for graph in range(GRAPHS)]

    with ExitStack() as ctx:
        ctx.enter_context(tc.manual_schedule())
        const = ctx.enter_context(tc.tile_pool(name="const", bufs=1))
        keep = ctx.enter_context(tc.tile_pool(name="keep", bufs=1))
        setup = ctx.enter_context(tc.tile_pool(name="setup", bufs=1))
        e_pool = ctx.enter_context(tc.tile_pool(name="e_pool", bufs=4))
        e_grp_pool = ctx.enter_context(tc.tile_pool(name="e_grp_pool", bufs=5))
        rep_pool = ctx.enter_context(tc.tile_pool(name="rep_pool", bufs=2))
        m_pool = ctx.enter_context(tc.tile_pool(name="m_pool", bufs=4))
        hit_pool = ctx.enter_context(tc.tile_pool(name="hit_pool", bufs=2))
        work = ctx.enter_context(tc.tile_pool(name="work", bufs=2))
        o_pool = ctx.enter_context(tc.tile_pool(name="o_pool", bufs=5))
        psum = ctx.enter_context(tc.psum_pool(name="psum", bufs=1))

        def short_lived(shape, dtype, name):
            return psum.tile(shape, dtype, tag="acc", bufs=SHORT_LIVED_BANKS, name=name)

        def load_table(rows, col0, dtype, name):
            table = setup.tile([P, HALF], dtype, name=name)
            nc.sync.dma_start(out=table[:], in_=rows[:, col0 : col0 + F].rearrange("n (h f) -> n h f", h=HALVES))
            return table

        hit_tables = {}

        def load_hit_tables(graph, col0, width):
            whole = width == HALF
            j_rows = hit_pool.tile([P, 2, PAIR, width], F32, bufs=1 + whole, name="j_rows" + str(width))
            g_hits = hit_pool.tile([P, 2, PAIR, width], BF16, bufs=1 + 2 * whole, name="g_hits" + str(width))
            for dst, rows, first in ((j_rows, arg_rows, 0), (g_hits, g_rows, F)):
                for a in range(2):
                    for sp in range(PAIR):
                        row0 = graph * NODES + sp * TARGETS
                        col = first + a * F + col0
                        nc.sync.dma_start(
                            out=dst[:, a, sp, :],
                            in_=rows[row0 : row0 + TARGETS, col : col + width]
                            .unsqueeze(1)
                            .to_broadcast([TARGETS, SPREAD, width]),
                        )
            for k, (group, of_graph) in enumerate(steps):
                at = GROUPS[group][0] - col0
                if of_graph == graph and 0 <= at < width:
                    hit_tables[k] = (j_rows[:, :, :, at : at + GROUPS[group][1]], g_hits[:, :, :, at : at + GROUPS[group][1]])

        def load_edges(unit):
            h, s = unit // PASSES, unit % PASSES
            e_raw = e_pool.tile([P, PACK, HALF], BF16, name="e_raw")
            rows = e_rows[s * K_PASS : (s + 1) * K_PASS, h * HALF : (h + 1) * HALF]
            nc.sync.dma_start(out=e_raw[:], in_=rows.rearrange("(p t) c -> p t c", t=PACK))
            return e_raw

        def load_messages(group, graph):
            col0, width = GROUPS[group]
            dm = m_pool.tile([P, PAIR, PACK, width], F32, name="dm")
            for sp in range(PAIR):
                row0 = (graph * PAIR + sp) * K_PASS
                nc.sync.dma_start(
                    out=dm[:, sp],
                    in_=m_rows[row0 : row0 + K_PASS, col0 : col0 + width].rearrange("(p t) f -> p t f", t=PACK),
                )
            return dm

        g_std = load_table(g_rows, 3 * F, BF16, "g_std")
        rstd = load_table(stat_rows, F, F32, "rstd")
        mean = load_table(stat_rows, 0, F32, "mean")
        g_mean = load_table(g_rows, 0, BF16, "g_mean")
        load_hit_tables(0, 0, WIDTHS[0])
        dm_of = {0: load_messages(*steps[0])}
        e_raw = {unit: load_edges(unit) for unit in range(2)}
        load_hit_tables(1, 0, HALF)
        dm_of[1] = load_messages(*steps[1])
        ident_f = const.tile([P, P], F32)
        make_identity(nc, ident_f[:])
        edge_i = const.tile([P, PACK], I32)
        nc.gpsimd.iota(edge_i[:], pattern=[[1, PACK]], base=0, channel_multiplier=PACK)
        col_i = const.tile([P, NODES], I32)
        nc.gpsimd.iota(col_i[:], pattern=[[1, NODES]], base=0, channel_multiplier=0)
        src_i = const.tile([P, PACK], I32)
        nc.vector.tensor_single_scalar(out=src_i[:], in_=edge_i[:], scalar=NODES - 1, op=ALU.bitwise_and)
        src_f = const.tile([P, PACK], F32)
        nc.vector.tensor_copy(out=src_f[:], in_=src_i[:])
        tgt_i = const.tile([P, 1], I32)
        nc.vector.tensor_single_scalar(out=tgt_i[:], in_=edge_i[:, 0:1], scalar=5, op=ALU.logical_shift_right)
        tgt_f = const.tile([P, 1], F32)
        nc.vector.tensor_copy(out=tgt_f[:], in_=tgt_i[:])
        col_f = const.tile([P, NODES], F32)
        nc.vector.tensor_copy(out=col_f[:], in_=col_i[:])
        pick = const.tile([P, PACK, SUMS], F32)
        for t in range(PACK):
            nc.vector.tensor_scalar(
                out=pick[:, t, 0:TARGETS], in0=col_f[:, 0:TARGETS], scalar1=tgt_f[:, 0:1], scalar2=None, op0=ALU.is_equal
            )
            nc.vector.tensor_scalar(
                out=pick[:, t, TARGETS:SUMS], in0=col_f[:], scalar1=src_f[:, t : t + 1], scalar2=None, op0=ALU.is_equal
            )
        c_tab = setup.tile([P, HALF], F32)
        nc.vector.scalar_tensor_tensor(
            out=c_tab[:], in0=g_std[:], scalar=1.0 / NODES, in1=rstd[:], op0=ALU.mult, op1=ALU.mult
        )
        nc.vector.tensor_tensor(out=mean[:], in0=c_tab[:], in1=mean[:], op=ALU.mult)
        a_tab = setup.tile([P, HALF], F32)
        nc.vector.scalar_tensor_tensor(
            out=a_tab[:], in0=g_mean[:], scalar=1.0 / NODES, in1=mean[:], op0=ALU.mult, op1=ALU.subtract
        )

        ca_t = keep.tile([P, BLKS, 2, P], F32)
        turned_ca = []

        def turn_table(table):
            turned = short_lived([P, BLKS, P], F32, "turned")
            for fb in range(BLKS):
                nc.tensor.transpose(out=turned[:, fb, :], in_=table[:, fb * BLK : (fb + 1) * BLK], identity=ident_f[:])
            turned_ca.append(turned)

        def take_turned(a, blks):
            nc.scalar.copy(out=ca_t[:, blks, a, :], in_=turned_ca[a][:, blks, :])

        rep_of = {}
        spread_of = {}
        jj_of = {}

        def repeat_rows(k, tables=(0, 1)):
            group, graph = steps[k]
            fb0, blks = GROUPS[group][0] // BLK, GROUPS[group][1] // BLK
            h = fb0 // BLKS
            if tables[0] == 0:
                rep_of[k] = rep_pool.tile([P, blks, 2, NODES, SPREAD], F32, name="ca_rep")
            rows = ca_t[:].rearrange("p f a (n h) -> p f a n h", h=HALVES)
            some = slice(tables[0], tables[-1] + 1)
            rows = rows[:, fb0 % BLKS : fb0 % BLKS + blks, some, graph * NODES : (graph + 1) * NODES, h]
            nc.scalar.copy(
                out=rep_of[k][:, :, some], in_=rows.unsqueeze(4).to_broadcast([P, blks, len(tables), NODES, SPREAD])
            )

        def spread_rows(k, tables=(0, 1)):
            width = GROUPS[steps[k][0]][1]
            for a in tables:
                spread = psum.tile([P, PAIR, width], F32, tag="ca"[a] + "_ps", bufs=2, name="ca"[a] + "_ps")
                for sp in range(PAIR):
                    for fb in range(width // BLK):
                        nc.tensor.transpose(
                            out=spread[:, sp, fb * BLK : (fb + 1) * BLK],
                            in_=rep_of[k][:, fb, a, sp * TARGETS : (sp + 1) * TARGETS, :].rearrange("p q r -> p (q r)"),
                            identity=ident_f[:],
                        )
                spread_of.setdefault(k, []).append(spread)

        def round_j(k, engine_copy):
            group, graph = steps[k]
            col0, width = GROUPS[group]
            jj_of[k] = work.tile([P, 2, PAIR, width], BF16, name="jj")
            engine_copy(out=jj_of[k][:], in_=hit_tables[k][0])

        hit_of = {}

        def masks(k):
            width = GROUPS[steps[k][0]][1]
            hit_of[k] = work.tile([P, 2, PAIR, PACK, width], BF16, name="hit")
            for t in range(PACK):
                nc.vector.tensor_scalar(
                    out=hit_of[k][:, :, :, t, :], in0=jj_of[k][:], scalar1=src_f[:, t : t + 1], scalar2=None, op0=ALU.is_equal
                )

        def hits(k):
            group, graph = steps[k]
            col0, width = GROUPS[group]
            g_hits = hit_tables[k][1]
            for a in range(2):
                nc.vector.tensor_tensor(
                    out=hit_of[k][:, a],
                    in0=hit_of[k][:, a],
                    in1=g_hits[:, a].unsqueeze(2).to_broadcast([P, PAIR, PACK, width]),
                    op=ALU.mult,
                )

        both_hits_of = {}

        def add_hits(k, engine):
            width = GROUPS[steps[k][0]][1]
            slots = slice(0, CUT) if engine is nc.gpsimd else slice(CUT, PAIR * PACK)
            both = work.tile(
                [P, slots.stop - slots.start, width], F32, bufs=1 if engine is nc.gpsimd else 2, name="both" + str(slots.start)
            )
            hit = [hit_of[k][:, a].rearrange("p s t f -> p (s t) f")[:, slots] for a in range(2)]
            engine.tensor_tensor(out=both[:], in0=hit[0], in1=hit[1], op=ALU.add)
            both_hits_of.setdefault(k, []).append((slots, both))

        x_f = keep.tile([P, 2, C], F32)

        def cast_x():
            nc.scalar.copy(out=x_f[0:ALL_NODES, 0, :], in_=x_b[0:ALL_NODES, 0, :])
            nc.scalar.copy(out=x_f[:, 1, :], in_=x_b[:, 1, :])

        e_codes = keep.tile([P, PASSES, C], U32, align_bytes=64)
        e_scales = keep.tile([P, PASSES, C], U8, align_bytes=64)
        d_codes = [keep.tile([P, PASSES, HALF], U32, align_bytes=64, name="d_codes" + str(h)) for h in range(HALVES)]
        d_scales = [keep.tile([P, PASSES, HALF], U8, align_bytes=64, name="d_scales" + str(h)) for h in range(HALVES)]
        e_grp = {}
        d_grp = {}

        def regroup(engine_copy, grouped, raw):
            engine_copy(out=grouped.rearrange("p (c i) t -> p c t i", i=4), in_=raw.rearrange("p t (c i) -> p c t i", i=4))

        def quantise(grouped, codes, scales, fmt):
            nc.vector.quantize_mx(out=codes.bitcast(fmt), scales=scales, in_=grouped.rearrange("p c t -> p (c t)"))

        def regroup_edges(unit, piece, engine_copy):
            if piece == 0:
                e_grp[unit] = e_grp_pool.tile([P, HALF, PACK], BF16, align_bytes=64, name="e_grp")
            cols = slice(piece * HALF // E_PIECES, (piece + 1) * HALF // E_PIECES)
            regroup(engine_copy, e_grp[unit][:, cols, :], e_raw[unit][:, :, cols])

        def quantise_edges(unit):
            h, s = unit // PASSES, unit % PASSES
            cols = slice(h * HALF, (h + 1) * HALF)
            quantise(e_grp[unit][:], e_codes[:, s, cols], e_scales[:, s, cols], E4M3X4)

        def regroup_gradient(k, engine_copy):
            width = GROUPS[steps[k][0]][1]
            d_grp[k] = work.tile([P, PAIR, width, PACK], BF16, align_bytes=64, name="d_grp")
            for sp in range(PAIR):
                regroup(engine_copy, d_grp[k][:, sp], dm_of[k][:, sp])

        def quantise_gradient(k, sp):
            group, graph = steps[k]
            col0, width = GROUPS[group]
            h, col = col0 // HALF, col0 % HALF
            s = graph * PAIR + sp
            quantise(d_grp[k][:, sp], d_codes[h][:, s, col : col + width], d_scales[h][:, s, col : col + width], E5M2X4)

        sums_ps_of = {}
        sums_of = {}
        sums_t_of = [keep.tile([P, 2, WIDE // BLK, P], F32, name="sums_t" + str(i)) for i in range(2)]
        for sums_t in sums_t_of:
            nc.gpsimd.memset(sums_t[:, 0], 0.0)
        nc.gpsimd.memset(x_f[ALL_NODES:P, 0, :], 0.0)

        def partial_sums(k):
            group, graph = steps[k]
            if k in TURNED:
                turned_sums(k)
                return
            blks = GROUPS[group][1] // BLK
            if graph == 0:
                sums_ps_of[group] = psum.tile([P, PASSES, blks, SUMS], F32, name="sums_ps")
            for sp in range(PAIR):
                for fb in range(blks):
                    for t in range(PACK):
                        nc.tensor.matmul(
                            out=sums_ps_of[group][:, graph * PAIR + sp, fb, :],
                            lhsT=dm_of[k][:, sp, t, fb * BLK : (fb + 1) * BLK],
                            rhs=pick[:, t, :],
                            start=(t == 0),
                            stop=(t == PACK - 1),
                        )

        def turned_sums(k):
            group, graph = steps[k]
            for sp in range(PAIR):
                s = graph * PAIR + sp
                for fb in range(GROUPS[group][1] // BLK):
                    turned = psum.tile([P, PACK, BLK], F32, tag="ca"[fb % 2] + "_ps", bufs=2, name="dm_turn")
                    for t in range(PACK):
                        nc.tensor.transpose(
                            out=turned[:, t, :], in_=dm_of[k][:, sp, t, fb * BLK : (fb + 1) * BLK], identity=ident_f[:]
                        )
                    sums_t = sums_t_of[group % 2]
                    nc.vector.tensor_reduce(
                        out=sums_t[:, 0, fb, s * TARGETS : (s + 1) * TARGETS],
                        in_=turned[:].rearrange("p t (q r) -> p q t r", r=SPREAD),
                        axis=mybir.AxisListType.XY,
                        op=ALU.add,
                    )
                    nc.vector.tensor_reduce(
                        out=sums_t[:, 1, fb, s * NODES : (s + 1) * NODES].rearrange("p (r t) -> p r t", t=PACK),
                        in_=turned[:].rearrange("p t (q r) -> p r t q", r=SPREAD),
                        axis=mybir.AxisListType.X,
                        op=ALU.add,
                    )

        def take_sums(group, engine_copy):
            sums_ps, blks = sums_ps_of[group], GROUPS[group][1] // BLK
            sums_t = sums_t_of[group % 2][:, :, 0:blks, :]
            done = PAIR * sum(1 for graph in range(GRAPHS) if group * GRAPHS + graph not in TURNED)
            engine_copy(
                out=sums_t[:, 0, :, 0 : done * TARGETS].rearrange("p f (s q) -> p s f q", q=TARGETS), in_=sums_ps[:, 0:done, :, 0:TARGETS]
            )
            engine_copy(out=sums_t[:, 1, :, 0 : done * NODES].rearrange("p f (s j) -> p s f j", j=NODES), in_=sums_ps[:, 0:done, :, TARGETS:SUMS])

        def turn_sums(group, engine_copy):
            width = GROUPS[group][1]
            turned = short_lived([P, 2, width], F32, "ps_turn")
            for plane in range(2):
                for fb in range(width // BLK):
                    nc.tensor.transpose(
                        out=turned[:, plane, fb * BLK : (fb + 1) * BLK],
                        in_=sums_t_of[group % 2][:, plane, fb, :],
                        identity=ident_f[:],
                    )
            sums_of[group] = work.tile([P, 2, width], F32, name="sums")
            engine_copy(out=sums_of[group][:], in_=turned[:])

        def node_products(group, cb, engine_copy):
            col0, width = GROUPS[group]
            acc = short_lived([P, 2, width], F32, "acc")
            for plane in range(2):
                nc.tensor.matmul(
                    out=acc[:, plane, :],
                    lhsT=x_f[:, plane, cb * BLK : (cb + 1) * BLK],
                    rhs=sums_of[group][:, plane, :],
                    start=True,
                    stop=True,
                )
            result = o_pool.tile([P, 2, width], F32, name="result")
            engine_copy(out=result[:], in_=acc[:])
            both = out[0 : 2 * C, col0 : col0 + width].rearrange("(a r) f -> r a f", a=2)
            nc.sync.dma_start(out=both[cb * BLK : (cb + 1) * BLK], in_=result[:])

        def edge_passes(acc, h, cb, passes):
            for s in passes:
                nc.tensor.matmul_mx(
                    out=acc,
                    lhsT=e_codes[:, s, cb * BLK : (cb + 1) * BLK].bitcast(E4M3X4),
                    lhsT_scale=e_scales[:, s, cb * BLK : (cb + 1) * BLK],
                    rhs=d_codes[h][:, s, :].bitcast(E5M2X4),
                    rhs_scale=d_scales[h][:, s, :],
                    start=(s == 0),
                    stop=(s == PASSES - 1),
                )

        def store_edge_product(acc, h, cb, engine_copy):
            result = o_pool.tile([P, HALF], F32, name="result")
            engine_copy(out=result[:], in_=acc)
            row0 = 2 * C + cb * BLK
            nc.sync.dma_start(out=out[row0 : row0 + BLK, h * HALF : (h + 1) * HALF], in_=result[:])

        def first_half_edges(cb):
            acc = short_lived([P, HALF], F32, "acc")
            edge_passes(acc[:], 0, cb, range(PASSES))
            store_edge_product(acc[:], 0, cb, nc.scalar.copy)

        pending = []
        last_of_half_0 = max(k for k in range(STEPS) if GROUPS[steps[k][0]][0] < HALF)

        side = [(unit, piece) for unit in range(2 * PASSES) for piece in range(E_PIECES)]
        regrouped = []
        quantised = {"edges": 0, "gradients": 0}
        half_0 = list(range(C_BLKS))

        def edge_pieces(count):
            for unit, piece in side[0:count]:
                if unit in e_raw:
                    regroup_edges(unit, piece, nc.scalar.copy)
                    side.remove((unit, piece))
                    if piece + 1 == E_PIECES:
                        regrouped.append(unit)

        def outputs(count):
            for make in pending[0:count]:
                make()
                edge_pieces(1)
            pending[0:count] = []

        def more_half_0():
            while half_0 and quantised["gradients"] > last_of_half_0 and quantised["edges"] >= PASSES * (half_0[0] * BLK // HALF + 1):
                pending.append(lambda cb=half_0.pop(0): first_half_edges(cb))

        def step(k):
            group, graph = steps[k]
            col0, width = GROUPS[group]
            if k + 2 < STEPS:
                dm_of[k + 2] = load_messages(*steps[k + 2])
            for unit in range(len(e_raw), 2 * PASSES):
                if not any(earlier == unit - 4 for earlier, piece in side):
                    e_raw[unit] = load_edges(unit)
            if k in (1, 2):
                load_hit_tables(k - 1, HALF, HALF)
            c_row, a_row = spread_of[k]
            dm = dm_of[k]
            over_slots = [P, PACK, width]
            for row, op in ((c_row, ALU.mult), (a_row, ALU.add)):
                for sp in range(PAIR):
                    nc.vector.tensor_tensor(
                        out=dm[:, sp], in0=dm[:, sp], in1=row[:, sp, :].unsqueeze(1).to_broadcast(over_slots), op=op
                    )
            complete = k >= 1 and steps[k - 1][1] == GRAPHS - 1
            if k > last_of_half_0:
                for unit in regrouped:
                    quantise_edges(unit)
                quantised["edges"] += len(regrouped)
                regrouped.clear()
                more_half_0()
            at_start, in_gap, at_end = OUTPUTS.get(k, (0, 0, 0))
            if k >= 1:
                regroup_gradient(k - 1, nc.scalar.copy)
                if k - 1 not in TURNED:
                    partial_sums(k - 1)
            if k + 2 < STEPS and not complete:
                repeat_rows(k + 2)
                round_j(k + 2, nc.scalar.copy)
            if complete and k - 2 not in TURNED:
                take_sums(steps[k - 1][0], nc.scalar.copy)
            if k + 1 < STEPS:
                spread_rows(k + 1)
            edge_pieces(E1.get(k, 0))
            outputs(at_start)
            if k == XCAST:
                cast_x()
            outputs(in_gap)
            if complete and k - 1 not in TURNED:
                turn_sums(steps[k - 1][0], nc.scalar.copy)
                pending.extend([lambda cb=cb, g=steps[k - 1][0]: node_products(g, cb, nc.scalar.copy) for cb in range(C_BLKS)])
            if k + 2 < STEPS and complete:
                repeat_rows(k + 2)
                round_j(k + 2, nc.scalar.copy)
            edge_pieces(E2.get(k, 0))
            outputs(at_end)
            if k + 1 < STEPS:
                masks(k + 1)
            if k >= LAG:
                quantise_gradient(k - LAG, 0)
            if k + 1 < STEPS:
                hits(k + 1)
            if k >= LAG:
                quantise_gradient(k - LAG, 1)
                quantised["gradients"] += 1
                more_half_0()
            if k + 1 < STEPS:
                add_hits(k + 1, nc.vector)
            flat = dm[:].rearrange("p s t f -> p (s t) f")
            for slots, both in both_hits_of[k]:
                nc.vector.tensor_tensor(out=flat[:, slots], in0=flat[:, slots], in1=both[:], op=ALU.add)
            if k + 1 < STEPS:
                add_hits(k + 1, nc.gpsimd)
            if k >= 1 and k + 1 < STEPS and k - 1 in TURNED:
                partial_sums(k - 1)
                if complete:
                    turn_sums(steps[k - 1][0], nc.vector.tensor_copy)
                    pending.extend([lambda cb=cb, g=steps[k - 1][0]: node_products(g, cb, nc.scalar.copy) for cb in range(C_BLKS)])

        first_blks = slice(0, WIDTHS[0] // BLK)
        for a, table in enumerate((c_tab, a_tab)):
            turn_table(table)
            take_turned(a, first_blks)
            repeat_rows(0, (a,))
            spread_rows(0, (a,))
        round_j(0, nc.vector.tensor_copy)
        masks(0)
        hits(0)
        add_hits(0, nc.gpsimd)
        add_hits(0, nc.vector)
        load_hit_tables(0, WIDTHS[0], HALF - WIDTHS[0])
        e_raw[2] = load_edges(2)
        e_raw[3] = load_edges(3)
        x_b = setup.tile([P, 2, C], BF16)
        nc.sync.dma_start(out=x_b[0:ALL_NODES, 0, :], in_=x_rows)
        for s in range(PASSES):
            graph = s // PAIR
            nc.sync.dma_start(
                out=x_b[s * NODES : (s + 1) * NODES, 1, :], in_=x_rows[graph * NODES : (graph + 1) * NODES, :]
            )
        for a in range(2):
            take_turned(a, slice(first_blks.stop, BLKS))
        repeat_rows(1)
        round_j(1, nc.scalar.copy)

        for k in range(STEPS):
            step(k)

        last = STEPS - 1
        copies = (nc.scalar.copy, nc.vector.tensor_copy)
        regroup_gradient(last, nc.vector.tensor_copy)
        for old in range(last - LAG + 1, last + 1):
            for sp in range(PAIR):
                quantise_gradient(old, sp)
        turned_sums(last - 1)
        def last_edges(cb, engine_copy):
            acc = short_lived([P, HALF], F32, "acc")
            edge_passes(acc[:], 1, cb, range(PASSES))
            store_edge_product(acc[:], 1, cb, engine_copy)
        for cb in range(TA):
            last_edges(cb, copies[0])
        turned_sums(last)
        for cb in range(TA, TB):
            last_edges(cb, copies[0])
        turn_sums(len(GROUPS) - 1, nc.vector.tensor_copy)
        for cb in range(TB, C_BLKS):
            last_edges(cb, copies[cb % 2])
        for cb in range(C_BLKS):
            node_products(len(GROUPS) - 1, cb, copies[cb % 2])
